import numpy as np
import ml_dtypes


def mxq(x, axis, fmt="e4m3"):
    dtype, down = {"e4m3": (ml_dtypes.float8_e4m3fn, 7), "e5m2": (ml_dtypes.float8_e5m2, 14)}[fmt]
    v = np.moveaxis(np.asarray(x, np.float32).astype(ml_dtypes.bfloat16).astype(np.float64), axis, -1)
    blocks = v.reshape(v.shape[:-1] + (-1, 32))
    amax = np.abs(blocks).max(-1, keepdims=True)
    byte = np.maximum(np.where(amax > 0, np.frexp(amax)[1] - 1 + 127, 0) - down, 1)
    scale = np.exp2(byte - 127.0)
    codes = (blocks / scale).astype(np.float32).astype(dtype).astype(np.float64)
    return np.moveaxis((codes * scale).reshape(v.shape), -1, axis)


BF16 = ml_dtypes.bfloat16


def bf(x):
    return np.asarray(x, np.float32).astype(BF16)


def f64(x):
    return np.asarray(x).astype(np.float64)


N, D, H = 2048, 256, 4

EPS = 1e-12


def l2_normalize(v):
    sq = np.sum(v * v, axis=-1, keepdims=True)
    return v * (1.0 / np.sqrt(np.maximum(sq, EPS)))


def setup_inputs():
    shared = np.random.standard_normal((1, D))
    return {"x": bf(0.8 * np.random.standard_normal((N, D)) + 0.6 * shared), "attn_vectors": bf(np.random.random((H, D)))}


def reference(x, attn_vectors):
    x, a = f64(x), f64(attn_vectors)
    e = l2_normalize(a[:, None, :] * x[None, :, :])
    y = np.transpose(e, (1, 0, 2)).reshape(N, H * D)
    yq = mxq(y, 1, "e4m3")
    return (yq @ yq.T) / H

@@ -1,0 +1,542 @@
+from contextlib import ExitStack
+
+import concourse.mybir as mybir
+from concourse.masks import make_identity
+
+F32 = mybir.dt.float32
+BF16 = mybir.dt.bfloat16
+U32 = mybir.dt.uint32
+U8 = mybir.dt.uint8
+FP8X4 = mybir.dt.float8_e4m3fn_x4
+ACT = mybir.ActivationFunctionType
+ALU = mybir.AluOpType
+
+N, D, H = 2048, 256, 4
+K = H * D
+P = 128
+NT = N // P
+CH = 512
+NCH = N // CH
+PR = 256
+EPS = 1e-12
+FLOPS = 2 * N * N * K
+MANUAL = True
+
+PROGRAM = [
+    ("xt", 0, "xtS_0", "fr"),
+    ("xt", 0, "xtV_1", "fr"),
+    ("sqp", 0, "xtS_0"),
+    ("cp", 0, "xtV_1"),
+    ("xa", "V", 0, 0),
+    ("xa", "V", 0, 1),
+    ("xa", "V", 0, 2),
+    ("xa", "V", 0, 3),
+    ("xa", "G", 0, 5),
+    ("xa", "G", 0, 6),
+    ("xa", "G", 0, 7),
+    ("xt", 1, "xt_2", "acc"),
+    ("smm", 0, "s_3"),
+    ("cp", 1, "xt_2"),
+    ("max", 0, "s_3"),
+    ("sqrt", 0),
+    ("xa", "V", 0, 4),
+    ("rec", 0),
+    ("R", 0, 0, "R_4"),
+    ("R", 0, 1, "R_5"),
+    ("xa", "G", 1, 0),
+    ("xa", "G", 1, 1),
+    ("xa", "G", 1, 2),
+    ("xa", "G", 1, 3),
+    ("xa", "G", 1, 4),
+    ("xa", "G", 1, 5),
+    ("xa", "G", 1, 6),
+    ("xa", "G", 1, 7),
+    ("sqs", 1),
+    ("xt", 2, "xt_6", "acc"),
+    ("xt", 3, "xt_7", "acc"),
+    ("smm", 1, "s_8"),
+    ("TT", 0, 0, "R_4"),
+    ("max", 1, "s_8"),
+    ("sqrt", 1),
+    ("TT", 0, 1, "R_5"),
+    ("rec", 1),
+    ("cp", 2, "xt_6"),
+    ("xa", "G", 2, 0),
+    ("xa", "G", 2, 1),
+    ("xa", "G", 2, 2),
+    ("xa", "G", 2, 3),
+    ("xa", "G", 2, 4),
+    ("xa", "G", 2, 5),
+    ("xa", "G", 2, 6),
+    ("xa", "G", 2, 7),
+    ("sqs", 2),
+    ("Q", 0, 0),
+    ("Q", 0, 1),
+    ("R", 1, 0, "R_9"),
+    ("R", 1, 1, "R_10"),
+    ("R", 2, 0, "R_11"),
+    ("R", 2, 1, "R_12"),
+    ("TT", 1, 0, "R_9"),
+    ("TT", 1, 1, "R_10"),
+    ("cp", 3, "xt_7"),
+    ("xa", "G", 3, 0),
+    ("xa", "G", 3, 1),
+    ("xa", "G", 3, 2),
+    ("xa", "G", 3, 3),
+    ("xa", "G", 3, 4),
+    ("xa", "G", 3, 5),
+    ("xa", "G", 3, 6),
+    ("xa", "G", 3, 7),
+    ("sqs", 3),
+    ("Q", 1, 0),
+    ("Q", 1, 1),
+    ("smm", 2, "s_13"),
+    ("max", 2, "s_13"),
+    ("sqrt", 2),
+    ("rec", 2),
+    ("R", 3, 0, "R_14"),
+    ("R", 3, 1, "R_15"),
+    ("TT", 2, 0, "R_11"),
+    ("TT", 2, 1, "R_12"),
+    ("Q", 2, 0),
+    ("Q", 2, 1),
+    ("stage", "st_16", 512, "s1"),
+    ("mx", 3, 0, "acc_17"),
+    ("ev", "S", "acc_17", "st_16", 0),
+    ("store", "st_16", 3, 0, 1, 0),
+    ("stage", "st_18", 512, "s1"),
+    ("mx", 2, 0, "acc_19"),
+    ("ev", "S", "acc_19", "st_18", 0),
+    ("store", "st_18", 2, 0, 1, 0),
+    ("stage", "st_20", 512, "s1"),
+    ("mx", 1, 0, "acc_21"),
+    ("ev", "S", "acc_21", "st_20", 0),
+    ("store", "st_20", 1, 0, 1, 0),
+    ("stage", "st_22", 512, "s1"),
+    ("mx", 0, 0, "acc_23"),
+    ("ev", "S", "acc_23", "st_22", 0),
+    ("store", "st_22", 0, 0, 1, 0),
+    ("smm", 3, "s_24"),
+    ("max", 3, "s_24"),
+    ("sqrt", 3),
+    ("rec", 3),
+    ("R", 4, 0, "R_25"),
+    ("R", 4, 1, "R_26"),
+    ("TT", 3, 0, "R_14"),
+    ("TT", 3, 1, "R_15"),
+    ("Q", 3, 0),
+    ("Q", 3, 1),
+    ("stage", "st_27", 512, "s1"),
+    ("mx", 5, 0, "acc_28"),
+    ("ev", "S", "acc_28", "st_27", 0),
+    ("store", "st_27", 5, 0, 1, 0),
+    ("stage", "st_29", 512, "s1"),
+    ("mx", 4, 0, "acc_30"),
+    ("ev", "S", "acc_30", "st_29", 0),
+    ("store", "st_29", 4, 0, 1, 0),
+    ("R", 5, 0, "R_31"),
+    ("R", 5, 1, "R_32"),
+    ("TT", 4, 0, "R_25"),
+    ("TT", 4, 1, "R_26"),
+    ("Q", 4, 0),
+    ("Q", 4, 1),
+    ("stage", "st_33", 1024, "st"),
+    ("mx", 7, 0, "acc_34"),
+    ("ev", "S", "acc_34", "st_33", 0),
+    ("mx", 7, 1, "acc_35"),
+    ("ev", "S", "acc_35", "st_33", 512),
+    ("store", "st_33", 7, 0, 2, 0),
+    ("stage", "st_36", 1024, "st"),
+    ("mx", 6, 0, "acc_37"),
+    ("ev", "S", "acc_37", "st_36", 0),
+    ("mx", 6, 1, "acc_38"),
+    ("ev", "S", "acc_38", "st_36", 512),
+    ("store", "st_36", 6, 0, 2, 0),
+    ("R", 6, 0, "R_39"),
+    ("R", 6, 1, "R_40"),
+    ("TT", 5, 0, "R_31"),
+    ("TT", 5, 1, "R_32"),
+    ("Q", 5, 0),
+    ("Q", 5, 1),
+    ("stage", "st_41", 1024, "st"),
+    ("mx", 9, 0, "acc_42"),
+    ("ev", "S", "acc_42", "st_41", 0),
+    ("mx", 9, 1, "acc_43"),
+    ("ev", "S", "acc_43", "st_41", 512),
+    ("store", "st_41", 9, 0, 2, 0),
+    ("stage", "st_44", 1024, "st"),
+    ("mx", 8, 0, "acc_45"),
+    ("ev", "S", "acc_45", "st_44", 0),
+    ("mx", 8, 1, "acc_46"),
+    ("ev", "S", "acc_46", "st_44", 512),
+    ("store", "st_44", 8, 0, 2, 0),
+    ("R", 7, 0, "R_47"),
+    ("R", 7, 1, "R_48"),
+    ("TT", 6, 0, "R_39"),
+    ("TT", 6, 1, "R_40"),
+    ("Q", 6, 0),
+    ("Q", 6, 1),
+    ("stage", "st_49", 1536, "st"),
+    ("mx", 11, 0, "acc_50"),
+    ("ev", "S", "acc_50", "st_49", 0),
+    ("mx", 11, 1, "acc_51"),
+    ("ev", "S", "acc_51", "st_49", 512),
+    ("mx", 11, 2, "acc_52"),
+    ("ev", "S", "acc_52", "st_49", 1024),
+    ("store", "st_49", 11, 0, 3, 0),
+    ("stage", "st_53", 512, "s1"),
+    ("mx", 10, 0, "acc_54"),
+    ("ev", "S", "acc_54", "st_53", 0),
+    ("store", "st_53", 10, 0, 1, 0),
+    ("TT", 7, 0, "R_47"),
+    ("TT", 7, 1, "R_48"),
+    ("Q", 7, 0),
+    ("Q", 7, 1),
+    ("stage", "st_55", 1536, "st"),
+    ("mx", 13, 0, "acc_56"),
+    ("ev", "S", "acc_56", "st_55", 0),
+    ("mx", 13, 1, "acc_57"),
+    ("ev", "S", "acc_57", "st_55", 512),
+    ("mx", 13, 2, "acc_58"),
+    ("ev", "S", "acc_58", "st_55", 1024),
+    ("store", "st_55", 13, 0, 3, 0),
+    ("stage", "st_59", 512, "s1"),
+    ("mx", 12, 0, "acc_60"),
+    ("ev", "S", "acc_60", "st_59", 0),
+    ("store", "st_59", 12, 0, 1, 0),
+    ("stage", "st_61", 2048, "st"),
+    ("mx", 15, 0, "acc_62"),
+    ("ev", "S", "acc_62", "st_61", 0),
+    ("mx", 15, 1, "acc_63"),
+    ("ev", "V", "acc_63", "st_61", 512),
+    ("mx", 15, 2, "acc_64"),
+    ("ev", "S", "acc_64", "st_61", 1024),
+    ("mx", 15, 3, "acc_65"),
+    ("ev", "V", "acc_65", "st_61", 1536),
+    ("store", "st_61", 15, 0, 4, 0),
+    ("stage", "st_66", 2048, "st"),
+    ("mx", 14, 0, "acc_67"),
+    ("ev", "S", "acc_67", "st_66", 0),
+    ("mx", 14, 1, "acc_68"),
+    ("ev", "V", "acc_68", "st_66", 512),
+    ("mx", 14, 2, "acc_69"),
+    ("ev", "S", "acc_69", "st_66", 1024),
+    ("mx", 14, 3, "acc_70"),
+    ("ev", "V", "acc_70", "st_66", 1536),
+    ("store", "st_66", 14, 0, 4, 0),
+    ("stage", "st_71", 512, "s1"),
+    ("mx", 13, 3, "acc_72"),
+    ("ev", "S", "acc_72", "st_71", 0),
+    ("store", "st_71", 13, 3, 1, 0),
+    ("stage", "st_73", 1536, "st"),
+    ("mx", 12, 1, "acc_74"),
+    ("ev", "V", "acc_74", "st_73", 0),
+    ("mx", 12, 2, "acc_75"),
+    ("ev", "S", "acc_75", "st_73", 512),
+    ("mx", 12, 3, "acc_76"),
+    ("ev", "V", "acc_76", "st_73", 1024),
+    ("store", "st_73", 12, 1, 3, 0),
+    ("stage", "st_77", 512, "s1"),
+    ("mx", 11, 3, "acc_78"),
+    ("ev", "S", "acc_78", "st_77", 0),
+    ("store", "st_77", 11, 3, 1, 0),
+    ("stage", "st_79", 1536, "st"),
+    ("mx", 10, 1, "acc_80"),
+    ("ev", "V", "acc_80", "st_79", 0),
+    ("mx", 10, 2, "acc_81"),
+    ("ev", "S", "acc_81", "st_79", 512),
+    ("mx", 10, 3, "acc_82"),
+    ("ev", "V", "acc_82", "st_79", 1024),
+    ("store", "st_79", 10, 1, 3, 0),
+    ("stage", "st_83", 1024, "st"),
+    ("mx", 9, 2, "acc_84"),
+    ("ev", "S", "acc_84", "st_83", 0),
+    ("mx", 9, 3, "acc_85"),
+    ("ev", "V", "acc_85", "st_83", 512),
+    ("store", "st_83", 9, 2, 2, 0),
+    ("stage", "st_86", 1024, "st"),
+    ("mx", 8, 2, "acc_87"),
+    ("ev", "S", "acc_87", "st_86", 0),
+    ("mx", 8, 3, "acc_88"),
+    ("ev", "V", "acc_88", "st_86", 512),
+    ("store", "st_86", 8, 2, 2, 0),
+    ("stage", "st_89", 1024, "st"),
+    ("mx", 7, 2, "acc_90"),
+    ("ev", "S", "acc_90", "st_89", 0),
+    ("mx", 7, 3, "acc_91"),
+    ("ev", "V", "acc_91", "st_89", 512),
+    ("store", "st_89", 7, 2, 2, 0),
+    ("stage", "st_92", 1024, "st"),
+    ("mx", 6, 2, "acc_93"),
+    ("ev", "S", "acc_93", "st_92", 0),
+    ("mx", 6, 3, "acc_94"),
+    ("ev", "V", "acc_94", "st_92", 512),
+    ("store", "st_92", 6, 2, 2, 0),
+    ("stage", "st_95", 1536, "st"),
+    ("mx", 5, 1, "acc_96"),
+    ("ev", "S", "acc_96", "st_95", 0),
+    ("mx", 5, 2, "acc_97"),
+    ("ev", "V", "acc_97", "st_95", 512),
+    ("mx", 5, 3, "acc_98"),
+    ("ev", "S", "acc_98", "st_95", 1024),
+    ("store", "st_95", 5, 1, 3, 0),
+    ("stage", "st_99", 1536, "st"),
+    ("mx", 4, 1, "acc_100"),
+    ("ev", "V", "acc_100", "st_99", 0),
+    ("mx", 4, 2, "acc_101"),
+    ("ev", "S", "acc_101", "st_99", 512),
+    ("mx", 4, 3, "acc_102"),
+    ("ev", "V", "acc_102", "st_99", 1024),
+    ("store", "st_99", 4, 1, 3, 0),
+    ("stage", "st_103", 1536, "st"),
+    ("mx", 3, 1, "acc_104"),
+    ("ev", "S", "acc_104", "st_103", 0),
+    ("mx", 3, 2, "acc_105"),
+    ("ev", "V", "acc_105", "st_103", 512),
+    ("mx", 3, 3, "acc_106"),
+    ("ev", "S", "acc_106", "st_103", 1024),
+    ("store", "st_103", 3, 1, 3, 0),
+    ("stage", "st_107", 1536, "st"),
+    ("mx", 2, 1, "acc_108"),
+    ("ev", "V", "acc_108", "st_107", 0),
+    ("mx", 2, 2, "acc_109"),
+    ("ev", "S", "acc_109", "st_107", 512),
+    ("mx", 2, 3, "acc_110"),
+    ("ev", "V", "acc_110", "st_107", 1024),
+    ("store", "st_107", 2, 1, 3, 0),
+    ("stage", "st_111", 512, "s1"),
+    ("mx", 1, 1, "acc_112"),
+    ("ev", "S", "acc_112", "st_111", 0),
+    ("store", "st_111", 1, 1, 1, 0),
+    ("stage", "st_113", 512, "s1"),
+    ("mx", 1, 2, "acc_114"),
+    ("ev", "V", "acc_114", "st_113", 0),
+    ("store", "st_113", 1, 2, 1, 0),
+    ("stage", "st_115", 512, "s1"),
+    ("mx", 1, 3, "acc_116"),
+    ("ev", "S", "acc_116", "st_115", 0),
+    ("store", "st_115", 1, 3, 1, 0),
+    ("stage", "st_117", 512, "s1"),
+    ("mx", 0, 1, "acc_118"),
+    ("ev", "V", "acc_118", "st_117", 0),
+    ("store", "st_117", 0, 1, 1, 0),
+    ("stage", "st_119", 512, "s1"),
+    ("mx", 0, 2, "acc_120"),
+    ("ev", "S", "acc_120", "st_119", 0),
+    ("store", "st_119", 0, 2, 1, 0),
+    ("stage", "st_121", 512, "s1"),
+    ("mx", 0, 3, "acc_122"),
+    ("ev", "V", "acc_122", "st_121", 0),
+    ("store", "st_121", 0, 3, 1, 0),
+]
+
+
+def tile_attentive_kernel(tc, x, attn_vectors, out):
+    nc = tc.nc
+    with ExitStack() as ctx:
+        if MANUAL:
+            ctx.enter_context(tc.manual_schedule())
+        keep = ctx.enter_context(tc.tile_pool(name="keep", bufs=1))
+        small = ctx.enter_context(tc.tile_pool(name="small", bufs=4))
+        pools = {
+            "st": ctx.enter_context(tc.tile_pool(name="st", bufs=5)),
+            "s1": ctx.enter_context(tc.tile_pool(name="s1", bufs=8)),
+            "fr": ctx.enter_context(tc.psum_pool(name="fr", bufs=4)),
+            "acc": ctx.enter_context(tc.psum_pool(name="acc", bufs=4)),
+        }
+
+        a0 = keep.tile([P, D], BF16)
+        nc.vector.memset(a0[:], 0.0)
+        nc.scalar.dma_start(out=a0[0:H, :], in_=attn_vectors)
+        x_sb = keep.tile([P, NT * D], BF16)
+        for g in range(NCH):
+            nc.sync.dma_start(
+                out=x_sb[:, g * 4 * D:(g + 1) * 4 * D].rearrange("p (t d) -> p t d", d=D),
+                in_=x[g * CH:(g + 1) * CH, :].rearrange("(t p) d -> p t d", p=P),
+            )
+        warm = keep.tile([P, 1], F32)
+        nc.vector.memset(warm[:], 1.0)
+        warm2 = keep.tile([P, 1], F32)
+        nc.scalar.activation(out=warm2[:], in_=warm[:], func=ACT.Sqrt)
+        ident_f = keep.tile([P, P], F32)
+        make_identity(nc, ident_f[:])
+
+        xT_w = keep.tile([P, N], F32)
+        x2T = keep.tile([P, 2, N], F32)
+        aT_f = keep.tile([P, 2 * H], F32)
+        a2T = keep.tile([P, 2, H], F32)
+        r_sb = keep.tile([P, NT * H], F32)
+        xa = keep.tile([P, 2, 4, N], F32)
+        grouped = keep.tile([P, 2, N, 4], BF16, align_bytes=64)
+        codes = keep.tile([P, 2, N], U32, align_bytes=64)
+        scl = keep.tile([P, 2, N], U8, align_bytes=64)
+
+        xw = x_sb[:].bitcast(F32)
+        xT_b = xT_w[:].bitcast(BF16).rearrange("p (n e) -> p n e", e=2)
+
+        aT_ps = pools["fr"].tile([P, P], F32, tag="fr")
+        nc.tensor.transpose(aT_ps[:], a0[:].bitcast(F32), ident_f[:])
+        nc.vector.tensor_copy(out=aT_f[:], in_=aT_ps[:].bitcast(BF16)[:, 0:2 * H])
+        nc.scalar.activation(out=a2T[:], in_=aT_f[:].rearrange("p (h e) -> p e h", e=2), func=ACT.Square)
+
+        tiles = {}
+
+        for call in PROGRAM:
+            op = call[0]
+            if op == "xt":
+                g, key, pool = call[1], call[2], call[3]
+                tl = pools[pool].tile([P, CH], F32, tag=pool)
+                tiles[key] = tl
+                for j in range(4):
+                    t = 4 * g + j
+                    nc.tensor.transpose(tl[:, j * P:(j + 1) * P], xw[:, t * P:(t + 1) * P], ident_f[:])
+            elif op == "sqp":
+                g, key = call[1], call[2]
+                nc.scalar.activation(
+                    out=x2T[:, :, g * CH:(g + 1) * CH],
+                    in_=tiles[key][:].bitcast(BF16).rearrange("p (n e) -> p e n", e=2),
+                    func=ACT.Square,
+                )
+            elif op == "sqs":
+                g = call[1]
+                nc.scalar.activation(
+                    out=x2T[:, :, g * CH:(g + 1) * CH],
+                    in_=xT_b[:, g * CH:(g + 1) * CH, :].rearrange("p n e -> p e n"),
+                    func=ACT.Square,
+                )
+            elif op == "cp":
+                g, key = call[1], call[2]
+                nc.vector.tensor_copy(out=xT_w[:, g * CH:(g + 1) * CH], in_=tiles[key][:])
+            elif op == "cps":
+                g, key = call[1], call[2]
+                nc.scalar.copy(out=xT_w[:, g * CH:(g + 1) * CH], in_=tiles[key][:])
+            elif op == "xa":
+                eng, g, k = call[1], call[2], call[3]
+                c, t = k // 4, k % 4
+                h, e = 2 * c + t // 2, t % 2
+                if eng == "V":
+                    nc.vector.tensor_scalar_mul(
+                        out=xa[:, c, t, g * CH:(g + 1) * CH],
+                        in0=xT_b[:, g * CH:(g + 1) * CH, e],
+                        scalar1=aT_f[:, 2 * h + e:2 * h + e + 1],
+                    )
+                elif eng == "S":
+                    nc.scalar.activation(
+                        out=xa[:, c, t, g * CH:(g + 1) * CH],
+                        in_=xT_b[:, g * CH:(g + 1) * CH, e],
+                        func=ACT.Copy,
+                        scale=aT_f[:, 2 * h + e:2 * h + e + 1],
+                    )
+                else:
+                    nc.gpsimd.tensor_scalar(
+                        out=xa[:, c, t, g * CH:(g + 1) * CH],
+                        in0=xT_b[:, g * CH:(g + 1) * CH, e],
+                        scalar1=aT_f[:, 2 * h + e:2 * h + e + 1],
+                        scalar2=0.0,
+                        op0=ALU.mult,
+                        op1=ALU.add,
+                    )
+            elif op == "smm":
+                g, key = call[1], call[2]
+                tl = pools["fr"].tile([P, 4 * H], F32, tag="fr")
+                tiles[key] = tl
+                for j in range(4):
+                    t = 4 * g + j
+                    for e in range(2):
+                        nc.tensor.matmul(
+                            out=tl[:, j * H:(j + 1) * H],
+                            lhsT=x2T[:, e, t * P:(t + 1) * P],
+                            rhs=a2T[:, e, :],
+                            start=(e == 0),
+                            stop=(e == 1),
+                        )
+            elif op == "max":
+                g, key = call[1], call[2]
+                sm = small.tile([P, 4 * H], F32, tag="sm")
+                tiles["sm%d" % g] = sm
+                nc.vector.tensor_scalar_max(out=sm[:], in0=tiles[key][:], scalar1=EPS)
+            elif op == "sqrt":
+                g = call[1]
+                sq = small.tile([P, 4 * H], F32, tag="sq")
+                tiles["sq%d" % g] = sq
+                nc.scalar.activation(out=sq[:], in_=tiles["sm%d" % g][:], func=ACT.Sqrt)
+            elif op == "rec":
+                g = call[1]
+                nc.vector.reciprocal(out=r_sb[:, g * 4 * H:(g + 1) * 4 * H], in_=tiles["sq%d" % g][:])
+            elif op == "R":
+                u, c, key = call[1], call[2], call[3]
+                tl = pools["fr"].tile([P, 2, PR], F32, tag="fr")
+                tiles[key] = tl
+                for hh in range(2):
+                    for q in range(2):
+                        col = (2 * u + q) * H + 2 * c + hh
+                        nc.tensor.transpose(
+                            tl[:, hh, q * P:(q + 1) * P],
+                            r_sb[:, col:col + 1].to_broadcast([P, P]),
+                            ident_f[:],
+                        )
+            elif op == "TT":
+                u, c, key = call[1], call[2], call[3]
+                n0 = u * PR
+                nc.vector.tensor_tensor(
+                    out=grouped[:, c, n0:n0 + PR, :].rearrange("p n (h e) -> p n h e", e=2),
+                    in0=xa[:, c, :, n0:n0 + PR].rearrange("p (h e) n -> p n h e", e=2),
+                    in1=tiles[key][:].rearrange("p h n -> p n h").unsqueeze(3).to_broadcast([P, PR, 2, 2]),
+                    op=ALU.mult,
+                )
+            elif op == "Q":
+                u, c = call[1], call[2]
+                n0 = u * PR
+                nc.vector.quantize_mx(
+                    out=codes[:, c, n0:n0 + PR].bitcast(FP8X4),
+                    scales=scl[:, c, n0:n0 + PR],
+                    in_=grouped[:, c, n0:n0 + PR, :].rearrange("p n j -> p (n j)"),
+                )
+            elif op == "stage":
+                key, width, tag = call[1], call[2], call[3]
+                tl = pools[tag].tile([P, width], F32, tag=tag)
+                tiles[key] = tl
+            elif op == "mx":
+                i, jc, key = call[1], call[2], call[3]
+                tl = pools["acc"].tile([P, CH], F32, tag="acc")
+                tiles[key] = tl
+                for c in range(2):
+                    nc.tensor.matmul_mx(
+                        out=tl[:],
+                        lhsT=codes[:, c, i * P:(i + 1) * P].bitcast(FP8X4),
+                        lhsT_scale=scl[:, c, i * P:(i + 1) * P],
+                        rhs=codes[:, c, jc * CH:(jc + 1) * CH].bitcast(FP8X4),
+                        rhs_scale=scl[:, c, jc * CH:(jc + 1) * CH],
+                        start=(c == 0),
+                        stop=(c == 1),
+                    )
+            elif op == "ev":
+                eng, key, st, off = call[1], call[2], call[3], call[4]
+                if eng == "V":
+                    nc.vector.tensor_scalar_mul(out=tiles[st][:, off:off + CH], in0=tiles[key][:], scalar1=0.25)
+                else:
+                    nc.scalar.mul(out=tiles[st][:, off:off + CH], in_=tiles[key][:], mul=0.25)
+            elif op == "mir":
+                j, jp, key = call[1], call[2], call[3]
+                tl = pools["acc"].tile([P, CH], F32, tag="acc")
+                tiles[key] = tl
+                for q in range(4):
+                    nc.tensor.transpose(
+                        tl[:, q * P:(q + 1) * P],
+                        tiles["hd%d" % (4 * jp + q)][:, j * P:(j + 1) * P],
+                        ident_f[:],
+                    )
+            elif op == "evc":
+                eng, key, st, off = call[1], call[2], call[3], call[4]
+                if eng == "V":
+                    nc.vector.tensor_copy(out=tiles[st][:, off:off + CH], in_=tiles[key][:])
+                else:
+                    nc.scalar.copy(out=tiles[st][:, off:off + CH], in_=tiles[key][:])
+            elif op == "store":
+                st, i, j0, nj, off = call[1], call[2], call[3], call[4], call[5]
+                nc.sync.dma_start(
+                    out=out[i * P:(i + 1) * P, j0 * CH:(j0 + nj) * CH],
+                    in_=tiles[st][:, off:off + nj * CH],
+                )
+            else:
+                assert False, op

@@ -20,327 +20,370 @@ NCH = N // CH
 PR = 256
 EPS = 1e-12
 FLOPS = 2 * N * N * K
-MANUAL = True
 
 PROGRAM = [
-    ("xt", 0, "xtS_0", "fr"),
-    ("xt", 0, "xtV_1", "fr"),
+    ("xt", 0, "xtS_0", "acc"),
+    ("xt", 0, "xtV_1", "acc"),
     ("sqp", 0, "xtS_0"),
     ("cp", 0, "xtV_1"),
-    ("xa", "V", 0, 0),
-    ("xa", "V", 0, 1),
-    ("xa", "V", 0, 2),
-    ("xa", "V", 0, 3),
-    ("xa", "G", 0, 5),
-    ("xa", "G", 0, 6),
-    ("xa", "G", 0, 7),
-    ("xt", 1, "xt_2", "acc"),
-    ("smm", 0, "s_3"),
-    ("cp", 1, "xt_2"),
-    ("max", 0, "s_3"),
+    ("xt", 1, "xtS_3", "acc"),
+    ("xt", 1, "xtV_4", "acc"),
+    ("sqp", 1, "xtS_3"),
+    ("cp", 1, "xtV_4"),
+    ("smm", 0, "s_2"),
+    ("max", 0, "s_2"),
     ("sqrt", 0),
-    ("xa", "V", 0, 4),
     ("rec", 0),
-    ("R", 0, 0, "R_4"),
-    ("R", 0, 1, "R_5"),
-    ("xa", "G", 1, 0),
-    ("xa", "G", 1, 1),
-    ("xa", "G", 1, 2),
-    ("xa", "G", 1, 3),
-    ("xa", "G", 1, 4),
-    ("xa", "G", 1, 5),
-    ("xa", "G", 1, 6),
-    ("xa", "G", 1, 7),
-    ("sqs", 1),
-    ("xt", 2, "xt_6", "acc"),
-    ("xt", 3, "xt_7", "acc"),
-    ("smm", 1, "s_8"),
-    ("TT", 0, 0, "R_4"),
-    ("max", 1, "s_8"),
+    ("xt", 2, "xtS_6", "acc"),
+    ("xt", 2, "xtV_7", "acc"),
+    ("sqp", 2, "xtS_6"),
+    ("R", 0, 0, "R_12"),
+    ("R", 0, 1, "R_13"),
+    ("R", 1, 0, "R_14"),
+    ("R", 1, 1, "R_15"),
+    ("cp", 2, "xtV_7"),
+    ("smm", 1, "s_5"),
+    ("xt", 3, "xtS_9", "acc"),
+    ("xt", 3, "xtV_10", "acc"),
+    ("sqp", 3, "xtS_9"),
+    ("smm", 2, "s_8"),
+    ("stt", 0, 0, 0, "R_12"),
+    ("stt", 0, 0, 1, "R_12"),
+    ("stt", 0, 0, 2, "R_12"),
+    ("stt", 0, 0, 3, "R_12"),
+    ("max", 1, "s_5"),
     ("sqrt", 1),
-    ("TT", 0, 1, "R_5"),
+    ("stt", 0, 1, 0, "R_13"),
+    ("stt", 0, 1, 1, "R_13"),
+    ("stt", 0, 1, 2, "R_13"),
+    ("stt", 0, 1, 3, "R_13"),
     ("rec", 1),
-    ("cp", 2, "xt_6"),
-    ("xa", "G", 2, 0),
-    ("xa", "G", 2, 1),
-    ("xa", "G", 2, 2),
-    ("xa", "G", 2, 3),
-    ("xa", "G", 2, 4),
-    ("xa", "G", 2, 5),
-    ("xa", "G", 2, 6),
-    ("xa", "G", 2, 7),
-    ("sqs", 2),
+    ("cp", 3, "xtV_10"),
+    ("rg", "S", 0, 0),
+    ("rg", "S", 0, 1),
+    ("R", 2, 0, "R_16"),
+    ("R", 2, 1, "R_17"),
+    ("stt", 1, 0, 0, "R_14"),
+    ("stt", 1, 0, 1, "R_14"),
+    ("stt", 1, 0, 2, "R_14"),
+    ("stt", 1, 0, 3, "R_14"),
+    ("max", 2, "s_8"),
+    ("sqrt", 2),
+    ("smm", 3, "s_11"),
+    ("stt", 1, 1, 0, "R_15"),
+    ("stt", 1, 1, 1, "R_15"),
+    ("stt", 1, 1, 2, "R_15"),
+    ("stt", 1, 1, 3, "R_15"),
+    ("rec", 2),
+    ("rg", "S", 1, 0),
+    ("rg", "S", 1, 1),
     ("Q", 0, 0),
     ("Q", 0, 1),
-    ("R", 1, 0, "R_9"),
-    ("R", 1, 1, "R_10"),
-    ("R", 2, 0, "R_11"),
-    ("R", 2, 1, "R_12"),
-    ("TT", 1, 0, "R_9"),
-    ("TT", 1, 1, "R_10"),
-    ("cp", 3, "xt_7"),
-    ("xa", "G", 3, 0),
-    ("xa", "G", 3, 1),
-    ("xa", "G", 3, 2),
-    ("xa", "G", 3, 3),
-    ("xa", "G", 3, 4),
-    ("xa", "G", 3, 5),
-    ("xa", "G", 3, 6),
-    ("xa", "G", 3, 7),
-    ("sqs", 3),
+    ("R", 3, 0, "R_18"),
+    ("R", 3, 1, "R_19"),
+    ("stt", 2, 0, 0, "R_16"),
+    ("stt", 2, 0, 1, "R_16"),
+    ("stt", 2, 0, 2, "R_16"),
+    ("stt", 2, 0, 3, "R_16"),
+    ("max", 3, "s_11"),
+    ("sqrt", 3),
+    ("stt", 2, 1, 0, "R_17"),
+    ("stt", 2, 1, 1, "R_17"),
+    ("stt", 2, 1, 2, "R_17"),
+    ("stt", 2, 1, 3, "R_17"),
+    ("rec", 3),
+    ("rg", "S", 2, 0),
+    ("rg", "S", 2, 1),
     ("Q", 1, 0),
     ("Q", 1, 1),
-    ("smm", 2, "s_13"),
-    ("max", 2, "s_13"),
-    ("sqrt", 2),
-    ("rec", 2),
-    ("R", 3, 0, "R_14"),
-    ("R", 3, 1, "R_15"),
-    ("TT", 2, 0, "R_11"),
-    ("TT", 2, 1, "R_12"),
+    ("stage", "H0", 512, "hv"),
+    ("mxu", 0, 0, "acc_20"),
+    ("evu", "S", "acc_20", "H0", 0),
+    ("storeu", "H0", 0, 0, 1, 0),
+    ("R", 4, 0, "R_21"),
+    ("R", 4, 1, "R_22"),
+    ("stt", 3, 0, 0, "R_18"),
+    ("stt", 3, 0, 1, "R_18"),
+    ("stt", 3, 0, 2, "R_18"),
+    ("stt", 3, 0, 3, "R_18"),
+    ("stt", 3, 1, 0, "R_19"),
+    ("stt", 3, 1, 1, "R_19"),
+    ("stt", 3, 1, 2, "R_19"),
+    ("stt", 3, 1, 3, "R_19"),
     ("Q", 2, 0),
     ("Q", 2, 1),
-    ("stage", "st_16", 512, "s1"),
-    ("mx", 3, 0, "acc_17"),
-    ("ev", "S", "acc_17", "st_16", 0),
-    ("store", "st_16", 3, 0, 1, 0),
-    ("stage", "st_18", 512, "s1"),
-    ("mx", 2, 0, "acc_19"),
-    ("ev", "S", "acc_19", "st_18", 0),
-    ("store", "st_18", 2, 0, 1, 0),
-    ("stage", "st_20", 512, "s1"),
-    ("mx", 1, 0, "acc_21"),
-    ("ev", "S", "acc_21", "st_20", 0),
-    ("store", "st_20", 1, 0, 1, 0),
-    ("stage", "st_22", 512, "s1"),
-    ("mx", 0, 0, "acc_23"),
-    ("ev", "S", "acc_23", "st_22", 0),
-    ("store", "st_22", 0, 0, 1, 0),
-    ("smm", 3, "s_24"),
-    ("max", 3, "s_24"),
-    ("sqrt", 3),
-    ("rec", 3),
-    ("R", 4, 0, "R_25"),
-    ("R", 4, 1, "R_26"),
-    ("TT", 3, 0, "R_14"),
-    ("TT", 3, 1, "R_15"),
+    ("stage", "H1", 1024, "hv"),
+    ("mxu", 1, 0, "acc_23"),
+    ("evu", "S", "acc_23", "H1", 0),
+    ("mxu", 1, 1, "acc_24"),
+    ("evu", "S", "acc_24", "H1", 256),
+    ("storeu", "H1", 1, 0, 2, 0),
+    ("mxu", 0, 1, "acc_25"),
+    ("stage", "sp_26", 512, "sp"),
+    ("evu", "S", "acc_25", "sp_26", 0),
+    ("storeu", "sp_26", 0, 1, 1, 0),
+    ("R", 5, 0, "R_27"),
+    ("R", 5, 1, "R_28"),
+    ("stt", 4, 0, 0, "R_21"),
+    ("stt", 4, 0, 1, "R_21"),
+    ("stt", 4, 0, 2, "R_21"),
+    ("stt", 4, 0, 3, "R_21"),
+    ("stt", 4, 1, 0, "R_22"),
+    ("stt", 4, 1, 1, "R_22"),
+    ("stt", 4, 1, 2, "R_22"),
+    ("stt", 4, 1, 3, "R_22"),
+    ("rg", "V", 3, 0),
+    ("rg", "V", 3, 1),
     ("Q", 3, 0),
     ("Q", 3, 1),
-    ("stage", "st_27", 512, "s1"),
-    ("mx", 5, 0, "acc_28"),
-    ("ev", "S", "acc_28", "st_27", 0),
-    ("store", "st_27", 5, 0, 1, 0),
-    ("stage", "st_29", 512, "s1"),
-    ("mx", 4, 0, "acc_30"),
-    ("ev", "S", "acc_30", "st_29", 0),
-    ("store", "st_29", 4, 0, 1, 0),
-    ("R", 5, 0, "R_31"),
-    ("R", 5, 1, "R_32"),
-    ("TT", 4, 0, "R_25"),
-    ("TT", 4, 1, "R_26"),
+    ("stage", "H2", 1536, "hv"),
+    ("mxu", 2, 0, "acc_29"),
+    ("evu", "S", "acc_29", "H2", 0),
+    ("mxu", 2, 1, "acc_30"),
+    ("evu", "S", "acc_30", "H2", 256),
+    ("mxu", 2, 2, "acc_31"),
+    ("evu", "S", "acc_31", "H2", 512),
+    ("storeu", "H2", 2, 0, 3, 0),
+    ("mxu", 0, 2, "acc_32"),
+    ("stage", "sp_33", 512, "sp"),
+    ("evu", "S", "acc_32", "sp_33", 0),
+    ("storeu", "sp_33", 0, 2, 1, 0),
+    ("mxu", 1, 2, "acc_34"),
+    ("stage", "sp_35", 512, "sp"),
+    ("evu", "S", "acc_34", "sp_35", 0),
+    ("storeu", "sp_35", 1, 2, 1, 0),
+    ("R", 6, 0, "R_36"),
+    ("R", 6, 1, "R_37"),
+    ("stt", 5, 0, 0, "R_27"),
+    ("stt", 5, 0, 1, "R_27"),
+    ("stt", 5, 0, 2, "R_27"),
+    ("stt", 5, 0, 3, "R_27"),
+    ("stt", 5, 1, 0, "R_28"),
+    ("stt", 5, 1, 1, "R_28"),
+    ("stt", 5, 1, 2, "R_28"),
+    ("stt", 5, 1, 3, "R_28"),
+    ("rg", "V", 4, 0),
+    ("rg", "V", 4, 1),
     ("Q", 4, 0),
     ("Q", 4, 1),
-    ("stage", "st_33", 1024, "st"),
-    ("mx", 7, 0, "acc_34"),
-    ("ev", "S", "acc_34", "st_33", 0),
-    ("mx", 7, 1, "acc_35"),
-    ("ev", "S", "acc_35", "st_33", 512),
-    ("store", "st_33", 7, 0, 2, 0),
-    ("stage", "st_36", 1024, "st"),
-    ("mx", 6, 0, "acc_37"),
-    ("ev", "S", "acc_37", "st_36", 0),
-    ("mx", 6, 1, "acc_38"),
-    ("ev", "S", "acc_38", "st_36", 512),
-    ("store", "st_36", 6, 0, 2, 0),
-    ("R", 6, 0, "R_39"),
-    ("R", 6, 1, "R_40"),
-    ("TT", 5, 0, "R_31"),
-    ("TT", 5, 1, "R_32"),
+    ("stage", "H3", 2048, "hv"),
+    ("mxu", 3, 0, "acc_38"),
+    ("evu", "S", "acc_38", "H3", 0),
+    ("mxu", 3, 1, "acc_39"),
+    ("evu", "S", "acc_39", "H3", 256),
+    ("mxu", 3, 2, "acc_40"),
+    ("evu", "S", "acc_40", "H3", 512),
+    ("mxu", 3, 3, "acc_41"),
+    ("evu", "S", "acc_41", "H3", 768),
+    ("storeu", "H3", 3, 0, 4, 0),
+    ("mxu", 0, 3, "acc_42"),
+    ("stage", "sp_43", 512, "sp"),
+    ("evu", "S", "acc_42", "sp_43", 0),
+    ("storeu", "sp_43", 0, 3, 1, 0),
+    ("mxu", 1, 3, "acc_44"),
+    ("stage", "sp_45", 512, "sp"),
+    ("evu", "S", "acc_44", "sp_45", 0),
+    ("storeu", "sp_45", 1, 3, 1, 0),
+    ("mxu", 2, 3, "acc_46"),
+    ("stage", "sp_47", 512, "sp"),
+    ("evu", "V", "acc_46", "sp_47", 0),
+    ("storeu", "sp_47", 2, 3, 1, 0),
+    ("R", 7, 0, "R_48"),
+    ("R", 7, 1, "R_49"),
+    ("stt", 6, 0, 0, "R_36"),
+    ("stt", 6, 0, 1, "R_36"),
+    ("stt", 6, 0, 2, "R_36"),
+    ("stt", 6, 0, 3, "R_36"),
+    ("stt", 6, 1, 0, "R_37"),
+    ("stt", 6, 1, 1, "R_37"),
+    ("stt", 6, 1, 2, "R_37"),
+    ("stt", 6, 1, 3, "R_37"),
+    ("rg", "V", 5, 0),
+    ("rg", "V", 5, 1),
     ("Q", 5, 0),
     ("Q", 5, 1),
-    ("stage", "st_41", 1024, "st"),
-    ("mx", 9, 0, "acc_42"),
-    ("ev", "S", "acc_42", "st_41", 0),
-    ("mx", 9, 1, "acc_43"),
-    ("ev", "S", "acc_43", "st_41", 512),
-    ("store", "st_41", 9, 0, 2, 0),
-    ("stage", "st_44", 1024, "st"),
-    ("mx", 8, 0, "acc_45"),
-    ("ev", "S", "acc_45", "st_44", 0),
-    ("mx", 8, 1, "acc_46"),
-    ("ev", "S", "acc_46", "st_44", 512),
-    ("store", "st_44", 8, 0, 2, 0),
-    ("R", 7, 0, "R_47"),
-    ("R", 7, 1, "R_48"),
-    ("TT", 6, 0, "R_39"),
-    ("TT", 6, 1, "R_40"),
+    ("stage", "H4", 2560, "hv"),
+    ("mxu", 4, 0, "acc_50"),
+    ("evu", "S", "acc_50", "H4", 0),
+    ("mxu", 4, 1, "acc_51"),
+    ("evu", "S", "acc_51", "H4", 256),
+    ("mxu", 4, 2, "acc_52"),
+    ("evu", "S", "acc_52", "H4", 512),
+    ("mxu", 4, 3, "acc_53"),
+    ("evu", "S", "acc_53", "H4", 768),
+    ("storeu", "H4", 4, 0, 4, 0),
+    ("mxu", 4, 4, "acc_54"),
+    ("evu", "S", "acc_54", "H4", 1024),
+    ("storeu", "H4", 4, 4, 1, 1024),
+    ("mxu", 0, 4, "acc_55"),
+    ("stage", "sp_56", 512, "sp"),
+    ("evu", "S", "acc_55", "sp_56", 0),
+    ("storeu", "sp_56", 0, 4, 1, 0),
+    ("mxu", 1, 4, "acc_57"),
+    ("stage", "sp_58", 512, "sp"),
+    ("evu", "S", "acc_57", "sp_58", 0),
+    ("storeu", "sp_58", 1, 4, 1, 0),
+    ("mxu", 2, 4, "acc_59"),
+    ("stage", "sp_60", 512, "sp"),
+    ("evu", "V", "acc_59", "sp_60", 0),
+    ("storeu", "sp_60", 2, 4, 1, 0),
+    ("mxu", 3, 4, "acc_61"),
+    ("stage", "sp_62", 512, "sp"),
+    ("evu", "V", "acc_61", "sp_62", 0),
+    ("storeu", "sp_62", 3, 4, 1, 0),
+    ("stt", 7, 0, 0, "R_48"),
+    ("stt", 7, 0, 1, "R_48"),
+    ("stt", 7, 0, 2, "R_48"),
+    ("stt", 7, 0, 3, "R_48"),
+    ("stt", 7, 1, 0, "R_49"),
+    ("stt", 7, 1, 1, "R_49"),
+    ("stt", 7, 1, 2, "R_49"),
+    ("stt", 7, 1, 3, "R_49"),
+    ("rg", "V", 6, 0),
+    ("rg", "V", 6, 1),
     ("Q", 6, 0),
     ("Q", 6, 1),
-    ("stage", "st_49", 1536, "st"),
-    ("mx", 11, 0, "acc_50"),
-    ("ev", "S", "acc_50", "st_49", 0),
-    ("mx", 11, 1, "acc_51"),
-    ("ev", "S", "acc_51", "st_49", 512),
-    ("mx", 11, 2, "acc_52"),
-    ("ev", "S", "acc_52", "st_49", 1024),
-    ("store", "st_49", 11, 0, 3, 0),
-    ("stage", "st_53", 512, "s1"),
-    ("mx", 10, 0, "acc_54"),
-    ("ev", "S", "acc_54", "st_53", 0),
-    ("store", "st_53", 10, 0, 1, 0),
-    ("TT", 7, 0, "R_47"),
-    ("TT", 7, 1, "R_48"),
+    ("stage", "H5", 3072, "hv"),
+    ("mxu", 5, 0, "acc_63"),
+    ("evu", "S", "acc_63", "H5", 0),
+    ("mxu", 5, 1, "acc_64"),
+    ("evu", "S", "acc_64", "H5", 256),
+    ("mxu", 5, 2, "acc_65"),
+    ("evu", "S", "acc_65", "H5", 512),
+    ("mxu", 5, 3, "acc_66"),
+    ("evu", "S", "acc_66", "H5", 768),
+    ("storeu", "H5", 5, 0, 4, 0),
+    ("mxu", 5, 4, "acc_67"),
+    ("evu", "S", "acc_67", "H5", 1024),
+    ("mxu", 5, 5, "acc_68"),
+    ("evu", "S", "acc_68", "H5", 1280),
+    ("storeu", "H5", 5, 4, 2, 1024),
+    ("mxu", 0, 5, "acc_69"),
+    ("stage", "sp_70", 512, "sp"),
+    ("evu", "S", "acc_69", "sp_70", 0),
+    ("storeu", "sp_70", 0, 5, 1, 0),
+    ("mxu", 1, 5, "acc_71"),
+    ("stage", "sp_72", 512, "sp"),
+    ("evu", "V", "acc_71", "sp_72", 0),
+    ("storeu", "sp_72", 1, 5, 1, 0),
+    ("mxu", 2, 5, "acc_73"),
+    ("stage", "sp_74", 512, "sp"),
+    ("evu", "V", "acc_73", "sp_74", 0),
+    ("storeu", "sp_74", 2, 5, 1, 0),
+    ("mxu", 3, 5, "acc_75"),
+    ("stage", "sp_76", 512, "sp"),
+    ("evu", "V", "acc_75", "sp_76", 0),
+    ("storeu", "sp_76", 3, 5, 1, 0),
+    ("mxu", 4, 5, "acc_77"),
+    ("stage", "sp_78", 512, "sp"),
+    ("evu", "V", "acc_77", "sp_78", 0),
+    ("storeu", "sp_78", 4, 5, 1, 0),
+    ("rg", "V", 7, 0),
+    ("rg", "V", 7, 1),
     ("Q", 7, 0),
     ("Q", 7, 1),
-    ("stage", "st_55", 1536, "st"),
-    ("mx", 13, 0, "acc_56"),
-    ("ev", "S", "acc_56", "st_55", 0),
-    ("mx", 13, 1, "acc_57"),
-    ("ev", "S", "acc_57", "st_55", 512),
-    ("mx", 13, 2, "acc_58"),
-    ("ev", "S", "acc_58", "st_55", 1024),
-    ("store", "st_55", 13, 0, 3, 0),
-    ("stage", "st_59", 512, "s1"),
-    ("mx", 12, 0, "acc_60"),
-    ("ev", "S", "acc_60", "st_59", 0),
-    ("store", "st_59", 12, 0, 1, 0),
-    ("stage", "st_61", 2048, "st"),
-    ("mx", 15, 0, "acc_62"),
-    ("ev", "S", "acc_62", "st_61", 0),
-    ("mx", 15, 1, "acc_63"),
-    ("ev", "V", "acc_63", "st_61", 512),
-    ("mx", 15, 2, "acc_64"),
-    ("ev", "S", "acc_64", "st_61", 1024),
-    ("mx", 15, 3, "acc_65"),
-    ("ev", "V", "acc_65", "st_61", 1536),
-    ("store", "st_61", 15, 0, 4, 0),
-    ("stage", "st_66", 2048, "st"),
-    ("mx", 14, 0, "acc_67"),
-    ("ev", "S", "acc_67", "st_66", 0),
-    ("mx", 14, 1, "acc_68"),
-    ("ev", "V", "acc_68", "st_66", 512),
-    ("mx", 14, 2, "acc_69"),
-    ("ev", "S", "acc_69", "st_66", 1024),
-    ("mx", 14, 3, "acc_70"),
-    ("ev", "V", "acc_70", "st_66", 1536),
-    ("store", "st_66", 14, 0, 4, 0),
-    ("stage", "st_71", 512, "s1"),
-    ("mx", 13, 3, "acc_72"),
-    ("ev", "S", "acc_72", "st_71", 0),
-    ("store", "st_71", 13, 3, 1, 0),
-    ("stage", "st_73", 1536, "st"),
-    ("mx", 12, 1, "acc_74"),
-    ("ev", "V", "acc_74", "st_73", 0),
-    ("mx", 12, 2, "acc_75"),
-    ("ev", "S", "acc_75", "st_73", 512),
-    ("mx", 12, 3, "acc_76"),
-    ("ev", "V", "acc_76", "st_73", 1024),
-    ("store", "st_73", 12, 1, 3, 0),
-    ("stage", "st_77", 512, "s1"),
-    ("mx", 11, 3, "acc_78"),
-    ("ev", "S", "acc_78", "st_77", 0),
-    ("store", "st_77", 11, 3, 1, 0),
-    ("stage", "st_79", 1536, "st"),
-    ("mx", 10, 1, "acc_80"),
-    ("ev", "V", "acc_80", "st_79", 0),
-    ("mx", 10, 2, "acc_81"),
-    ("ev", "S", "acc_81", "st_79", 512),
-    ("mx", 10, 3, "acc_82"),
-    ("ev", "V", "acc_82", "st_79", 1024),
-    ("store", "st_79", 10, 1, 3, 0),
-    ("stage", "st_83", 1024, "st"),
-    ("mx", 9, 2, "acc_84"),
-    ("ev", "S", "acc_84", "st_83", 0),
-    ("mx", 9, 3, "acc_85"),
-    ("ev", "V", "acc_85", "st_83", 512),
-    ("store", "st_83", 9, 2, 2, 0),
-    ("stage", "st_86", 1024, "st"),
-    ("mx", 8, 2, "acc_87"),
-    ("ev", "S", "acc_87", "st_86", 0),
-    ("mx", 8, 3, "acc_88"),
-    ("ev", "V", "acc_88", "st_86", 512),
-    ("store", "st_86", 8, 2, 2, 0),
-    ("stage", "st_89", 1024, "st"),
-    ("mx", 7, 2, "acc_90"),
-    ("ev", "S", "acc_90", "st_89", 0),
-    ("mx", 7, 3, "acc_91"),
-    ("ev", "V", "acc_91", "st_89", 512),
-    ("store", "st_89", 7, 2, 2, 0),
-    ("stage", "st_92", 1024, "st"),
-    ("mx", 6, 2, "acc_93"),
-    ("ev", "S", "acc_93", "st_92", 0),
-    ("mx", 6, 3, "acc_94"),
-    ("ev", "V", "acc_94", "st_92", 512),
-    ("store", "st_92", 6, 2, 2, 0),
-    ("stage", "st_95", 1536, "st"),
-    ("mx", 5, 1, "acc_96"),
-    ("ev", "S", "acc_96", "st_95", 0),
-    ("mx", 5, 2, "acc_97"),
-    ("ev", "V", "acc_97", "st_95", 512),
-    ("mx", 5, 3, "acc_98"),
-    ("ev", "S", "acc_98", "st_95", 1024),
-    ("store", "st_95", 5, 1, 3, 0),
-    ("stage", "st_99", 1536, "st"),
-    ("mx", 4, 1, "acc_100"),
-    ("ev", "V", "acc_100", "st_99", 0),
-    ("mx", 4, 2, "acc_101"),
-    ("ev", "S", "acc_101", "st_99", 512),
-    ("mx", 4, 3, "acc_102"),
-    ("ev", "V", "acc_102", "st_99", 1024),
-    ("store", "st_99", 4, 1, 3, 0),
-    ("stage", "st_103", 1536, "st"),
-    ("mx", 3, 1, "acc_104"),
-    ("ev", "S", "acc_104", "st_103", 0),
-    ("mx", 3, 2, "acc_105"),
-    ("ev", "V", "acc_105", "st_103", 512),
-    ("mx", 3, 3, "acc_106"),
-    ("ev", "S", "acc_106", "st_103", 1024),
-    ("store", "st_103", 3, 1, 3, 0),
-    ("stage", "st_107", 1536, "st"),
-    ("mx", 2, 1, "acc_108"),
-    ("ev", "V", "acc_108", "st_107", 0),
-    ("mx", 2, 2, "acc_109"),
-    ("ev", "S", "acc_109", "st_107", 512),
-    ("mx", 2, 3, "acc_110"),
-    ("ev", "V", "acc_110", "st_107", 1024),
-    ("store", "st_107", 2, 1, 3, 0),
-    ("stage", "st_111", 512, "s1"),
-    ("mx", 1, 1, "acc_112"),
-    ("ev", "S", "acc_112", "st_111", 0),
-    ("store", "st_111", 1, 1, 1, 0),
-    ("stage", "st_113", 512, "s1"),
-    ("mx", 1, 2, "acc_114"),
-    ("ev", "V", "acc_114", "st_113", 0),
-    ("store", "st_113", 1, 2, 1, 0),
-    ("stage", "st_115", 512, "s1"),
-    ("mx", 1, 3, "acc_116"),
-    ("ev", "S", "acc_116", "st_115", 0),
-    ("store", "st_115", 1, 3, 1, 0),
-    ("stage", "st_117", 512, "s1"),
-    ("mx", 0, 1, "acc_118"),
-    ("ev", "V", "acc_118", "st_117", 0),
-    ("store", "st_117", 0, 1, 1, 0),
-    ("stage", "st_119", 512, "s1"),
-    ("mx", 0, 2, "acc_120"),
-    ("ev", "S", "acc_120", "st_119", 0),
-    ("store", "st_119", 0, 2, 1, 0),
-    ("stage", "st_121", 512, "s1"),
-    ("mx", 0, 3, "acc_122"),
-    ("ev", "V", "acc_122", "st_121", 0),
-    ("store", "st_121", 0, 3, 1, 0),
+    ("stage", "H6", 3584, "hv"),
+    ("mxu", 6, 0, "acc_79"),
+    ("evu", "S", "acc_79", "H6", 0),
+    ("mxu", 6, 1, "acc_80"),
+    ("evu", "S", "acc_80", "H6", 256),
+    ("mxu", 6, 2, "acc_81"),
+    ("evu", "S", "acc_81", "H6", 512),
+    ("mxu", 6, 3, "acc_82"),
+    ("evu", "S", "acc_82", "H6", 768),
+    ("storeu", "H6", 6, 0, 4, 0),
+    ("mxu", 6, 4, "acc_83"),
+    ("evu", "S", "acc_83", "H6", 1024),
+    ("mxu", 6, 5, "acc_84"),
+    ("evu", "S", "acc_84", "H6", 1280),
+    ("mxu", 6, 6, "acc_85"),
+    ("evu", "S", "acc_85", "H6", 1536),
+    ("storeu", "H6", 6, 4, 3, 1024),
+    ("mxu", 0, 6, "acc_86"),
+    ("stage", "sp_87", 512, "sp"),
+    ("evu", "V", "acc_86", "sp_87", 0),
+    ("storeu", "sp_87", 0, 6, 1, 0),
+    ("mxu", 1, 6, "acc_88"),
+    ("stage", "sp_89", 512, "sp"),
+    ("evu", "V", "acc_88", "sp_89", 0),
+    ("storeu", "sp_89", 1, 6, 1, 0),
+    ("mxu", 2, 6, "acc_90"),
+    ("stage", "sp_91", 512, "sp"),
+    ("evu", "V", "acc_90", "sp_91", 0),
+    ("storeu", "sp_91", 2, 6, 1, 0),
+    ("mxu", 3, 6, "acc_92"),
+    ("stage", "sp_93", 512, "sp"),
+    ("evu", "V", "acc_92", "sp_93", 0),
+    ("storeu", "sp_93", 3, 6, 1, 0),
+    ("mxu", 4, 6, "acc_94"),
+    ("stage", "sp_95", 512, "sp"),
+    ("evu", "V", "acc_94", "sp_95", 0),
+    ("storeu", "sp_95", 4, 6, 1, 0),
+    ("mxu", 5, 6, "acc_96"),
+    ("stage", "sp_97", 512, "sp"),
+    ("evu", "V", "acc_96", "sp_97", 0),
+    ("storeu", "sp_97", 5, 6, 1, 0),
+    ("stage", "H7", 4096, "hv"),
+    ("mxu", 7, 0, "acc_98"),
+    ("evu", "S", "acc_98", "H7", 0),
+    ("mxu", 7, 1, "acc_99"),
+    ("evu", "S", "acc_99", "H7", 256),
+    ("mxu", 7, 2, "acc_100"),
+    ("evu", "S", "acc_100", "H7", 512),
+    ("mxu", 7, 3, "acc_101"),
+    ("evu", "S", "acc_101", "H7", 768),
+    ("storeu", "H7", 7, 0, 4, 0),
+    ("mxu", 7, 4, "acc_102"),
+    ("evu", "S", "acc_102", "H7", 1024),
+    ("mxu", 7, 5, "acc_103"),
+    ("evu", "S", "acc_103", "H7", 1280),
+    ("mxu", 7, 6, "acc_104"),
+    ("evu", "S", "acc_104", "H7", 1536),
+    ("mxu", 7, 7, "acc_105"),
+    ("evu", "S", "acc_105", "H7", 1792),
+    ("storeu", "H7", 7, 4, 4, 1024),
+    ("mxu", 0, 7, "acc_106"),
+    ("stage", "sp_107", 512, "sp"),
+    ("evu", "V", "acc_106", "sp_107", 0),
+    ("storeu", "sp_107", 0, 7, 1, 0),
+    ("mxu", 1, 7, "acc_108"),
+    ("stage", "sp_109", 512, "sp"),
+    ("evu", "V", "acc_108", "sp_109", 0),
+    ("storeu", "sp_109", 1, 7, 1, 0),
+    ("mxu", 2, 7, "acc_110"),
+    ("stage", "sp_111", 512, "sp"),
+    ("evu", "V", "acc_110", "sp_111", 0),
+    ("storeu", "sp_111", 2, 7, 1, 0),
+    ("mxu", 3, 7, "acc_112"),
+    ("stage", "sp_113", 512, "sp"),
+    ("evu", "V", "acc_112", "sp_113", 0),
+    ("storeu", "sp_113", 3, 7, 1, 0),
+    ("mxu", 4, 7, "acc_114"),
+    ("stage", "sp_115", 512, "sp"),
+    ("evu", "V", "acc_114", "sp_115", 0),
+    ("storeu", "sp_115", 4, 7, 1, 0),
+    ("mxu", 5, 7, "acc_116"),
+    ("stage", "sp_117", 512, "sp"),
+    ("evu", "V", "acc_116", "sp_117", 0),
+    ("storeu", "sp_117", 5, 7, 1, 0),
+    ("mxu", 6, 7, "acc_118"),
+    ("stage", "sp_119", 512, "sp"),
+    ("evu", "V", "acc_118", "sp_119", 0),
+    ("storeu", "sp_119", 6, 7, 1, 0),
 ]
 
 
 def tile_attentive_kernel(tc, x, attn_vectors, out):
     nc = tc.nc
     with ExitStack() as ctx:
-        if MANUAL:
-            ctx.enter_context(tc.manual_schedule())
+        ctx.enter_context(tc.manual_schedule())
         keep = ctx.enter_context(tc.tile_pool(name="keep", bufs=1))
         small = ctx.enter_context(tc.tile_pool(name="small", bufs=4))
+        ypool = ctx.enter_context(tc.tile_pool(name="yp", bufs=3))
+        gpool = ctx.enter_context(tc.tile_pool(name="gp", bufs=3))
         pools = {
-            "st": ctx.enter_context(tc.tile_pool(name="st", bufs=5)),
-            "s1": ctx.enter_context(tc.tile_pool(name="s1", bufs=8)),
+            "hv": ctx.enter_context(tc.tile_pool(name="hv", bufs=3)),
+            "sp": ctx.enter_context(tc.tile_pool(name="sp", bufs=8)),
             "fr": ctx.enter_context(tc.psum_pool(name="fr", bufs=4)),
             "acc": ctx.enter_context(tc.psum_pool(name="acc", bufs=4)),
         }
@@ -366,8 +409,6 @@ def tile_attentive_kernel(tc, x, attn_vectors, out):
         aT_f = keep.tile([P, 2 * H], F32)
         a2T = keep.tile([P, 2, H], F32)
         r_sb = keep.tile([P, NT * H], F32)
-        xa = keep.tile([P, 2, 4, N], F32)
-        grouped = keep.tile([P, 2, N, 4], BF16, align_bytes=64)
         codes = keep.tile([P, 2, N], U32, align_bytes=64)
         scl = keep.tile([P, 2, N], U8, align_bytes=64)
 
@@ -397,48 +438,12 @@ def tile_attentive_kernel(tc, x, attn_vectors, out):
                     in_=tiles[key][:].bitcast(BF16).rearrange("p (n e) -> p e n", e=2),
                     func=ACT.Square,
                 )
-            elif op == "sqs":
-                g = call[1]
-                nc.scalar.activation(
-                    out=x2T[:, :, g * CH:(g + 1) * CH],
-                    in_=xT_b[:, g * CH:(g + 1) * CH, :].rearrange("p n e -> p e n"),
-                    func=ACT.Square,
-                )
             elif op == "cp":
                 g, key = call[1], call[2]
                 nc.vector.tensor_copy(out=xT_w[:, g * CH:(g + 1) * CH], in_=tiles[key][:])
-            elif op == "cps":
-                g, key = call[1], call[2]
-                nc.scalar.copy(out=xT_w[:, g * CH:(g + 1) * CH], in_=tiles[key][:])
-            elif op == "xa":
-                eng, g, k = call[1], call[2], call[3]
-                c, t = k // 4, k % 4
-                h, e = 2 * c + t // 2, t % 2
-                if eng == "V":
-                    nc.vector.tensor_scalar_mul(
-                        out=xa[:, c, t, g * CH:(g + 1) * CH],
-                        in0=xT_b[:, g * CH:(g + 1) * CH, e],
-                        scalar1=aT_f[:, 2 * h + e:2 * h + e + 1],
-                    )
-                elif eng == "S":
-                    nc.scalar.activation(
-                        out=xa[:, c, t, g * CH:(g + 1) * CH],
-                        in_=xT_b[:, g * CH:(g + 1) * CH, e],
-                        func=ACT.Copy,
-                        scale=aT_f[:, 2 * h + e:2 * h + e + 1],
-                    )
-                else:
-                    nc.gpsimd.tensor_scalar(
-                        out=xa[:, c, t, g * CH:(g + 1) * CH],
-                        in0=xT_b[:, g * CH:(g + 1) * CH, e],
-                        scalar1=aT_f[:, 2 * h + e:2 * h + e + 1],
-                        scalar2=0.0,
-                        op0=ALU.mult,
-                        op1=ALU.add,
-                    )
             elif op == "smm":
                 g, key = call[1], call[2]
-                tl = pools["fr"].tile([P, 4 * H], F32, tag="fr")
+                tl = pools["acc"].tile([P, 4 * H], F32, tag="acc")
                 tiles[key] = tl
                 for j in range(4):
                     t = 4 * g + j
@@ -475,68 +480,87 @@ def tile_attentive_kernel(tc, x, attn_vectors, out):
                             r_sb[:, col:col + 1].to_broadcast([P, P]),
                             ident_f[:],
                         )
-            elif op == "TT":
-                u, c, key = call[1], call[2], call[3]
-                n0 = u * PR
-                nc.vector.tensor_tensor(
-                    out=grouped[:, c, n0:n0 + PR, :].rearrange("p n (h e) -> p n h e", e=2),
-                    in0=xa[:, c, :, n0:n0 + PR].rearrange("p (h e) n -> p n h e", e=2),
-                    in1=tiles[key][:].rearrange("p h n -> p n h").unsqueeze(3).to_broadcast([P, PR, 2, 2]),
-                    op=ALU.mult,
+            elif op == "stt":
+                u, c, t, key = call[1], call[2], call[3], call[4]
+                if c == 0 and t == 0:
+                    yp = ypool.tile([P, 2, 4, PR], BF16, tag="yp")
+                    tiles["yp%d" % u] = yp
+                h, e = 2 * c + t // 2, t % 2
+                nc.vector.scalar_tensor_tensor(
+                    out=tiles["yp%d" % u][:, c, t, :],
+                    in0=xT_b[:, u * PR:(u + 1) * PR, e],
+                    scalar=aT_f[:, 2 * h + e:2 * h + e + 1],
+                    in1=tiles[key][:, t // 2, :],
+                    op0=ALU.mult,
+                    op1=ALU.mult,
                 )
+            elif op == "rg":
+                eng, u, c = call[1], call[2], call[3]
+                if ("gp%d" % u) not in tiles:
+                    gp = gpool.tile([P, 2, PR, 4], BF16, tag="gp", align_bytes=64)
+                    tiles["gp%d" % u] = gp
+                dst = tiles["gp%d" % u][:, c, :, :].rearrange("p (m i) t -> p m t i", i=4)
+                src = tiles["yp%d" % u][:, c, :, :].rearrange("p t (m i) -> p m t i", i=4)
+                if eng == "V":
+                    nc.vector.tensor_copy(out=dst, in_=src)
+                else:
+                    nc.scalar.copy(out=dst, in_=src)
             elif op == "Q":
                 u, c = call[1], call[2]
                 n0 = u * PR
                 nc.vector.quantize_mx(
                     out=codes[:, c, n0:n0 + PR].bitcast(FP8X4),
                     scales=scl[:, c, n0:n0 + PR],
-                    in_=grouped[:, c, n0:n0 + PR, :].rearrange("p n j -> p (n j)"),
+                    in_=tiles["gp%d" % u][:, c, :, :].rearrange("p n j -> p (n j)"),
                 )
             elif op == "stage":
                 key, width, tag = call[1], call[2], call[3]
-                tl = pools[tag].tile([P, width], F32, tag=tag)
+                tl = pools[tag].tile([P, 2, width // 2], F32, tag=tag)
                 tiles[key] = tl
-            elif op == "mx":
-                i, jc, key = call[1], call[2], call[3]
-                tl = pools["acc"].tile([P, CH], F32, tag="acc")
+            elif op == "mxu":
+                v, w, key = call[1], call[2], call[3]
+                tl = pools["acc"].tile([P, 2, PR], F32, tag="acc")
                 tiles[key] = tl
-                for c in range(2):
-                    nc.tensor.matmul_mx(
-                        out=tl[:],
-                        lhsT=codes[:, c, i * P:(i + 1) * P].bitcast(FP8X4),
-                        lhsT_scale=scl[:, c, i * P:(i + 1) * P],
-                        rhs=codes[:, c, jc * CH:(jc + 1) * CH].bitcast(FP8X4),
-                        rhs_scale=scl[:, c, jc * CH:(jc + 1) * CH],
-                        start=(c == 0),
-                        stop=(c == 1),
-                    )
-            elif op == "ev":
+                for r in range(2):
+                    i = 2 * v + r
+                    for c in range(2):
+                        nc.tensor.matmul_mx(
+                            out=tl[:, r, :],
+                            lhsT=codes[:, c, i * P:(i + 1) * P].bitcast(FP8X4),
+                            lhsT_scale=scl[:, c, i * P:(i + 1) * P],
+                            rhs=codes[:, c, w * PR:(w + 1) * PR].bitcast(FP8X4),
+                            rhs_scale=scl[:, c, w * PR:(w + 1) * PR],
+                            start=(c == 0),
+                            stop=(c == 1),
+                        )
+            elif op == "evu":
                 eng, key, st, off = call[1], call[2], call[3], call[4]
                 if eng == "V":
-                    nc.vector.tensor_scalar_mul(out=tiles[st][:, off:off + CH], in0=tiles[key][:], scalar1=0.25)
+                    nc.vector.tensor_scalar_mul(out=tiles[st][:, :, off:off + PR], in0=tiles[key][:], scalar1=0.25)
                 else:
-                    nc.scalar.mul(out=tiles[st][:, off:off + CH], in_=tiles[key][:], mul=0.25)
-            elif op == "mir":
-                j, jp, key = call[1], call[2], call[3]
-                tl = pools["acc"].tile([P, CH], F32, tag="acc")
+                    nc.scalar.mul(out=tiles[st][:, :, off:off + PR], in_=tiles[key][:], mul=0.25)
+            elif op == "miru":
+                w, v, key = call[1], call[2], call[3]
+                tl = pools["acc"].tile([P, 2, PR], F32, tag="acc")
                 tiles[key] = tl
-                for q in range(4):
-                    nc.tensor.transpose(
-                        tl[:, q * P:(q + 1) * P],
-                        tiles["hd%d" % (4 * jp + q)][:, j * P:(j + 1) * P],
-                        ident_f[:],
-                    )
-            elif op == "evc":
+                for r in range(2):
+                    for q in range(2):
+                        nc.tensor.transpose(
+                            tl[:, r, q * P:(q + 1) * P],
+                            tiles["H%d" % v][:, q, (2 * w + r) * P:(2 * w + r + 1) * P],
+                            ident_f[:],
+                        )
+            elif op == "evm":
                 eng, key, st, off = call[1], call[2], call[3], call[4]
                 if eng == "V":
-                    nc.vector.tensor_copy(out=tiles[st][:, off:off + CH], in_=tiles[key][:])
+                    nc.vector.tensor_copy(out=tiles[st][:, :, off:off + PR], in_=tiles[key][:])
                 else:
-                    nc.scalar.copy(out=tiles[st][:, off:off + CH], in_=tiles[key][:])
-            elif op == "store":
-                st, i, j0, nj, off = call[1], call[2], call[3], call[4], call[5]
+                    nc.scalar.copy(out=tiles[st][:, :, off:off + PR], in_=tiles[key][:])
+            elif op == "storeu":
+                st, v, w0, m, off = call[1], call[2], call[3], call[4], call[5]
                 nc.sync.dma_start(
-                    out=out[i * P:(i + 1) * P, j0 * CH:(j0 + nj) * CH],
-                    in_=tiles[st][:, off:off + nj * CH],
+                    out=out[v * PR:(v + 1) * PR, w0 * PR:(w0 + m) * PR].rearrange("(r p) c -> p r c", p=P),
+                    in_=tiles[st][:, :, off:off + m * PR],
                 )
             else:
                 assert False, op

@@ -16,360 +16,329 @@ K = H * D
 P = 128
 NT = N // P
 CH = 512
-NCH = N // CH
 PR = 256
 EPS = 1e-12
 FLOPS = 2 * N * N * K
+UNITS = ((0, 2), (2, 2), (4, 4), (8, 4), (12, 4))
 
 PROGRAM = [
-    ("xt", 0, "xtS_0", "acc"),
-    ("xt", 0, "xtV_1", "acc"),
-    ("sqp", 0, "xtS_0"),
-    ("cp", 0, "xtV_1"),
-    ("xt", 1, "xtS_3", "acc"),
-    ("xt", 1, "xtV_4", "acc"),
-    ("sqp", 1, "xtS_3"),
-    ("cp", 1, "xtV_4"),
-    ("smm", 0, "s_2"),
-    ("max", 0, "s_2"),
-    ("sqrt", 0),
-    ("rec", 0),
-    ("xt", 2, "xtS_6", "acc"),
-    ("xt", 2, "xtV_7", "acc"),
-    ("sqp", 2, "xtS_6"),
-    ("R", 0, 0, "R_12"),
-    ("R", 0, 1, "R_13"),
-    ("R", 1, 0, "R_14"),
-    ("R", 1, 1, "R_15"),
-    ("cp", 2, "xtV_7"),
-    ("smm", 1, "s_5"),
-    ("xt", 3, "xtS_9", "acc"),
-    ("xt", 3, "xtV_10", "acc"),
-    ("sqp", 3, "xtS_9"),
-    ("smm", 2, "s_8"),
-    ("stt", 0, 0, 0, "R_12"),
-    ("stt", 0, 0, 1, "R_12"),
-    ("stt", 0, 0, 2, "R_12"),
-    ("stt", 0, 0, 3, "R_12"),
-    ("max", 1, "s_5"),
-    ("sqrt", 1),
-    ("stt", 0, 1, 0, "R_13"),
-    ("stt", 0, 1, 1, "R_13"),
-    ("stt", 0, 1, 2, "R_13"),
-    ("stt", 0, 1, 3, "R_13"),
-    ("rec", 1),
-    ("cp", 3, "xtV_10"),
-    ("rg", "S", 0, 0),
-    ("rg", "S", 0, 1),
-    ("R", 2, 0, "R_16"),
-    ("R", 2, 1, "R_17"),
-    ("stt", 1, 0, 0, "R_14"),
-    ("stt", 1, 0, 1, "R_14"),
-    ("stt", 1, 0, 2, "R_14"),
-    ("stt", 1, 0, 3, "R_14"),
-    ("max", 2, "s_8"),
-    ("sqrt", 2),
-    ("smm", 3, "s_11"),
-    ("stt", 1, 1, 0, "R_15"),
-    ("stt", 1, 1, 1, "R_15"),
-    ("stt", 1, 1, 2, "R_15"),
-    ("stt", 1, 1, 3, "R_15"),
-    ("rec", 2),
-    ("rg", "S", 1, 0),
-    ("rg", "S", 1, 1),
+    ("dm", "dm0"),
+    ("dm", "dm1"),
+    ("dm", "dm2"),
+    ("dm", "dm3"),
+    ("dm", "dm4"),
+    ("dm", "dm5"),
+    ("dm", "dm6"),
+    ("dm", "dm7"),
+    ("dm", "dm8"),
+    ("dm", "dm9"),
+    ("dm", "dm10"),
+    ("aT",),
+    ("xt", 0, 2, "xt0"),
+    ("dm", "dm11"),
+    ("aTf",),
+    ("sqp", 0, 2, "xt0"),
+    ("xt", 2, 2, "xt1"),
+    ("dm", "dm12"),
+    ("dm", "dm13"),
+    ("a2T",),
+    ("cpx", "S", 0, 2, "xt0"),
+    ("dm", "dm14"),
+    ("sqp", 2, 2, "xt1"),
+    ("smm", 0, 2, "s0"),
+    ("xa4", "V", 0, 2, 0),
+    ("xt", 4, 4, "xt2"),
+    ("cpx", "S", 2, 2, "xt1"),
+    ("smm", 2, 2, "s1"),
+    ("xa4", "S", 2, 2, 0),
+    ("max", 0, 0, 2, "s0"),
+    ("xa4", "V", 0, 2, 1),
+    ("dm", "dm15"),
+    ("dm", "dm16"),
+    ("xt", 8, 4, "xt3"),
+    ("max", 1, 2, 2, "s1"),
+    ("sqrt", 0, 2),
+    ("xa4", "V", 2, 2, 1),
+    ("sqp", 4, 4, "xt2"),
+    ("xt", 12, 4, "xt4"),
+    ("rec", 0, 0, 2),
+    ("R", 0, 0, "R0_0"),
+    ("sqrt", 1, 2),
+    ("cpx", "S", 4, 4, "xt2"),
+    ("smm", 4, 4, "s2"),
+    ("rec", 1, 2, 2),
+    ("TT", 0, 0, "R0_0"),
+    ("xa4", "S", 4, 4, 0),
+    ("R", 0, 1, "R0_1"),
+    ("max", 2, 4, 4, "s2"),
+    ("R", 1, 0, "R1_0"),
+    ("TT", 0, 1, "R0_1"),
+    ("R", 1, 1, "R1_1"),
+    ("sqrt", 2, 4),
     ("Q", 0, 0),
+    ("sqp", 8, 4, "xt3"),
+    ("rec", 2, 4, 4),
     ("Q", 0, 1),
-    ("R", 3, 0, "R_18"),
-    ("R", 3, 1, "R_19"),
-    ("stt", 2, 0, 0, "R_16"),
-    ("stt", 2, 0, 1, "R_16"),
-    ("stt", 2, 0, 2, "R_16"),
-    ("stt", 2, 0, 3, "R_16"),
-    ("max", 3, "s_11"),
-    ("sqrt", 3),
-    ("stt", 2, 1, 0, "R_17"),
-    ("stt", 2, 1, 1, "R_17"),
-    ("stt", 2, 1, 2, "R_17"),
-    ("stt", 2, 1, 3, "R_17"),
-    ("rec", 3),
-    ("rg", "S", 2, 0),
-    ("rg", "S", 2, 1),
+    ("R", 2, 0, "R2_0"),
+    ("TT", 1, 0, "R1_0"),
+    ("xa4", "S", 4, 4, 1),
+    ("mxu", 0, 0, "a0_0"),
+    ("cpx", "V", 8, 4, "xt3"),
+    ("TT", 1, 1, "R1_1"),
+    ("smm", 8, 4, "s3"),
+    ("xa4", "G", 8, 4, 0),
+    ("stage", "H0", 256, "hv"),
+    ("evu", "S", "a0_0", "H0", 0),
     ("Q", 1, 0),
+    ("R", 2, 1, "R2_1"),
     ("Q", 1, 1),
-    ("stage", "H0", 512, "hv"),
-    ("mxu", 0, 0, "acc_20"),
-    ("evu", "S", "acc_20", "H0", 0),
+    ("sqp", 12, 4, "xt4"),
+    ("R", 3, 0, "R3_0"),
+    ("max", 3, 8, 4, "s3"),
+    ("TT", 2, 0, "R2_0"),
     ("storeu", "H0", 0, 0, 1, 0),
-    ("R", 4, 0, "R_21"),
-    ("R", 4, 1, "R_22"),
-    ("stt", 3, 0, 0, "R_18"),
-    ("stt", 3, 0, 1, "R_18"),
-    ("stt", 3, 0, 2, "R_18"),
-    ("stt", 3, 0, 3, "R_18"),
-    ("stt", 3, 1, 0, "R_19"),
-    ("stt", 3, 1, 1, "R_19"),
-    ("stt", 3, 1, 2, "R_19"),
-    ("stt", 3, 1, 3, "R_19"),
+    ("mxu", 1, 0, "a1_0"),
+    ("sqrt", 3, 4),
+    ("mxu", 1, 1, "a1_1"),
+    ("cpx", "S", 12, 4, "xt4"),
+    ("TT", 2, 1, "R2_1"),
+    ("R", 3, 1, "R3_1"),
+    ("xa4", "G", 8, 4, 1),
+    ("stage", "H1", 512, "hv"),
+    ("evu", "S", "a1_0", "H1", 0),
+    ("smm", 12, 4, "s4"),
+    ("evu", "S", "a1_1", "H1", 256),
+    ("rec", 3, 8, 4),
     ("Q", 2, 0),
     ("Q", 2, 1),
-    ("stage", "H1", 1024, "hv"),
-    ("mxu", 1, 0, "acc_23"),
-    ("evu", "S", "acc_23", "H1", 0),
-    ("mxu", 1, 1, "acc_24"),
-    ("evu", "S", "acc_24", "H1", 256),
     ("storeu", "H1", 1, 0, 2, 0),
-    ("mxu", 0, 1, "acc_25"),
-    ("stage", "sp_26", 512, "sp"),
-    ("evu", "S", "acc_25", "sp_26", 0),
-    ("storeu", "sp_26", 0, 1, 1, 0),
-    ("R", 5, 0, "R_27"),
-    ("R", 5, 1, "R_28"),
-    ("stt", 4, 0, 0, "R_21"),
-    ("stt", 4, 0, 1, "R_21"),
-    ("stt", 4, 0, 2, "R_21"),
-    ("stt", 4, 0, 3, "R_21"),
-    ("stt", 4, 1, 0, "R_22"),
-    ("stt", 4, 1, 1, "R_22"),
-    ("stt", 4, 1, 2, "R_22"),
-    ("stt", 4, 1, 3, "R_22"),
-    ("rg", "V", 3, 0),
-    ("rg", "V", 3, 1),
+    ("TT", 3, 0, "R3_0"),
+    ("miru", 0, 1, "b0_1"),
+    ("mxu", 2, 0, "a2_0"),
+    ("stage", "sp0_1", 256, "sp"),
+    ("evm", "S", "b0_1", "sp0_1", 0),
+    ("mxu", 2, 1, "a2_1"),
+    ("max", 4, 12, 4, "s4"),
+    ("TT", 3, 1, "R3_1"),
+    ("stage", "H2", 768, "hv"),
+    ("evu", "S", "a2_0", "H2", 0),
+    ("storeu", "sp0_1", 0, 1, 1, 0),
+    ("mxu", 2, 2, "a2_2"),
+    ("xa4", "G", 12, 4, 0),
+    ("evu", "S", "a2_1", "H2", 256),
+    ("miru", 0, 2, "b0_2"),
+    ("evu", "S", "a2_2", "H2", 512),
     ("Q", 3, 0),
+    ("miru", 1, 2, "b1_2"),
     ("Q", 3, 1),
-    ("stage", "H2", 1536, "hv"),
-    ("mxu", 2, 0, "acc_29"),
-    ("evu", "S", "acc_29", "H2", 0),
-    ("mxu", 2, 1, "acc_30"),
-    ("evu", "S", "acc_30", "H2", 256),
-    ("mxu", 2, 2, "acc_31"),
-    ("evu", "S", "acc_31", "H2", 512),
+    ("stage", "sp0_2", 256, "sp"),
+    ("evm", "S", "b0_2", "sp0_2", 0),
+    ("R", 4, 0, "R4_0"),
     ("storeu", "H2", 2, 0, 3, 0),
-    ("mxu", 0, 2, "acc_32"),
-    ("stage", "sp_33", 512, "sp"),
-    ("evu", "S", "acc_32", "sp_33", 0),
-    ("storeu", "sp_33", 0, 2, 1, 0),
-    ("mxu", 1, 2, "acc_34"),
-    ("stage", "sp_35", 512, "sp"),
-    ("evu", "S", "acc_34", "sp_35", 0),
-    ("storeu", "sp_35", 1, 2, 1, 0),
-    ("R", 6, 0, "R_36"),
-    ("R", 6, 1, "R_37"),
-    ("stt", 5, 0, 0, "R_27"),
-    ("stt", 5, 0, 1, "R_27"),
-    ("stt", 5, 0, 2, "R_27"),
-    ("stt", 5, 0, 3, "R_27"),
-    ("stt", 5, 1, 0, "R_28"),
-    ("stt", 5, 1, 1, "R_28"),
-    ("stt", 5, 1, 2, "R_28"),
-    ("stt", 5, 1, 3, "R_28"),
-    ("rg", "V", 4, 0),
-    ("rg", "V", 4, 1),
+    ("R", 4, 1, "R4_1"),
+    ("stage", "sp1_2", 256, "sp"),
+    ("evm", "S", "b1_2", "sp1_2", 0),
+    ("TT", 4, 0, "R4_0"),
+    ("mxu", 3, 0, "a3_0"),
+    ("storeu", "sp0_2", 0, 2, 1, 0),
+    ("sqrt", 4, 4),
+    ("mxu", 3, 1, "a3_1"),
+    ("storeu", "sp1_2", 1, 2, 1, 0),
+    ("stage", "H3", 1024, "hv"),
+    ("evu", "S", "a3_0", "H3", 0),
+    ("rec", 4, 12, 4),
+    ("xa4", "G", 12, 4, 1),
+    ("TT", 4, 1, "R4_1"),
+    ("mxu", 3, 2, "a3_2"),
+    ("evu", "S", "a3_1", "H3", 256),
+    ("mxu", 3, 3, "a3_3"),
+    ("evu", "S", "a3_2", "H3", 512),
     ("Q", 4, 0),
+    ("miru", 0, 3, "b0_3"),
+    ("evu", "S", "a3_3", "H3", 768),
     ("Q", 4, 1),
-    ("stage", "H3", 2048, "hv"),
-    ("mxu", 3, 0, "acc_38"),
-    ("evu", "S", "acc_38", "H3", 0),
-    ("mxu", 3, 1, "acc_39"),
-    ("evu", "S", "acc_39", "H3", 256),
-    ("mxu", 3, 2, "acc_40"),
-    ("evu", "S", "acc_40", "H3", 512),
-    ("mxu", 3, 3, "acc_41"),
-    ("evu", "S", "acc_41", "H3", 768),
+    ("miru", 1, 3, "b1_3"),
+    ("miru", 2, 3, "b2_3"),
+    ("stage", "sp0_3", 256, "sp"),
+    ("evm", "S", "b0_3", "sp0_3", 0),
     ("storeu", "H3", 3, 0, 4, 0),
-    ("mxu", 0, 3, "acc_42"),
-    ("stage", "sp_43", 512, "sp"),
-    ("evu", "S", "acc_42", "sp_43", 0),
-    ("storeu", "sp_43", 0, 3, 1, 0),
-    ("mxu", 1, 3, "acc_44"),
-    ("stage", "sp_45", 512, "sp"),
-    ("evu", "S", "acc_44", "sp_45", 0),
-    ("storeu", "sp_45", 1, 3, 1, 0),
-    ("mxu", 2, 3, "acc_46"),
-    ("stage", "sp_47", 512, "sp"),
-    ("evu", "V", "acc_46", "sp_47", 0),
-    ("storeu", "sp_47", 2, 3, 1, 0),
-    ("R", 7, 0, "R_48"),
-    ("R", 7, 1, "R_49"),
-    ("stt", 6, 0, 0, "R_36"),
-    ("stt", 6, 0, 1, "R_36"),
-    ("stt", 6, 0, 2, "R_36"),
-    ("stt", 6, 0, 3, "R_36"),
-    ("stt", 6, 1, 0, "R_37"),
-    ("stt", 6, 1, 1, "R_37"),
-    ("stt", 6, 1, 2, "R_37"),
-    ("stt", 6, 1, 3, "R_37"),
-    ("rg", "V", 5, 0),
-    ("rg", "V", 5, 1),
+    ("R", 5, 0, "R5_0"),
+    ("stage", "sp1_3", 256, "sp"),
+    ("evm", "S", "b1_3", "sp1_3", 0),
+    ("R", 5, 1, "R5_1"),
+    ("storeu", "sp0_3", 0, 3, 1, 0),
+    ("TT", 5, 0, "R5_0"),
+    ("mxu", 4, 0, "a4_0"),
+    ("stage", "sp2_3", 256, "sp"),
+    ("evm", "S", "b2_3", "sp2_3", 0),
+    ("storeu", "sp1_3", 1, 3, 1, 0),
+    ("mxu", 4, 1, "a4_1"),
+    ("stage", "H4", 1280, "hv"),
+    ("evu", "S", "a4_0", "H4", 0),
+    ("storeu", "sp2_3", 2, 3, 1, 0),
+    ("TT", 5, 1, "R5_1"),
+    ("mxu", 4, 2, "a4_2"),
+    ("evu", "S", "a4_1", "H4", 256),
+    ("mxu", 4, 3, "a4_3"),
+    ("evu", "S", "a4_2", "H4", 512),
     ("Q", 5, 0),
+    ("mxu", 4, 4, "a4_4"),
     ("Q", 5, 1),
-    ("stage", "H4", 2560, "hv"),
-    ("mxu", 4, 0, "acc_50"),
-    ("evu", "S", "acc_50", "H4", 0),
-    ("mxu", 4, 1, "acc_51"),
-    ("evu", "S", "acc_51", "H4", 256),
-    ("mxu", 4, 2, "acc_52"),
-    ("evu", "S", "acc_52", "H4", 512),
-    ("mxu", 4, 3, "acc_53"),
-    ("evu", "S", "acc_53", "H4", 768),
+    ("evu", "S", "a4_3", "H4", 768),
+    ("miru", 0, 4, "b0_4"),
+    ("evu", "S", "a4_4", "H4", 1024),
+    ("miru", 1, 4, "b1_4"),
     ("storeu", "H4", 4, 0, 4, 0),
-    ("mxu", 4, 4, "acc_54"),
-    ("evu", "S", "acc_54", "H4", 1024),
+    ("miru", 2, 4, "b2_4"),
+    ("stage", "sp0_4", 256, "sp"),
+    ("evm", "S", "b0_4", "sp0_4", 0),
     ("storeu", "H4", 4, 4, 1, 1024),
-    ("mxu", 0, 4, "acc_55"),
-    ("stage", "sp_56", 512, "sp"),
-    ("evu", "S", "acc_55", "sp_56", 0),
-    ("storeu", "sp_56", 0, 4, 1, 0),
-    ("mxu", 1, 4, "acc_57"),
-    ("stage", "sp_58", 512, "sp"),
-    ("evu", "S", "acc_57", "sp_58", 0),
-    ("storeu", "sp_58", 1, 4, 1, 0),
-    ("mxu", 2, 4, "acc_59"),
-    ("stage", "sp_60", 512, "sp"),
-    ("evu", "V", "acc_59", "sp_60", 0),
-    ("storeu", "sp_60", 2, 4, 1, 0),
-    ("mxu", 3, 4, "acc_61"),
-    ("stage", "sp_62", 512, "sp"),
-    ("evu", "V", "acc_61", "sp_62", 0),
-    ("storeu", "sp_62", 3, 4, 1, 0),
-    ("stt", 7, 0, 0, "R_48"),
-    ("stt", 7, 0, 1, "R_48"),
-    ("stt", 7, 0, 2, "R_48"),
-    ("stt", 7, 0, 3, "R_48"),
-    ("stt", 7, 1, 0, "R_49"),
-    ("stt", 7, 1, 1, "R_49"),
-    ("stt", 7, 1, 2, "R_49"),
-    ("stt", 7, 1, 3, "R_49"),
-    ("rg", "V", 6, 0),
-    ("rg", "V", 6, 1),
+    ("miru", 3, 4, "b3_4"),
+    ("stage", "sp1_4", 256, "sp"),
+    ("evm", "S", "b1_4", "sp1_4", 0),
+    ("R", 6, 0, "R6_0"),
+    ("storeu", "sp0_4", 0, 4, 1, 0),
+    ("R", 6, 1, "R6_1"),
+    ("stage", "sp2_4", 256, "sp"),
+    ("evm", "S", "b2_4", "sp2_4", 0),
+    ("TT", 6, 0, "R6_0"),
+    ("mxu", 5, 0, "a5_0"),
+    ("storeu", "sp1_4", 1, 4, 1, 0),
+    ("stage", "sp3_4", 256, "sp"),
+    ("evm", "S", "b3_4", "sp3_4", 0),
+    ("storeu", "sp2_4", 2, 4, 1, 0),
+    ("TT", 6, 1, "R6_1"),
+    ("storeu", "sp3_4", 3, 4, 1, 0),
+    ("mxu", 5, 1, "a5_1"),
+    ("stage", "H5", 1536, "hv"),
+    ("evu", "S", "a5_0", "H5", 0),
     ("Q", 6, 0),
+    ("mxu", 5, 2, "a5_2"),
     ("Q", 6, 1),
-    ("stage", "H5", 3072, "hv"),
-    ("mxu", 5, 0, "acc_63"),
-    ("evu", "S", "acc_63", "H5", 0),
-    ("mxu", 5, 1, "acc_64"),
-    ("evu", "S", "acc_64", "H5", 256),
-    ("mxu", 5, 2, "acc_65"),
-    ("evu", "S", "acc_65", "H5", 512),
-    ("mxu", 5, 3, "acc_66"),
-    ("evu", "S", "acc_66", "H5", 768),
+    ("evu", "S", "a5_1", "H5", 256),
+    ("mxu", 5, 3, "a5_3"),
+    ("evu", "S", "a5_2", "H5", 512),
+    ("mxu", 5, 4, "a5_4"),
+    ("evu", "S", "a5_3", "H5", 768),
+    ("mxu", 5, 5, "a5_5"),
+    ("evu", "S", "a5_4", "H5", 1024),
     ("storeu", "H5", 5, 0, 4, 0),
-    ("mxu", 5, 4, "acc_67"),
-    ("evu", "S", "acc_67", "H5", 1024),
-    ("mxu", 5, 5, "acc_68"),
-    ("evu", "S", "acc_68", "H5", 1280),
+    ("miru", 0, 5, "b0_5"),
+    ("evu", "S", "a5_5", "H5", 1280),
+    ("miru", 1, 5, "b1_5"),
+    ("stage", "sp0_5", 256, "sp"),
+    ("evm", "V", "b0_5", "sp0_5", 0),
+    ("miru", 2, 5, "b2_5"),
+    ("stage", "sp1_5", 256, "sp"),
+    ("evm", "S", "b1_5", "sp1_5", 0),
     ("storeu", "H5", 5, 4, 2, 1024),
-    ("mxu", 0, 5, "acc_69"),
-    ("stage", "sp_70", 512, "sp"),
-    ("evu", "S", "acc_69", "sp_70", 0),
-    ("storeu", "sp_70", 0, 5, 1, 0),
-    ("mxu", 1, 5, "acc_71"),
-    ("stage", "sp_72", 512, "sp"),
-    ("evu", "V", "acc_71", "sp_72", 0),
-    ("storeu", "sp_72", 1, 5, 1, 0),
-    ("mxu", 2, 5, "acc_73"),
-    ("stage", "sp_74", 512, "sp"),
-    ("evu", "V", "acc_73", "sp_74", 0),
-    ("storeu", "sp_74", 2, 5, 1, 0),
-    ("mxu", 3, 5, "acc_75"),
-    ("stage", "sp_76", 512, "sp"),
-    ("evu", "V", "acc_75", "sp_76", 0),
-    ("storeu", "sp_76", 3, 5, 1, 0),
-    ("mxu", 4, 5, "acc_77"),
-    ("stage", "sp_78", 512, "sp"),
-    ("evu", "V", "acc_77", "sp_78", 0),
-    ("storeu", "sp_78", 4, 5, 1, 0),
-    ("rg", "V", 7, 0),
-    ("rg", "V", 7, 1),
+    ("miru", 3, 5, "b3_5"),
+    ("stage", "sp2_5", 256, "sp"),
+    ("evm", "V", "b2_5", "sp2_5", 0),
+    ("R", 7, 0, "R7_0"),
+    ("storeu", "sp0_5", 0, 5, 1, 0),
+    ("stage", "sp3_5", 256, "sp"),
+    ("evm", "S", "b3_5", "sp3_5", 0),
+    ("miru", 4, 5, "b4_5"),
+    ("storeu", "sp1_5", 1, 5, 1, 0),
+    ("TT", 7, 0, "R7_0"),
+    ("storeu", "sp2_5", 2, 5, 1, 0),
+    ("R", 7, 1, "R7_1"),
+    ("storeu", "sp3_5", 3, 5, 1, 0),
+    ("stage", "sp4_5", 256, "sp"),
+    ("evm", "S", "b4_5", "sp4_5", 0),
+    ("mxu", 6, 0, "a6_0"),
+    ("TT", 7, 1, "R7_1"),
+    ("storeu", "sp4_5", 4, 5, 1, 0),
+    ("mxu", 6, 1, "a6_1"),
     ("Q", 7, 0),
+    ("stage", "H6", 1792, "hv"),
+    ("evu", "S", "a6_0", "H6", 0),
     ("Q", 7, 1),
-    ("stage", "H6", 3584, "hv"),
-    ("mxu", 6, 0, "acc_79"),
-    ("evu", "S", "acc_79", "H6", 0),
-    ("mxu", 6, 1, "acc_80"),
-    ("evu", "S", "acc_80", "H6", 256),
-    ("mxu", 6, 2, "acc_81"),
-    ("evu", "S", "acc_81", "H6", 512),
-    ("mxu", 6, 3, "acc_82"),
-    ("evu", "S", "acc_82", "H6", 768),
+    ("mxu", 6, 2, "a6_2"),
+    ("evu", "S", "a6_1", "H6", 256),
+    ("mxu", 6, 3, "a6_3"),
+    ("evu", "S", "a6_2", "H6", 512),
+    ("mxu", 6, 4, "a6_4"),
+    ("evu", "S", "a6_3", "H6", 768),
+    ("mxu", 6, 5, "a6_5"),
+    ("evu", "S", "a6_4", "H6", 1024),
     ("storeu", "H6", 6, 0, 4, 0),
-    ("mxu", 6, 4, "acc_83"),
-    ("evu", "S", "acc_83", "H6", 1024),
-    ("mxu", 6, 5, "acc_84"),
-    ("evu", "S", "acc_84", "H6", 1280),
-    ("mxu", 6, 6, "acc_85"),
-    ("evu", "S", "acc_85", "H6", 1536),
+    ("mxu", 6, 6, "a6_6"),
+    ("evu", "S", "a6_5", "H6", 1280),
+    ("miru", 0, 6, "b0_6"),
+    ("evu", "S", "a6_6", "H6", 1536),
+    ("miru", 1, 6, "b1_6"),
+    ("stage", "sp0_6", 256, "sp"),
+    ("evm", "V", "b0_6", "sp0_6", 0),
+    ("miru", 2, 6, "b2_6"),
+    ("stage", "sp1_6", 256, "sp"),
+    ("evm", "S", "b1_6", "sp1_6", 0),
     ("storeu", "H6", 6, 4, 3, 1024),
-    ("mxu", 0, 6, "acc_86"),
-    ("stage", "sp_87", 512, "sp"),
-    ("evu", "V", "acc_86", "sp_87", 0),
-    ("storeu", "sp_87", 0, 6, 1, 0),
-    ("mxu", 1, 6, "acc_88"),
-    ("stage", "sp_89", 512, "sp"),
-    ("evu", "V", "acc_88", "sp_89", 0),
-    ("storeu", "sp_89", 1, 6, 1, 0),
-    ("mxu", 2, 6, "acc_90"),
-    ("stage", "sp_91", 512, "sp"),
-    ("evu", "V", "acc_90", "sp_91", 0),
-    ("storeu", "sp_91", 2, 6, 1, 0),
-    ("mxu", 3, 6, "acc_92"),
-    ("stage", "sp_93", 512, "sp"),
-    ("evu", "V", "acc_92", "sp_93", 0),
-    ("storeu", "sp_93", 3, 6, 1, 0),
-    ("mxu", 4, 6, "acc_94"),
-    ("stage", "sp_95", 512, "sp"),
-    ("evu", "V", "acc_94", "sp_95", 0),
-    ("storeu", "sp_95", 4, 6, 1, 0),
-    ("mxu", 5, 6, "acc_96"),
-    ("stage", "sp_97", 512, "sp"),
-    ("evu", "V", "acc_96", "sp_97", 0),
-    ("storeu", "sp_97", 5, 6, 1, 0),
-    ("stage", "H7", 4096, "hv"),
-    ("mxu", 7, 0, "acc_98"),
-    ("evu", "S", "acc_98", "H7", 0),
-    ("mxu", 7, 1, "acc_99"),
-    ("evu", "S", "acc_99", "H7", 256),
-    ("mxu", 7, 2, "acc_100"),
-    ("evu", "S", "acc_100", "H7", 512),
-    ("mxu", 7, 3, "acc_101"),
-    ("evu", "S", "acc_101", "H7", 768),
+    ("miru", 3, 6, "b3_6"),
+    ("stage", "sp2_6", 256, "sp"),
+    ("evm", "V", "b2_6", "sp2_6", 0),
+    ("storeu", "sp0_6", 0, 6, 1, 0),
+    ("miru", 4, 6, "b4_6"),
+    ("stage", "sp3_6", 256, "sp"),
+    ("evm", "S", "b3_6", "sp3_6", 0),
+    ("storeu", "sp1_6", 1, 6, 1, 0),
+    ("miru", 5, 6, "b5_6"),
+    ("stage", "sp4_6", 256, "sp"),
+    ("evm", "V", "b4_6", "sp4_6", 0),
+    ("storeu", "sp2_6", 2, 6, 1, 0),
+    ("mxu", 7, 0, "a7_0"),
+    ("stage", "sp5_6", 256, "sp"),
+    ("evm", "S", "b5_6", "sp5_6", 0),
+    ("storeu", "sp3_6", 3, 6, 1, 0),
+    ("mxu", 7, 1, "a7_1"),
+    ("storeu", "sp4_6", 4, 6, 1, 0),
+    ("stage", "H7", 2048, "hv"),
+    ("evu", "S", "a7_0", "H7", 0),
+    ("storeu", "sp5_6", 5, 6, 1, 0),
+    ("mxu", 7, 2, "a7_2"),
+    ("evu", "S", "a7_1", "H7", 256),
+    ("mxu", 7, 3, "a7_3"),
+    ("evu", "S", "a7_2", "H7", 512),
+    ("mxu", 7, 4, "a7_4"),
+    ("evu", "S", "a7_3", "H7", 768),
+    ("mxu", 7, 5, "a7_5"),
+    ("evu", "S", "a7_4", "H7", 1024),
     ("storeu", "H7", 7, 0, 4, 0),
-    ("mxu", 7, 4, "acc_102"),
-    ("evu", "S", "acc_102", "H7", 1024),
-    ("mxu", 7, 5, "acc_103"),
-    ("evu", "S", "acc_103", "H7", 1280),
-    ("mxu", 7, 6, "acc_104"),
-    ("evu", "S", "acc_104", "H7", 1536),
-    ("mxu", 7, 7, "acc_105"),
-    ("evu", "S", "acc_105", "H7", 1792),
+    ("mxu", 7, 6, "a7_6"),
+    ("evu", "S", "a7_5", "H7", 1280),
+    ("mxu", 7, 7, "a7_7"),
+    ("evu", "S", "a7_6", "H7", 1536),
+    ("miru", 0, 7, "b0_7"),
+    ("evu", "S", "a7_7", "H7", 1792),
+    ("miru", 1, 7, "b1_7"),
+    ("stage", "sp0_7", 256, "sp"),
+    ("evm", "V", "b0_7", "sp0_7", 0),
+    ("miru", 2, 7, "b2_7"),
+    ("stage", "sp1_7", 256, "sp"),
+    ("evm", "S", "b1_7", "sp1_7", 0),
     ("storeu", "H7", 7, 4, 4, 1024),
-    ("mxu", 0, 7, "acc_106"),
-    ("stage", "sp_107", 512, "sp"),
-    ("evu", "V", "acc_106", "sp_107", 0),
-    ("storeu", "sp_107", 0, 7, 1, 0),
-    ("mxu", 1, 7, "acc_108"),
-    ("stage", "sp_109", 512, "sp"),
-    ("evu", "V", "acc_108", "sp_109", 0),
-    ("storeu", "sp_109", 1, 7, 1, 0),
-    ("mxu", 2, 7, "acc_110"),
-    ("stage", "sp_111", 512, "sp"),
-    ("evu", "V", "acc_110", "sp_111", 0),
-    ("storeu", "sp_111", 2, 7, 1, 0),
-    ("mxu", 3, 7, "acc_112"),
-    ("stage", "sp_113", 512, "sp"),
-    ("evu", "V", "acc_112", "sp_113", 0),
-    ("storeu", "sp_113", 3, 7, 1, 0),
-    ("mxu", 4, 7, "acc_114"),
-    ("stage", "sp_115", 512, "sp"),
-    ("evu", "V", "acc_114", "sp_115", 0),
-    ("storeu", "sp_115", 4, 7, 1, 0),
-    ("mxu", 5, 7, "acc_116"),
-    ("stage", "sp_117", 512, "sp"),
-    ("evu", "V", "acc_116", "sp_117", 0),
-    ("storeu", "sp_117", 5, 7, 1, 0),
-    ("mxu", 6, 7, "acc_118"),
-    ("stage", "sp_119", 512, "sp"),
-    ("evu", "V", "acc_118", "sp_119", 0),
-    ("storeu", "sp_119", 6, 7, 1, 0),
+    ("miru", 3, 7, "b3_7"),
+    ("stage", "sp2_7", 256, "sp"),
+    ("evm", "V", "b2_7", "sp2_7", 0),
+    ("storeu", "sp0_7", 0, 7, 1, 0),
+    ("miru", 4, 7, "b4_7"),
+    ("stage", "sp3_7", 256, "sp"),
+    ("evm", "S", "b3_7", "sp3_7", 0),
+    ("storeu", "sp1_7", 1, 7, 1, 0),
+    ("miru", 5, 7, "b5_7"),
+    ("stage", "sp4_7", 256, "sp"),
+    ("evm", "V", "b4_7", "sp4_7", 0),
+    ("storeu", "sp2_7", 2, 7, 1, 0),
+    ("miru", 6, 7, "b6_7"),
+    ("stage", "sp5_7", 256, "sp"),
+    ("evm", "S", "b5_7", "sp5_7", 0),
+    ("storeu", "sp3_7", 3, 7, 1, 0),
+    ("storeu", "sp4_7", 4, 7, 1, 0),
+    ("stage", "sp6_7", 256, "sp"),
+    ("evm", "S", "b6_7", "sp6_7", 0),
+    ("storeu", "sp5_7", 5, 7, 1, 0),
+    ("storeu", "sp6_7", 6, 7, 1, 0),
 ]
 
 
@@ -378,12 +347,11 @@ def tile_attentive_kernel(tc, x, attn_vectors, out):
     with ExitStack() as ctx:
         ctx.enter_context(tc.manual_schedule())
         keep = ctx.enter_context(tc.tile_pool(name="keep", bufs=1))
-        small = ctx.enter_context(tc.tile_pool(name="small", bufs=4))
-        ypool = ctx.enter_context(tc.tile_pool(name="yp", bufs=3))
+        small = ctx.enter_context(tc.tile_pool(name="small", bufs=5))
         gpool = ctx.enter_context(tc.tile_pool(name="gp", bufs=3))
         pools = {
             "hv": ctx.enter_context(tc.tile_pool(name="hv", bufs=3)),
-            "sp": ctx.enter_context(tc.tile_pool(name="sp", bufs=8)),
+            "sp": ctx.enter_context(tc.tile_pool(name="sp", bufs=12)),
             "fr": ctx.enter_context(tc.psum_pool(name="fr", bufs=4)),
             "acc": ctx.enter_context(tc.psum_pool(name="acc", bufs=4)),
         }
@@ -392,11 +360,13 @@ def tile_attentive_kernel(tc, x, attn_vectors, out):
         nc.vector.memset(a0[:], 0.0)
         nc.scalar.dma_start(out=a0[0:H, :], in_=attn_vectors)
         x_sb = keep.tile([P, NT * D], BF16)
-        for g in range(NCH):
+        for t0, nt in UNITS:
             nc.sync.dma_start(
-                out=x_sb[:, g * 4 * D:(g + 1) * 4 * D].rearrange("p (t d) -> p t d", d=D),
-                in_=x[g * CH:(g + 1) * CH, :].rearrange("(t p) d -> p t d", p=P),
+                out=x_sb[:, t0 * D:(t0 + nt) * D].rearrange("p (t d) -> p t d", d=D),
+                in_=x[t0 * P:(t0 + nt) * P, :].rearrange("(t p) d -> p t d", p=P),
             )
+        dmz = keep.tile([P, CH], BF16)
+        nc.vector.memset(dmz[:], 0.0)
         warm = keep.tile([P, 1], F32)
         nc.vector.memset(warm[:], 1.0)
         warm2 = keep.tile([P, 1], F32)
@@ -409,44 +379,54 @@ def tile_attentive_kernel(tc, x, attn_vectors, out):
         aT_f = keep.tile([P, 2 * H], F32)
         a2T = keep.tile([P, 2, H], F32)
         r_sb = keep.tile([P, NT * H], F32)
+        xa = keep.tile([P, 2, 4, N], F32)
         codes = keep.tile([P, 2, N], U32, align_bytes=64)
         scl = keep.tile([P, 2, N], U8, align_bytes=64)
 
         xw = x_sb[:].bitcast(F32)
         xT_b = xT_w[:].bitcast(BF16).rearrange("p (n e) -> p n e", e=2)
 
-        aT_ps = pools["fr"].tile([P, P], F32, tag="fr")
-        nc.tensor.transpose(aT_ps[:], a0[:].bitcast(F32), ident_f[:])
-        nc.vector.tensor_copy(out=aT_f[:], in_=aT_ps[:].bitcast(BF16)[:, 0:2 * H])
-        nc.scalar.activation(out=a2T[:], in_=aT_f[:].rearrange("p (h e) -> p e h", e=2), func=ACT.Square)
-
         tiles = {}
 
         for call in PROGRAM:
             op = call[0]
-            if op == "xt":
-                g, key, pool = call[1], call[2], call[3]
-                tl = pools[pool].tile([P, CH], F32, tag=pool)
+            if op == "dm":
+                tl = pools["acc"].tile([P, CH], F32, tag="acc")
+                nc.tensor.matmul(out=tl[:], lhsT=dmz[:, 0:P], rhs=dmz[:], start=True, stop=True)
+            elif op == "aT":
+                tl = pools["fr"].tile([P, P], F32, tag="fr")
+                tiles["aT"] = tl
+                nc.tensor.transpose(tl[:], a0[:].bitcast(F32), ident_f[:])
+            elif op == "aTf":
+                nc.vector.tensor_copy(out=aT_f[:], in_=tiles["aT"][:].bitcast(BF16)[:, 0:2 * H])
+            elif op == "a2T":
+                nc.scalar.activation(out=a2T[:], in_=aT_f[:].rearrange("p (h e) -> p e h", e=2), func=ACT.Square)
+            elif op == "xt":
+                t0, nt, key = call[1], call[2], call[3]
+                tl = pools["acc"].tile([P, nt * P], F32, tag="acc")
                 tiles[key] = tl
-                for j in range(4):
-                    t = 4 * g + j
+                for j in range(nt):
+                    t = t0 + j
                     nc.tensor.transpose(tl[:, j * P:(j + 1) * P], xw[:, t * P:(t + 1) * P], ident_f[:])
             elif op == "sqp":
-                g, key = call[1], call[2]
+                t0, nt, key = call[1], call[2], call[3]
                 nc.scalar.activation(
-                    out=x2T[:, :, g * CH:(g + 1) * CH],
+                    out=x2T[:, :, t0 * P:(t0 + nt) * P],
                     in_=tiles[key][:].bitcast(BF16).rearrange("p (n e) -> p e n", e=2),
                     func=ACT.Square,
                 )
-            elif op == "cp":
-                g, key = call[1], call[2]
-                nc.vector.tensor_copy(out=xT_w[:, g * CH:(g + 1) * CH], in_=tiles[key][:])
+            elif op == "cpx":
+                eng, t0, nt, key = call[1], call[2], call[3], call[4]
+                if eng == "V":
+                    nc.vector.tensor_copy(out=xT_w[:, t0 * P:(t0 + nt) * P], in_=tiles[key][:])
+                else:
+                    nc.scalar.copy(out=xT_w[:, t0 * P:(t0 + nt) * P], in_=tiles[key][:])
             elif op == "smm":
-                g, key = call[1], call[2]
-                tl = pools["acc"].tile([P, 4 * H], F32, tag="acc")
+                t0, nt, key = call[1], call[2], call[3]
+                tl = pools["acc"].tile([P, nt * H], F32, tag="acc")
                 tiles[key] = tl
-                for j in range(4):
-                    t = 4 * g + j
+                for j in range(nt):
+                    t = t0 + j
                     for e in range(2):
                         nc.tensor.matmul(
                             out=tl[:, j * H:(j + 1) * H],
@@ -456,18 +436,31 @@ def tile_attentive_kernel(tc, x, attn_vectors, out):
                             stop=(e == 1),
                         )
             elif op == "max":
-                g, key = call[1], call[2]
-                sm = small.tile([P, 4 * H], F32, tag="sm")
-                tiles["sm%d" % g] = sm
+                i, t0, nt, key = call[1], call[2], call[3], call[4]
+                sm = small.tile([P, nt * H], F32, tag="sm")
+                tiles["sm%d" % i] = sm
                 nc.vector.tensor_scalar_max(out=sm[:], in0=tiles[key][:], scalar1=EPS)
             elif op == "sqrt":
-                g = call[1]
-                sq = small.tile([P, 4 * H], F32, tag="sq")
-                tiles["sq%d" % g] = sq
-                nc.scalar.activation(out=sq[:], in_=tiles["sm%d" % g][:], func=ACT.Sqrt)
+                i, nt = call[1], call[2]
+                sq = small.tile([P, nt * H], F32, tag="sq")
+                tiles["sq%d" % i] = sq
+                nc.scalar.activation(out=sq[:], in_=tiles["sm%d" % i][:], func=ACT.Sqrt)
             elif op == "rec":
-                g = call[1]
-                nc.vector.reciprocal(out=r_sb[:, g * 4 * H:(g + 1) * 4 * H], in_=tiles["sq%d" % g][:])
+                i, t0, nt = call[1], call[2], call[3]
+                nc.vector.reciprocal(out=r_sb[:, t0 * H:(t0 + nt) * H], in_=tiles["sq%d" % i][:])
+            elif op == "xa4":
+                eng, t0, nt, c = call[1], call[2], call[3], call[4]
+                for t in range(4):
+                    h, e = 2 * c + t // 2, t % 2
+                    dst = xa[:, c, t, t0 * P:(t0 + nt) * P]
+                    src = xT_b[:, t0 * P:(t0 + nt) * P, e]
+                    sca = aT_f[:, 2 * h + e:2 * h + e + 1]
+                    if eng == "V":
+                        nc.vector.tensor_scalar_mul(out=dst, in0=src, scalar1=sca)
+                    elif eng == "S":
+                        nc.scalar.activation(out=dst, in_=src, func=ACT.Copy, scale=sca)
+                    else:
+                        nc.gpsimd.tensor_scalar(out=dst, in0=src, scalar1=sca, scalar2=0.0, op0=ALU.mult, op1=ALU.add)
             elif op == "R":
                 u, c, key = call[1], call[2], call[3]
                 tl = pools["fr"].tile([P, 2, PR], F32, tag="fr")
@@ -480,31 +473,18 @@ def tile_attentive_kernel(tc, x, attn_vectors, out):
                             r_sb[:, col:col + 1].to_broadcast([P, P]),
                             ident_f[:],
                         )
-            elif op == "stt":
-                u, c, t, key = call[1], call[2], call[3], call[4]
-                if c == 0 and t == 0:
-                    yp = ypool.tile([P, 2, 4, PR], BF16, tag="yp")
-                    tiles["yp%d" % u] = yp
-                h, e = 2 * c + t // 2, t % 2
-                nc.vector.scalar_tensor_tensor(
-                    out=tiles["yp%d" % u][:, c, t, :],
-                    in0=xT_b[:, u * PR:(u + 1) * PR, e],
-                    scalar=aT_f[:, 2 * h + e:2 * h + e + 1],
-                    in1=tiles[key][:, t // 2, :],
-                    op0=ALU.mult,
-                    op1=ALU.mult,
-                )
-            elif op == "rg":
-                eng, u, c = call[1], call[2], call[3]
+            elif op == "TT":
+                u, c, key = call[1], call[2], call[3]
                 if ("gp%d" % u) not in tiles:
                     gp = gpool.tile([P, 2, PR, 4], BF16, tag="gp", align_bytes=64)
                     tiles["gp%d" % u] = gp
-                dst = tiles["gp%d" % u][:, c, :, :].rearrange("p (m i) t -> p m t i", i=4)
-                src = tiles["yp%d" % u][:, c, :, :].rearrange("p t (m i) -> p m t i", i=4)
-                if eng == "V":
-                    nc.vector.tensor_copy(out=dst, in_=src)
-                else:
-                    nc.scalar.copy(out=dst, in_=src)
+                n0 = u * PR
+                nc.vector.tensor_tensor(
+                    out=tiles["gp%d" % u][:, c, :, :].rearrange("p n (h e) -> p n h e", e=2),
+                    in0=xa[:, c, :, n0:n0 + PR].rearrange("p (h e) n -> p n h e", e=2),
+                    in1=tiles[key][:].rearrange("p h n -> p n h").unsqueeze(3).to_broadcast([P, PR, 2, 2]),
+                    op=ALU.mult,
+                )
             elif op == "Q":
                 u, c = call[1], call[2]
                 n0 = u * PR
@@ -515,7 +495,7 @@ def tile_attentive_kernel(tc, x, attn_vectors, out):
                 )
             elif op == "stage":
                 key, width, tag = call[1], call[2], call[3]
-                tl = pools[tag].tile([P, 2, width // 2], F32, tag=tag)
+                tl = pools[tag].tile([P, 2, width], F32, tag=tag)
                 tiles[key] = tl
             elif op == "mxu":
                 v, w, key = call[1], call[2], call[3]

@@ -14,332 +14,14 @@ ALU = mybir.AluOpType
 N, D, H = 2048, 256, 4
 K = H * D
 P = 128
-NT = N // P
-CH = 512
-PR = 256
+TILES = N // P
+PAIR = 2 * P
+PAIRS = N // PAIR
 EPS = 1e-12
 FLOPS = 2 * N * N * K
-UNITS = ((0, 2), (2, 2), (4, 4), (8, 4), (12, 4))
-
-PROGRAM = [
-    ("dm", "dm0"),
-    ("dm", "dm1"),
-    ("dm", "dm2"),
-    ("dm", "dm3"),
-    ("dm", "dm4"),
-    ("dm", "dm5"),
-    ("dm", "dm6"),
-    ("dm", "dm7"),
-    ("dm", "dm8"),
-    ("dm", "dm9"),
-    ("dm", "dm10"),
-    ("aT",),
-    ("xt", 0, 2, "xt0"),
-    ("dm", "dm11"),
-    ("aTf",),
-    ("sqp", 0, 2, "xt0"),
-    ("xt", 2, 2, "xt1"),
-    ("dm", "dm12"),
-    ("dm", "dm13"),
-    ("a2T",),
-    ("cpx", "S", 0, 2, "xt0"),
-    ("dm", "dm14"),
-    ("sqp", 2, 2, "xt1"),
-    ("smm", 0, 2, "s0"),
-    ("xa4", "V", 0, 2, 0),
-    ("xt", 4, 4, "xt2"),
-    ("cpx", "S", 2, 2, "xt1"),
-    ("smm", 2, 2, "s1"),
-    ("xa4", "S", 2, 2, 0),
-    ("max", 0, 0, 2, "s0"),
-    ("xa4", "V", 0, 2, 1),
-    ("dm", "dm15"),
-    ("dm", "dm16"),
-    ("xt", 8, 4, "xt3"),
-    ("max", 1, 2, 2, "s1"),
-    ("sqrt", 0, 2),
-    ("xa4", "V", 2, 2, 1),
-    ("sqp", 4, 4, "xt2"),
-    ("xt", 12, 4, "xt4"),
-    ("rec", 0, 0, 2),
-    ("R", 0, 0, "R0_0"),
-    ("sqrt", 1, 2),
-    ("cpx", "S", 4, 4, "xt2"),
-    ("smm", 4, 4, "s2"),
-    ("rec", 1, 2, 2),
-    ("TT", 0, 0, "R0_0"),
-    ("xa4", "S", 4, 4, 0),
-    ("R", 0, 1, "R0_1"),
-    ("max", 2, 4, 4, "s2"),
-    ("R", 1, 0, "R1_0"),
-    ("TT", 0, 1, "R0_1"),
-    ("R", 1, 1, "R1_1"),
-    ("sqrt", 2, 4),
-    ("Q", 0, 0),
-    ("sqp", 8, 4, "xt3"),
-    ("rec", 2, 4, 4),
-    ("Q", 0, 1),
-    ("R", 2, 0, "R2_0"),
-    ("TT", 1, 0, "R1_0"),
-    ("xa4", "S", 4, 4, 1),
-    ("mxu", 0, 0, "a0_0"),
-    ("cpx", "V", 8, 4, "xt3"),
-    ("TT", 1, 1, "R1_1"),
-    ("smm", 8, 4, "s3"),
-    ("xa4", "G", 8, 4, 0),
-    ("stage", "H0", 256, "hv"),
-    ("evu", "S", "a0_0", "H0", 0),
-    ("Q", 1, 0),
-    ("R", 2, 1, "R2_1"),
-    ("Q", 1, 1),
-    ("sqp", 12, 4, "xt4"),
-    ("R", 3, 0, "R3_0"),
-    ("max", 3, 8, 4, "s3"),
-    ("TT", 2, 0, "R2_0"),
-    ("storeu", "H0", 0, 0, 1, 0),
-    ("mxu", 1, 0, "a1_0"),
-    ("sqrt", 3, 4),
-    ("mxu", 1, 1, "a1_1"),
-    ("cpx", "S", 12, 4, "xt4"),
-    ("TT", 2, 1, "R2_1"),
-    ("R", 3, 1, "R3_1"),
-    ("xa4", "G", 8, 4, 1),
-    ("stage", "H1", 512, "hv"),
-    ("evu", "S", "a1_0", "H1", 0),
-    ("smm", 12, 4, "s4"),
-    ("evu", "S", "a1_1", "H1", 256),
-    ("rec", 3, 8, 4),
-    ("Q", 2, 0),
-    ("Q", 2, 1),
-    ("storeu", "H1", 1, 0, 2, 0),
-    ("TT", 3, 0, "R3_0"),
-    ("miru", 0, 1, "b0_1"),
-    ("mxu", 2, 0, "a2_0"),
-    ("stage", "sp0_1", 256, "sp"),
-    ("evm", "S", "b0_1", "sp0_1", 0),
-    ("mxu", 2, 1, "a2_1"),
-    ("max", 4, 12, 4, "s4"),
-    ("TT", 3, 1, "R3_1"),
-    ("stage", "H2", 768, "hv"),
-    ("evu", "S", "a2_0", "H2", 0),
-    ("storeu", "sp0_1", 0, 1, 1, 0),
-    ("mxu", 2, 2, "a2_2"),
-    ("xa4", "G", 12, 4, 0),
-    ("evu", "S", "a2_1", "H2", 256),
-    ("miru", 0, 2, "b0_2"),
-    ("evu", "S", "a2_2", "H2", 512),
-    ("Q", 3, 0),
-    ("miru", 1, 2, "b1_2"),
-    ("Q", 3, 1),
-    ("stage", "sp0_2", 256, "sp"),
-    ("evm", "S", "b0_2", "sp0_2", 0),
-    ("R", 4, 0, "R4_0"),
-    ("storeu", "H2", 2, 0, 3, 0),
-    ("R", 4, 1, "R4_1"),
-    ("stage", "sp1_2", 256, "sp"),
-    ("evm", "S", "b1_2", "sp1_2", 0),
-    ("TT", 4, 0, "R4_0"),
-    ("mxu", 3, 0, "a3_0"),
-    ("storeu", "sp0_2", 0, 2, 1, 0),
-    ("sqrt", 4, 4),
-    ("mxu", 3, 1, "a3_1"),
-    ("storeu", "sp1_2", 1, 2, 1, 0),
-    ("stage", "H3", 1024, "hv"),
-    ("evu", "S", "a3_0", "H3", 0),
-    ("rec", 4, 12, 4),
-    ("xa4", "G", 12, 4, 1),
-    ("TT", 4, 1, "R4_1"),
-    ("mxu", 3, 2, "a3_2"),
-    ("evu", "S", "a3_1", "H3", 256),
-    ("mxu", 3, 3, "a3_3"),
-    ("evu", "S", "a3_2", "H3", 512),
-    ("Q", 4, 0),
-    ("miru", 0, 3, "b0_3"),
-    ("evu", "S", "a3_3", "H3", 768),
-    ("Q", 4, 1),
-    ("miru", 1, 3, "b1_3"),
-    ("miru", 2, 3, "b2_3"),
-    ("stage", "sp0_3", 256, "sp"),
-    ("evm", "S", "b0_3", "sp0_3", 0),
-    ("storeu", "H3", 3, 0, 4, 0),
-    ("R", 5, 0, "R5_0"),
-    ("stage", "sp1_3", 256, "sp"),
-    ("evm", "S", "b1_3", "sp1_3", 0),
-    ("R", 5, 1, "R5_1"),
-    ("storeu", "sp0_3", 0, 3, 1, 0),
-    ("TT", 5, 0, "R5_0"),
-    ("mxu", 4, 0, "a4_0"),
-    ("stage", "sp2_3", 256, "sp"),
-    ("evm", "S", "b2_3", "sp2_3", 0),
-    ("storeu", "sp1_3", 1, 3, 1, 0),
-    ("mxu", 4, 1, "a4_1"),
-    ("stage", "H4", 1280, "hv"),
-    ("evu", "S", "a4_0", "H4", 0),
-    ("storeu", "sp2_3", 2, 3, 1, 0),
-    ("TT", 5, 1, "R5_1"),
-    ("mxu", 4, 2, "a4_2"),
-    ("evu", "S", "a4_1", "H4", 256),
-    ("mxu", 4, 3, "a4_3"),
-    ("evu", "S", "a4_2", "H4", 512),
-    ("Q", 5, 0),
-    ("mxu", 4, 4, "a4_4"),
-    ("Q", 5, 1),
-    ("evu", "S", "a4_3", "H4", 768),
-    ("miru", 0, 4, "b0_4"),
-    ("evu", "S", "a4_4", "H4", 1024),
-    ("miru", 1, 4, "b1_4"),
-    ("storeu", "H4", 4, 0, 4, 0),
-    ("miru", 2, 4, "b2_4"),
-    ("stage", "sp0_4", 256, "sp"),
-    ("evm", "S", "b0_4", "sp0_4", 0),
-    ("storeu", "H4", 4, 4, 1, 1024),
-    ("miru", 3, 4, "b3_4"),
-    ("stage", "sp1_4", 256, "sp"),
-    ("evm", "S", "b1_4", "sp1_4", 0),
-    ("R", 6, 0, "R6_0"),
-    ("storeu", "sp0_4", 0, 4, 1, 0),
-    ("R", 6, 1, "R6_1"),
-    ("stage", "sp2_4", 256, "sp"),
-    ("evm", "S", "b2_4", "sp2_4", 0),
-    ("TT", 6, 0, "R6_0"),
-    ("mxu", 5, 0, "a5_0"),
-    ("storeu", "sp1_4", 1, 4, 1, 0),
-    ("stage", "sp3_4", 256, "sp"),
-    ("evm", "S", "b3_4", "sp3_4", 0),
-    ("storeu", "sp2_4", 2, 4, 1, 0),
-    ("TT", 6, 1, "R6_1"),
-    ("storeu", "sp3_4", 3, 4, 1, 0),
-    ("mxu", 5, 1, "a5_1"),
-    ("stage", "H5", 1536, "hv"),
-    ("evu", "S", "a5_0", "H5", 0),
-    ("Q", 6, 0),
-    ("mxu", 5, 2, "a5_2"),
-    ("Q", 6, 1),
-    ("evu", "S", "a5_1", "H5", 256),
-    ("mxu", 5, 3, "a5_3"),
-    ("evu", "S", "a5_2", "H5", 512),
-    ("mxu", 5, 4, "a5_4"),
-    ("evu", "S", "a5_3", "H5", 768),
-    ("mxu", 5, 5, "a5_5"),
-    ("evu", "S", "a5_4", "H5", 1024),
-    ("storeu", "H5", 5, 0, 4, 0),
-    ("miru", 0, 5, "b0_5"),
-    ("evu", "S", "a5_5", "H5", 1280),
-    ("miru", 1, 5, "b1_5"),
-    ("stage", "sp0_5", 256, "sp"),
-    ("evm", "V", "b0_5", "sp0_5", 0),
-    ("miru", 2, 5, "b2_5"),
-    ("stage", "sp1_5", 256, "sp"),
-    ("evm", "S", "b1_5", "sp1_5", 0),
-    ("storeu", "H5", 5, 4, 2, 1024),
-    ("miru", 3, 5, "b3_5"),
-    ("stage", "sp2_5", 256, "sp"),
-    ("evm", "V", "b2_5", "sp2_5", 0),
-    ("R", 7, 0, "R7_0"),
-    ("storeu", "sp0_5", 0, 5, 1, 0),
-    ("stage", "sp3_5", 256, "sp"),
-    ("evm", "S", "b3_5", "sp3_5", 0),
-    ("miru", 4, 5, "b4_5"),
-    ("storeu", "sp1_5", 1, 5, 1, 0),
-    ("TT", 7, 0, "R7_0"),
-    ("storeu", "sp2_5", 2, 5, 1, 0),
-    ("R", 7, 1, "R7_1"),
-    ("storeu", "sp3_5", 3, 5, 1, 0),
-    ("stage", "sp4_5", 256, "sp"),
-    ("evm", "S", "b4_5", "sp4_5", 0),
-    ("mxu", 6, 0, "a6_0"),
-    ("TT", 7, 1, "R7_1"),
-    ("storeu", "sp4_5", 4, 5, 1, 0),
-    ("mxu", 6, 1, "a6_1"),
-    ("Q", 7, 0),
-    ("stage", "H6", 1792, "hv"),
-    ("evu", "S", "a6_0", "H6", 0),
-    ("Q", 7, 1),
-    ("mxu", 6, 2, "a6_2"),
-    ("evu", "S", "a6_1", "H6", 256),
-    ("mxu", 6, 3, "a6_3"),
-    ("evu", "S", "a6_2", "H6", 512),
-    ("mxu", 6, 4, "a6_4"),
-    ("evu", "S", "a6_3", "H6", 768),
-    ("mxu", 6, 5, "a6_5"),
-    ("evu", "S", "a6_4", "H6", 1024),
-    ("storeu", "H6", 6, 0, 4, 0),
-    ("mxu", 6, 6, "a6_6"),
-    ("evu", "S", "a6_5", "H6", 1280),
-    ("miru", 0, 6, "b0_6"),
-    ("evu", "S", "a6_6", "H6", 1536),
-    ("miru", 1, 6, "b1_6"),
-    ("stage", "sp0_6", 256, "sp"),
-    ("evm", "V", "b0_6", "sp0_6", 0),
-    ("miru", 2, 6, "b2_6"),
-    ("stage", "sp1_6", 256, "sp"),
-    ("evm", "S", "b1_6", "sp1_6", 0),
-    ("storeu", "H6", 6, 4, 3, 1024),
-    ("miru", 3, 6, "b3_6"),
-    ("stage", "sp2_6", 256, "sp"),
-    ("evm", "V", "b2_6", "sp2_6", 0),
-    ("storeu", "sp0_6", 0, 6, 1, 0),
-    ("miru", 4, 6, "b4_6"),
-    ("stage", "sp3_6", 256, "sp"),
-    ("evm", "S", "b3_6", "sp3_6", 0),
-    ("storeu", "sp1_6", 1, 6, 1, 0),
-    ("miru", 5, 6, "b5_6"),
-    ("stage", "sp4_6", 256, "sp"),
-    ("evm", "V", "b4_6", "sp4_6", 0),
-    ("storeu", "sp2_6", 2, 6, 1, 0),
-    ("mxu", 7, 0, "a7_0"),
-    ("stage", "sp5_6", 256, "sp"),
-    ("evm", "S", "b5_6", "sp5_6", 0),
-    ("storeu", "sp3_6", 3, 6, 1, 0),
-    ("mxu", 7, 1, "a7_1"),
-    ("storeu", "sp4_6", 4, 6, 1, 0),
-    ("stage", "H7", 2048, "hv"),
-    ("evu", "S", "a7_0", "H7", 0),
-    ("storeu", "sp5_6", 5, 6, 1, 0),
-    ("mxu", 7, 2, "a7_2"),
-    ("evu", "S", "a7_1", "H7", 256),
-    ("mxu", 7, 3, "a7_3"),
-    ("evu", "S", "a7_2", "H7", 512),
-    ("mxu", 7, 4, "a7_4"),
-    ("evu", "S", "a7_3", "H7", 768),
-    ("mxu", 7, 5, "a7_5"),
-    ("evu", "S", "a7_4", "H7", 1024),
-    ("storeu", "H7", 7, 0, 4, 0),
-    ("mxu", 7, 6, "a7_6"),
-    ("evu", "S", "a7_5", "H7", 1280),
-    ("mxu", 7, 7, "a7_7"),
-    ("evu", "S", "a7_6", "H7", 1536),
-    ("miru", 0, 7, "b0_7"),
-    ("evu", "S", "a7_7", "H7", 1792),
-    ("miru", 1, 7, "b1_7"),
-    ("stage", "sp0_7", 256, "sp"),
-    ("evm", "V", "b0_7", "sp0_7", 0),
-    ("miru", 2, 7, "b2_7"),
-    ("stage", "sp1_7", 256, "sp"),
-    ("evm", "S", "b1_7", "sp1_7", 0),
-    ("storeu", "H7", 7, 4, 4, 1024),
-    ("miru", 3, 7, "b3_7"),
-    ("stage", "sp2_7", 256, "sp"),
-    ("evm", "V", "b2_7", "sp2_7", 0),
-    ("storeu", "sp0_7", 0, 7, 1, 0),
-    ("miru", 4, 7, "b4_7"),
-    ("stage", "sp3_7", 256, "sp"),
-    ("evm", "S", "b3_7", "sp3_7", 0),
-    ("storeu", "sp1_7", 1, 7, 1, 0),
-    ("miru", 5, 7, "b5_7"),
-    ("stage", "sp4_7", 256, "sp"),
-    ("evm", "V", "b4_7", "sp4_7", 0),
-    ("storeu", "sp2_7", 2, 7, 1, 0),
-    ("miru", 6, 7, "b6_7"),
-    ("stage", "sp5_7", 256, "sp"),
-    ("evm", "S", "b5_7", "sp5_7", 0),
-    ("storeu", "sp3_7", 3, 7, 1, 0),
-    ("storeu", "sp4_7", 4, 7, 1, 0),
-    ("stage", "sp6_7", 256, "sp"),
-    ("evm", "S", "b6_7", "sp6_7", 0),
-    ("storeu", "sp5_7", 5, 7, 1, 0),
-    ("storeu", "sp6_7", 6, 7, 1, 0),
-]
+GROUPS = ((0, 2), (2, 2), (4, 4), (8, 4), (12, 4))
+STORE_UNITS = 4
+VECTOR_HELPS_FROM = 5
 
 
 def tile_attentive_kernel(tc, x, attn_vectors, out):
@@ -348,199 +30,277 @@ def tile_attentive_kernel(tc, x, attn_vectors, out):
         ctx.enter_context(tc.manual_schedule())
         keep = ctx.enter_context(tc.tile_pool(name="keep", bufs=1))
         small = ctx.enter_context(tc.tile_pool(name="small", bufs=5))
-        gpool = ctx.enter_context(tc.tile_pool(name="gp", bufs=3))
-        pools = {
-            "hv": ctx.enter_context(tc.tile_pool(name="hv", bufs=3)),
-            "sp": ctx.enter_context(tc.tile_pool(name="sp", bufs=12)),
-            "fr": ctx.enter_context(tc.psum_pool(name="fr", bufs=4)),
-            "acc": ctx.enter_context(tc.psum_pool(name="acc", bufs=4)),
-        }
+        grouped_pool = ctx.enter_context(tc.tile_pool(name="grouped", bufs=3))
+        rows_pool = ctx.enter_context(tc.tile_pool(name="rows", bufs=3))
+        mirror_pool = ctx.enter_context(tc.tile_pool(name="mirror", bufs=12))
+        spread_psum = ctx.enter_context(tc.psum_pool(name="spread", bufs=4))
+        work_psum = ctx.enter_context(tc.psum_pool(name="work", bufs=4))
 
-        a0 = keep.tile([P, D], BF16)
-        nc.vector.memset(a0[:], 0.0)
-        nc.scalar.dma_start(out=a0[0:H, :], in_=attn_vectors)
-        x_sb = keep.tile([P, NT * D], BF16)
-        for t0, nt in UNITS:
+        a_rows = keep.tile([P, D], BF16)
+        nc.vector.memset(a_rows[:], 0.0)
+        nc.scalar.dma_start(out=a_rows[0:H, :], in_=attn_vectors)
+        x_sb = keep.tile([P, TILES * D], BF16)
+        for first, count in GROUPS:
             nc.sync.dma_start(
-                out=x_sb[:, t0 * D:(t0 + nt) * D].rearrange("p (t d) -> p t d", d=D),
-                in_=x[t0 * P:(t0 + nt) * P, :].rearrange("(t p) d -> p t d", p=P),
+                out=x_sb[:, first * D:(first + count) * D].rearrange("p (t d) -> p t d", d=D),
+                in_=x[first * P:(first + count) * P, :].rearrange("(t p) d -> p t d", p=P),
             )
-        dmz = keep.tile([P, CH], BF16)
-        nc.vector.memset(dmz[:], 0.0)
-        warm = keep.tile([P, 1], F32)
-        nc.vector.memset(warm[:], 1.0)
-        warm2 = keep.tile([P, 1], F32)
-        nc.scalar.activation(out=warm2[:], in_=warm[:], func=ACT.Sqrt)
-        ident_f = keep.tile([P, P], F32)
-        make_identity(nc, ident_f[:])
+        zeros = keep.tile([P, 4 * P], BF16)
+        nc.vector.memset(zeros[:], 0.0)
+        one = keep.tile([P, 1], F32)
+        nc.vector.memset(one[:], 1.0)
+        unused_root = keep.tile([P, 1], F32)
+        nc.scalar.activation(out=unused_root[:], in_=one[:], func=ACT.Sqrt)
+        identity = keep.tile([P, P], F32)
+        make_identity(nc, identity[:])
 
-        xT_w = keep.tile([P, N], F32)
+        xT_words = keep.tile([P, N], F32)
         x2T = keep.tile([P, 2, N], F32)
-        aT_f = keep.tile([P, 2 * H], F32)
+        aT = keep.tile([P, 2 * H], F32)
         a2T = keep.tile([P, 2, H], F32)
-        r_sb = keep.tile([P, NT * H], F32)
-        xa = keep.tile([P, 2, 4, N], F32)
+        r_sb = keep.tile([P, TILES * H], F32)
+        ax = keep.tile([P, 2, 4, N], F32)
         codes = keep.tile([P, 2, N], U32, align_bytes=64)
-        scl = keep.tile([P, 2, N], U8, align_bytes=64)
+        scales = keep.tile([P, 2, N], U8, align_bytes=64)
 
-        xw = x_sb[:].bitcast(F32)
-        xT_b = xT_w[:].bitcast(BF16).rearrange("p (n e) -> p n e", e=2)
+        x_words = x_sb[:].bitcast(F32)
+        xT = xT_words[:].bitcast(BF16).rearrange("p (n e) -> p n e", e=2)
 
-        tiles = {}
+        xT_psum, sums_psum, clamped, roots, spread, grouped, rows = {}, {}, {}, {}, {}, {}, {}
 
-        for call in PROGRAM:
-            op = call[0]
-            if op == "dm":
-                tl = pools["acc"].tile([P, CH], F32, tag="acc")
-                nc.tensor.matmul(out=tl[:], lhsT=dmz[:, 0:P], rhs=dmz[:], start=True, stop=True)
-            elif op == "aT":
-                tl = pools["fr"].tile([P, P], F32, tag="fr")
-                tiles["aT"] = tl
-                nc.tensor.transpose(tl[:], a0[:].bitcast(F32), ident_f[:])
-            elif op == "aTf":
-                nc.vector.tensor_copy(out=aT_f[:], in_=tiles["aT"][:].bitcast(BF16)[:, 0:2 * H])
-            elif op == "a2T":
-                nc.scalar.activation(out=a2T[:], in_=aT_f[:].rearrange("p (h e) -> p e h", e=2), func=ACT.Square)
-            elif op == "xt":
-                t0, nt, key = call[1], call[2], call[3]
-                tl = pools["acc"].tile([P, nt * P], F32, tag="acc")
-                tiles[key] = tl
-                for j in range(nt):
-                    t = t0 + j
-                    nc.tensor.transpose(tl[:, j * P:(j + 1) * P], xw[:, t * P:(t + 1) * P], ident_f[:])
-            elif op == "sqp":
-                t0, nt, key = call[1], call[2], call[3]
-                nc.scalar.activation(
-                    out=x2T[:, :, t0 * P:(t0 + nt) * P],
-                    in_=tiles[key][:].bitcast(BF16).rearrange("p (n e) -> p e n", e=2),
-                    func=ACT.Square,
-                )
-            elif op == "cpx":
-                eng, t0, nt, key = call[1], call[2], call[3], call[4]
-                if eng == "V":
-                    nc.vector.tensor_copy(out=xT_w[:, t0 * P:(t0 + nt) * P], in_=tiles[key][:])
+        def keep_clock_up(count):
+            for repeat in range(count):
+                idle = work_psum.tile([P, 4 * P], F32, tag="work")
+                nc.tensor.matmul(out=idle[:], lhsT=zeros[:, 0:P], rhs=zeros[:], start=True, stop=True)
+
+        def transpose_x(g):
+            first, count = GROUPS[g]
+            bank = work_psum.tile([P, count * P], F32, tag="work")
+            xT_psum[g] = bank
+            for j in range(count):
+                t = first + j
+                nc.tensor.transpose(bank[:, j * P:(j + 1) * P], x_words[:, t * P:(t + 1) * P], identity[:])
+
+        def square_x(g):
+            first, count = GROUPS[g]
+            nc.scalar.activation(
+                out=x2T[:, :, first * P:(first + count) * P],
+                in_=xT_psum[g][:].bitcast(BF16).rearrange("p (n e) -> p e n", e=2),
+                func=ACT.Square,
+            )
+
+        def copy_x(engine, g):
+            first, count = GROUPS[g]
+            if engine == "vector":
+                nc.vector.tensor_copy(out=xT_words[:, first * P:(first + count) * P], in_=xT_psum[g][:])
+            else:
+                nc.scalar.copy(out=xT_words[:, first * P:(first + count) * P], in_=xT_psum[g][:])
+
+        def sum_squares(g):
+            first, count = GROUPS[g]
+            bank = work_psum.tile([P, count * H], F32, tag="work")
+            sums_psum[g] = bank
+            for j in range(count):
+                t = first + j
+                for e in range(2):
+                    nc.tensor.matmul(
+                        out=bank[:, j * H:(j + 1) * H],
+                        lhsT=x2T[:, e, t * P:(t + 1) * P],
+                        rhs=a2T[:, e, :],
+                        start=(e == 0),
+                        stop=(e == 1),
+                    )
+
+        def clamp(g):
+            at_least_eps = small.tile([P, GROUPS[g][1] * H], F32, tag="clamped")
+            clamped[g] = at_least_eps
+            nc.vector.tensor_scalar_max(out=at_least_eps[:], in0=sums_psum[g][:], scalar1=EPS)
+
+        def root(g):
+            norm = small.tile([P, GROUPS[g][1] * H], F32, tag="roots")
+            roots[g] = norm
+            nc.scalar.activation(out=norm[:], in_=clamped[g][:], func=ACT.Sqrt)
+
+        def invert(g):
+            first, count = GROUPS[g]
+            nc.vector.reciprocal(out=r_sb[:, first * H:(first + count) * H], in_=roots[g][:])
+
+        def times_a(engine, g, planes):
+            first, count = GROUPS[g]
+            for plane in planes:
+                c, t = plane // 4, plane % 4
+                h, e = 2 * c + t // 2, t % 2
+                dst = ax[:, c, t, first * P:(first + count) * P]
+                src = xT[:, first * P:(first + count) * P, e]
+                a_col = aT[:, 2 * h + e:2 * h + e + 1]
+                if engine == "vector":
+                    nc.vector.tensor_scalar_mul(out=dst, in0=src, scalar1=a_col)
+                elif engine == "scalar":
+                    nc.scalar.activation(out=dst, in_=src, func=ACT.Copy, scale=a_col)
                 else:
-                    nc.scalar.copy(out=xT_w[:, t0 * P:(t0 + nt) * P], in_=tiles[key][:])
-            elif op == "smm":
-                t0, nt, key = call[1], call[2], call[3]
-                tl = pools["acc"].tile([P, nt * H], F32, tag="acc")
-                tiles[key] = tl
-                for j in range(nt):
-                    t = t0 + j
-                    for e in range(2):
-                        nc.tensor.matmul(
-                            out=tl[:, j * H:(j + 1) * H],
-                            lhsT=x2T[:, e, t * P:(t + 1) * P],
-                            rhs=a2T[:, e, :],
-                            start=(e == 0),
-                            stop=(e == 1),
-                        )
-            elif op == "max":
-                i, t0, nt, key = call[1], call[2], call[3], call[4]
-                sm = small.tile([P, nt * H], F32, tag="sm")
-                tiles["sm%d" % i] = sm
-                nc.vector.tensor_scalar_max(out=sm[:], in0=tiles[key][:], scalar1=EPS)
-            elif op == "sqrt":
-                i, nt = call[1], call[2]
-                sq = small.tile([P, nt * H], F32, tag="sq")
-                tiles["sq%d" % i] = sq
-                nc.scalar.activation(out=sq[:], in_=tiles["sm%d" % i][:], func=ACT.Sqrt)
-            elif op == "rec":
-                i, t0, nt = call[1], call[2], call[3]
-                nc.vector.reciprocal(out=r_sb[:, t0 * H:(t0 + nt) * H], in_=tiles["sq%d" % i][:])
-            elif op == "xa4":
-                eng, t0, nt, c = call[1], call[2], call[3], call[4]
-                for t in range(4):
-                    h, e = 2 * c + t // 2, t % 2
-                    dst = xa[:, c, t, t0 * P:(t0 + nt) * P]
-                    src = xT_b[:, t0 * P:(t0 + nt) * P, e]
-                    sca = aT_f[:, 2 * h + e:2 * h + e + 1]
-                    if eng == "V":
-                        nc.vector.tensor_scalar_mul(out=dst, in0=src, scalar1=sca)
-                    elif eng == "S":
-                        nc.scalar.activation(out=dst, in_=src, func=ACT.Copy, scale=sca)
-                    else:
-                        nc.gpsimd.tensor_scalar(out=dst, in0=src, scalar1=sca, scalar2=0.0, op0=ALU.mult, op1=ALU.add)
-            elif op == "R":
-                u, c, key = call[1], call[2], call[3]
-                tl = pools["fr"].tile([P, 2, PR], F32, tag="fr")
-                tiles[key] = tl
-                for hh in range(2):
-                    for q in range(2):
-                        col = (2 * u + q) * H + 2 * c + hh
-                        nc.tensor.transpose(
-                            tl[:, hh, q * P:(q + 1) * P],
-                            r_sb[:, col:col + 1].to_broadcast([P, P]),
-                            ident_f[:],
-                        )
-            elif op == "TT":
-                u, c, key = call[1], call[2], call[3]
-                if ("gp%d" % u) not in tiles:
-                    gp = gpool.tile([P, 2, PR, 4], BF16, tag="gp", align_bytes=64)
-                    tiles["gp%d" % u] = gp
-                n0 = u * PR
-                nc.vector.tensor_tensor(
-                    out=tiles["gp%d" % u][:, c, :, :].rearrange("p n (h e) -> p n h e", e=2),
-                    in0=xa[:, c, :, n0:n0 + PR].rearrange("p (h e) n -> p n h e", e=2),
-                    in1=tiles[key][:].rearrange("p h n -> p n h").unsqueeze(3).to_broadcast([P, PR, 2, 2]),
-                    op=ALU.mult,
-                )
-            elif op == "Q":
-                u, c = call[1], call[2]
-                n0 = u * PR
+                    nc.gpsimd.tensor_scalar(out=dst, in0=src, scalar1=a_col, scalar2=0.0, op0=ALU.mult, op1=ALU.add)
+
+        def spread_r(u, c):
+            bank = spread_psum.tile([P, 2, PAIR], F32, tag="spread")
+            spread[u, c] = bank
+            for hh in range(2):
+                for q in range(2):
+                    col = (2 * u + q) * H + 2 * c + hh
+                    nc.tensor.transpose(
+                        bank[:, hh, q * P:(q + 1) * P],
+                        r_sb[:, col:col + 1].to_broadcast([P, P]),
+                        identity[:],
+                    )
+
+        def normalise(u, c):
+            if c == 0:
+                words = grouped_pool.tile([P, 2, PAIR, 4], BF16, tag="grouped", align_bytes=64)
+                grouped[u] = words
+            nc.vector.tensor_tensor(
+                out=grouped[u][:, c, :, :].rearrange("p n (h e) -> p n h e", e=2),
+                in0=ax[:, c, :, u * PAIR:(u + 1) * PAIR].rearrange("p (h e) n -> p n h e", e=2),
+                in1=spread[u, c][:].rearrange("p h n -> p n h").unsqueeze(3).to_broadcast([P, PAIR, 2, 2]),
+                op=ALU.mult,
+            )
+
+        def quantise(u):
+            for c in range(2):
                 nc.vector.quantize_mx(
-                    out=codes[:, c, n0:n0 + PR].bitcast(FP8X4),
-                    scales=scl[:, c, n0:n0 + PR],
-                    in_=tiles["gp%d" % u][:, c, :, :].rearrange("p n j -> p (n j)"),
+                    out=codes[:, c, u * PAIR:(u + 1) * PAIR].bitcast(FP8X4),
+                    scales=scales[:, c, u * PAIR:(u + 1) * PAIR],
+                    in_=grouped[u][:, c, :, :].rearrange("p n j -> p (n j)"),
                 )
-            elif op == "stage":
-                key, width, tag = call[1], call[2], call[3]
-                tl = pools[tag].tile([P, 2, width], F32, tag=tag)
-                tiles[key] = tl
-            elif op == "mxu":
-                v, w, key = call[1], call[2], call[3]
-                tl = pools["acc"].tile([P, 2, PR], F32, tag="acc")
-                tiles[key] = tl
+
+        def store(tile_ap, v, w, units):
+            nc.sync.dma_start(
+                out=out[v * PAIR:(v + 1) * PAIR, w * PAIR:(w + units) * PAIR].rearrange("(r p) c -> p r c", p=P),
+                in_=tile_ap,
+            )
+
+        def row_block(v):
+            block = rows_pool.tile([P, 2, (v + 1) * PAIR], F32, tag="rows")
+            rows[v] = block
+            for w in range(v + 1):
+                bank = work_psum.tile([P, 2, PAIR], F32, tag="work")
                 for r in range(2):
                     i = 2 * v + r
                     for c in range(2):
                         nc.tensor.matmul_mx(
-                            out=tl[:, r, :],
+                            out=bank[:, r, :],
                             lhsT=codes[:, c, i * P:(i + 1) * P].bitcast(FP8X4),
-                            lhsT_scale=scl[:, c, i * P:(i + 1) * P],
-                            rhs=codes[:, c, w * PR:(w + 1) * PR].bitcast(FP8X4),
-                            rhs_scale=scl[:, c, w * PR:(w + 1) * PR],
+                            lhsT_scale=scales[:, c, i * P:(i + 1) * P],
+                            rhs=codes[:, c, w * PAIR:(w + 1) * PAIR].bitcast(FP8X4),
+                            rhs_scale=scales[:, c, w * PAIR:(w + 1) * PAIR],
                             start=(c == 0),
                             stop=(c == 1),
                         )
-            elif op == "evu":
-                eng, key, st, off = call[1], call[2], call[3], call[4]
-                if eng == "V":
-                    nc.vector.tensor_scalar_mul(out=tiles[st][:, :, off:off + PR], in0=tiles[key][:], scalar1=0.25)
-                else:
-                    nc.scalar.mul(out=tiles[st][:, :, off:off + PR], in_=tiles[key][:], mul=0.25)
-            elif op == "miru":
-                w, v, key = call[1], call[2], call[3]
-                tl = pools["acc"].tile([P, 2, PR], F32, tag="acc")
-                tiles[key] = tl
+                nc.scalar.mul(out=block[:, :, w * PAIR:(w + 1) * PAIR], in_=bank[:], mul=0.25)
+                if (w + 1) % STORE_UNITS == 0 or w == v:
+                    w0 = w - w % STORE_UNITS
+                    store(block[:, :, w0 * PAIR:(w + 1) * PAIR], v, w0, w - w0 + 1)
+
+        def mirror_block(v):
+            for w in range(v):
+                bank = work_psum.tile([P, 2, PAIR], F32, tag="work")
                 for r in range(2):
                     for q in range(2):
                         nc.tensor.transpose(
-                            tl[:, r, q * P:(q + 1) * P],
-                            tiles["H%d" % v][:, q, (2 * w + r) * P:(2 * w + r + 1) * P],
-                            ident_f[:],
+                            bank[:, r, q * P:(q + 1) * P],
+                            rows[v][:, q, (2 * w + r) * P:(2 * w + r + 1) * P],
+                            identity[:],
                         )
-            elif op == "evm":
-                eng, key, st, off = call[1], call[2], call[3], call[4]
-                if eng == "V":
-                    nc.vector.tensor_copy(out=tiles[st][:, :, off:off + PR], in_=tiles[key][:])
+                unit = mirror_pool.tile([P, 2, PAIR], F32, tag="mirror")
+                if v >= VECTOR_HELPS_FROM and w % 2 == 0:
+                    nc.vector.tensor_copy(out=unit[:], in_=bank[:])
                 else:
-                    nc.scalar.copy(out=tiles[st][:, :, off:off + PR], in_=tiles[key][:])
-            elif op == "storeu":
-                st, v, w0, m, off = call[1], call[2], call[3], call[4], call[5]
-                nc.sync.dma_start(
-                    out=out[v * PR:(v + 1) * PR, w0 * PR:(w0 + m) * PR].rearrange("(r p) c -> p r c", p=P),
-                    in_=tiles[st][:, :, off:off + m * PR],
-                )
-            else:
-                assert False, op
+                    nc.scalar.copy(out=unit[:], in_=bank[:])
+                store(unit[:], w, v, 1)
+
+        keep_clock_up(6)
+        aT_psum = spread_psum.tile([P, P], F32, tag="spread")
+        nc.tensor.transpose(aT_psum[:], a_rows[:].bitcast(F32), identity[:])
+        nc.vector.tensor_copy(out=aT[:], in_=aT_psum[:].bitcast(BF16)[:, 0:2 * H])
+        nc.scalar.activation(out=a2T[:], in_=aT[:].rearrange("p (h e) -> p e h", e=2), func=ACT.Square)
+        transpose_x(0)
+        keep_clock_up(1)
+        square_x(0)
+        copy_x("scalar", 0)
+        transpose_x(1)
+        keep_clock_up(2)
+        square_x(1)
+        copy_x("scalar", 1)
+        sum_squares(0)
+        transpose_x(2)
+        keep_clock_up(2)
+        times_a("vector", 0, range(0, 3))
+        clamp(0)
+        times_a("scalar", 1, range(0, 2))
+        root(0)
+        times_a("vector", 0, range(3, 7))
+        invert(0)
+        sum_squares(1)
+        transpose_x(3)
+        keep_clock_up(1)
+        square_x(2)
+        times_a("vector", 0, range(7, 8))
+        clamp(1)
+        root(1)
+        times_a("vector", 1, range(2, 6))
+        invert(1)
+        times_a("vector", 1, range(6, 8))
+        spread_r(0, 0)
+        spread_r(0, 1)
+        keep_clock_up(1)
+        copy_x("scalar", 2)
+        sum_squares(2)
+        keep_clock_up(2)
+        times_a("scalar", 2, range(0, 3))
+        spread_r(1, 0)
+        keep_clock_up(1)
+        spread_r(1, 1)
+        transpose_x(4)
+        keep_clock_up(1)
+        normalise(0, 0)
+        clamp(2)
+        root(2)
+        times_a("scalar", 2, range(3, 4))
+        square_x(3)
+        normalise(0, 1)
+        invert(2)
+        quantise(0)
+        spread_r(2, 0)
+        spread_r(2, 1)
+        keep_clock_up(1)
+        sum_squares(3)
+        times_a("scalar", 2, range(4, 8))
+        square_x(4)
+
+        for v in range(PAIRS):
+            u = v + 1
+            if u < PAIRS:
+                normalise(u, 0)
+                if u == 1:
+                    copy_x("vector", 3)
+                    times_a("gpsimd", 3, range(0, 8))
+                elif u == 2:
+                    invert(3)
+                elif u == 3:
+                    invert(4)
+                normalise(u, 1)
+                if u == 1:
+                    clamp(3)
+                quantise(u)
+            row_block(v)
+            if v == 0:
+                root(3)
+                copy_x("scalar", 4)
+                times_a("gpsimd", 4, range(0, 8))
+            elif v == 1:
+                sum_squares(4)
+            mirror_block(v)
+            if v == 1:
+                clamp(4)
+                root(4)
+            if v + 3 < PAIRS:
+                spread_r(v + 3, 0)
+                spread_r(v + 3, 1)

@@ -20,8 +20,11 @@ PAIRS = N // PAIR
 EPS = 1e-12
 FLOPS = 2 * N * N * K
 GROUPS = ((0, 2), (2, 2), (4, 4), (8, 4), (12, 4))
-STORE_UNITS = 4
-VECTOR_HELPS_FROM = 5
+VD = (0,0,0,0,0,0,4,4)
+MD = (0,0,0,0,0,0,7,7)
+WIDE_FROM = 6
+VP = 2
+R_MAX = EPS ** -0.5
 
 
 def tile_attentive_kernel(tc, x, attn_vectors, out):
@@ -32,15 +35,16 @@ def tile_attentive_kernel(tc, x, attn_vectors, out):
         small = ctx.enter_context(tc.tile_pool(name="small", bufs=5))
         grouped_pool = ctx.enter_context(tc.tile_pool(name="grouped", bufs=3))
         rows_pool = ctx.enter_context(tc.tile_pool(name="rows", bufs=3))
-        mirror_pool = ctx.enter_context(tc.tile_pool(name="mirror", bufs=12))
+        mirror_pool = ctx.enter_context(tc.tile_pool(name="mirror", bufs=10))
         spread_psum = ctx.enter_context(tc.psum_pool(name="spread", bufs=4))
         work_psum = ctx.enter_context(tc.psum_pool(name="work", bufs=4))
 
         a_rows = keep.tile([P, D], BF16)
         nc.vector.memset(a_rows[:], 0.0)
-        nc.scalar.dma_start(out=a_rows[0:H, :], in_=attn_vectors)
         x_sb = keep.tile([P, TILES * D], BF16)
         for first, count in GROUPS:
+            if first == 2:
+                nc.sync.dma_start(out=a_rows[0:H, :], in_=attn_vectors)
             nc.sync.dma_start(
                 out=x_sb[:, first * D:(first + count) * D].rearrange("p (t d) -> p t d", d=D),
                 in_=x[first * P:(first + count) * P, :].rearrange("(t p) d -> p t d", p=P),
@@ -50,7 +54,7 @@ def tile_attentive_kernel(tc, x, attn_vectors, out):
         one = keep.tile([P, 1], F32)
         nc.vector.memset(one[:], 1.0)
         unused_root = keep.tile([P, 1], F32)
-        nc.scalar.activation(out=unused_root[:], in_=one[:], func=ACT.Sqrt)
+        nc.scalar.activation(out=unused_root[:], in_=one[:], func=ACT.Abs_reciprocal_sqrt)
         identity = keep.tile([P, P], F32)
         make_identity(nc, identity[:])
 
@@ -66,35 +70,35 @@ def tile_attentive_kernel(tc, x, attn_vectors, out):
         x_words = x_sb[:].bitcast(F32)
         xT = xT_words[:].bitcast(BF16).rearrange("p (n e) -> p n e", e=2)
 
-        xT_psum, sums_psum, clamped, roots, spread, grouped, rows = {}, {}, {}, {}, {}, {}, {}
+        sums_psum, roots, spread, grouped, rows = {}, {}, {}, {}, {}
 
         def keep_clock_up(count):
             for repeat in range(count):
                 idle = work_psum.tile([P, 4 * P], F32, tag="work")
                 nc.tensor.matmul(out=idle[:], lhsT=zeros[:, 0:P], rhs=zeros[:], start=True, stop=True)
 
-        def transpose_x(g):
+        def transpose_x(g, pool=None, tag="work"):
             first, count = GROUPS[g]
-            bank = work_psum.tile([P, count * P], F32, tag="work")
-            xT_psum[g] = bank
+            bank = (pool or work_psum).tile([P, count * P], F32, tag=tag)
             for j in range(count):
                 t = first + j
                 nc.tensor.transpose(bank[:, j * P:(j + 1) * P], x_words[:, t * P:(t + 1) * P], identity[:])
+            return bank
 
-        def square_x(g):
+        def square_x(g, bank):
             first, count = GROUPS[g]
             nc.scalar.activation(
                 out=x2T[:, :, first * P:(first + count) * P],
-                in_=xT_psum[g][:].bitcast(BF16).rearrange("p (n e) -> p e n", e=2),
+                in_=bank[:].bitcast(BF16).rearrange("p (n e) -> p e n", e=2),
                 func=ACT.Square,
             )
 
-        def copy_x(engine, g):
+        def copy_x(engine, g, bank):
             first, count = GROUPS[g]
             if engine == "vector":
-                nc.vector.tensor_copy(out=xT_words[:, first * P:(first + count) * P], in_=xT_psum[g][:])
+                nc.vector.tensor_copy(out=xT_words[:, first * P:(first + count) * P], in_=bank[:])
             else:
-                nc.scalar.copy(out=xT_words[:, first * P:(first + count) * P], in_=xT_psum[g][:])
+                nc.scalar.copy(out=xT_words[:, first * P:(first + count) * P], in_=bank[:])
 
         def sum_squares(g):
             first, count = GROUPS[g]
@@ -111,27 +115,26 @@ def tile_attentive_kernel(tc, x, attn_vectors, out):
                         stop=(e == 1),
                     )
 
-        def clamp(g):
-            at_least_eps = small.tile([P, GROUPS[g][1] * H], F32, tag="clamped")
-            clamped[g] = at_least_eps
-            nc.vector.tensor_scalar_max(out=at_least_eps[:], in0=sums_psum[g][:], scalar1=EPS)
-
         def root(g):
-            norm = small.tile([P, GROUPS[g][1] * H], F32, tag="roots")
-            roots[g] = norm
-            nc.scalar.activation(out=norm[:], in_=clamped[g][:], func=ACT.Sqrt)
+            rsqrt = small.tile([P, GROUPS[g][1] * H], F32, tag="roots")
+            roots[g] = rsqrt
+            nc.scalar.activation(out=rsqrt[:], in_=sums_psum[g][:], func=ACT.Abs_reciprocal_sqrt)
 
-        def invert(g):
+        def cap(engine, g):
             first, count = GROUPS[g]
-            nc.vector.reciprocal(out=r_sb[:, first * H:(first + count) * H], in_=roots[g][:])
+            dst = r_sb[:, first * H:(first + count) * H]
+            if engine == "vector":
+                nc.vector.tensor_scalar_min(out=dst, in0=roots[g][:], scalar1=R_MAX)
+            else:
+                nc.gpsimd.tensor_scalar_min(out=dst, in0=roots[g][:], scalar1=R_MAX)
 
-        def times_a(engine, g, planes):
-            first, count = GROUPS[g]
+        def times_a(engine, u, planes):
+            cols = slice(u * PAIR, (u + 1) * PAIR)
             for plane in planes:
                 c, t = plane // 4, plane % 4
                 h, e = 2 * c + t // 2, t % 2
-                dst = ax[:, c, t, first * P:(first + count) * P]
-                src = xT[:, first * P:(first + count) * P, e]
+                dst = ax[:, c, t, cols]
+                src = xT[:, cols, e]
                 a_col = aT[:, 2 * h + e:2 * h + e + 1]
                 if engine == "vector":
                     nc.vector.tensor_scalar_mul(out=dst, in0=src, scalar1=a_col)
@@ -140,17 +143,18 @@ def tile_attentive_kernel(tc, x, attn_vectors, out):
                 else:
                     nc.gpsimd.tensor_scalar(out=dst, in0=src, scalar1=a_col, scalar2=0.0, op0=ALU.mult, op1=ALU.add)
 
-        def spread_r(u, c):
-            bank = spread_psum.tile([P, 2, PAIR], F32, tag="spread")
-            spread[u, c] = bank
-            for hh in range(2):
-                for q in range(2):
-                    col = (2 * u + q) * H + 2 * c + hh
-                    nc.tensor.transpose(
-                        bank[:, hh, q * P:(q + 1) * P],
-                        r_sb[:, col:col + 1].to_broadcast([P, P]),
-                        identity[:],
-                    )
+        def spread_r(u):
+            for c in range(2):
+                bank = spread_psum.tile([P, 2, PAIR], F32, tag="spread")
+                spread[u, c] = bank
+                for hh in range(2):
+                    for q in range(2):
+                        col = (2 * u + q) * H + 2 * c + hh
+                        nc.tensor.transpose(
+                            bank[:, hh, q * P:(q + 1) * P],
+                            r_sb[:, col:col + 1].to_broadcast([P, P]),
+                            identity[:],
+                        )
 
         def normalise(u, c):
             if c == 0:
@@ -177,6 +181,19 @@ def tile_attentive_kernel(tc, x, attn_vectors, out):
                 in_=tile_ap,
             )
 
+        def drain(engine, dst, bank, scale):
+            if engine == "vector" and scale:
+                nc.vector.tensor_scalar_mul(out=dst, in0=bank[:], scalar1=0.25)
+            elif engine == "vector":
+                nc.vector.tensor_copy(out=dst, in_=bank[:])
+            elif scale:
+                nc.scalar.mul(out=dst, in_=bank[:], mul=0.25)
+            else:
+                nc.scalar.copy(out=dst, in_=bank[:])
+
+        def pick(n, left):
+            return "vector" if left < 2 * n and left % 2 == 0 else "scalar"
+
         def row_block(v):
             block = rows_pool.tile([P, 2, (v + 1) * PAIR], F32, tag="rows")
             rows[v] = block
@@ -194,113 +211,104 @@ def tile_attentive_kernel(tc, x, attn_vectors, out):
                             start=(c == 0),
                             stop=(c == 1),
                         )
-                nc.scalar.mul(out=block[:, :, w * PAIR:(w + 1) * PAIR], in_=bank[:], mul=0.25)
-                if (w + 1) % STORE_UNITS == 0 or w == v:
-                    w0 = w - w % STORE_UNITS
+                drain(pick(VD[v], v - w), block[:, :, w * PAIR:(w + 1) * PAIR], bank, True)
+                n_store = 2 if v < 5 else 4
+                if (w + 1) % n_store == 0 or w == v:
+                    w0 = w - w % n_store
                     store(block[:, :, w0 * PAIR:(w + 1) * PAIR], v, w0, w - w0 + 1)
 
-        def mirror_block(v):
-            for w in range(v):
-                bank = work_psum.tile([P, 2, PAIR], F32, tag="work")
-                for r in range(2):
-                    for q in range(2):
-                        nc.tensor.transpose(
-                            bank[:, r, q * P:(q + 1) * P],
-                            rows[v][:, q, (2 * w + r) * P:(2 * w + r + 1) * P],
-                            identity[:],
-                        )
-                unit = mirror_pool.tile([P, 2, PAIR], F32, tag="mirror")
-                if v >= VECTOR_HELPS_FROM and w % 2 == 0:
-                    nc.vector.tensor_copy(out=unit[:], in_=bank[:])
-                else:
-                    nc.scalar.copy(out=unit[:], in_=bank[:])
-                store(unit[:], w, v, 1)
+        def mirror_block(pairs):
+            for w in range(pairs[-1]):
+                unit = mirror_pool.tile([P, 2, 2 * PAIR], F32, tag="mirror")
+                vs = [v for v in pairs if v > w]
+                for at, v in enumerate(vs):
+                    bank = work_psum.tile([P, 2, PAIR], F32, tag="work")
+                    for r in range(2):
+                        for q in range(2):
+                            nc.tensor.transpose(
+                                bank[:, r, q * P:(q + 1) * P],
+                                rows[v][:, q, (2 * w + r) * P:(2 * w + r + 1) * P],
+                                identity[:],
+                            )
+                    drain(pick(MD[v], v - 1 - w), unit[:, :, at * PAIR:(at + 1) * PAIR], bank, False)
+                store(unit[:, :, 0:len(vs) * PAIR], w, vs[0], len(vs))
 
-        keep_clock_up(6)
+        keep_clock_up(3)
         aT_psum = spread_psum.tile([P, P], F32, tag="spread")
         nc.tensor.transpose(aT_psum[:], a_rows[:].bitcast(F32), identity[:])
         nc.vector.tensor_copy(out=aT[:], in_=aT_psum[:].bitcast(BF16)[:, 0:2 * H])
         nc.scalar.activation(out=a2T[:], in_=aT[:].rearrange("p (h e) -> p e h", e=2), func=ACT.Square)
-        transpose_x(0)
-        keep_clock_up(1)
-        square_x(0)
-        copy_x("scalar", 0)
-        transpose_x(1)
-        keep_clock_up(2)
-        square_x(1)
-        copy_x("scalar", 1)
+        b0 = transpose_x(0)
+        b0b = transpose_x(0, spread_psum, "spread")
+        b1 = transpose_x(1)
+        b2 = transpose_x(2)
+        square_x(0, b0)
+        copy_x("vector", 0, b0b)
+        times_a("vector", 0, range(0, 5))
         sum_squares(0)
-        transpose_x(2)
-        keep_clock_up(2)
-        times_a("vector", 0, range(0, 3))
-        clamp(0)
-        times_a("scalar", 1, range(0, 2))
+        square_x(1, b1)
         root(0)
-        times_a("vector", 0, range(3, 7))
-        invert(0)
+        copy_x("scalar", 1, b1)
+        cap("vector", 0)
         sum_squares(1)
-        transpose_x(3)
-        keep_clock_up(1)
-        square_x(2)
-        times_a("vector", 0, range(7, 8))
-        clamp(1)
         root(1)
-        times_a("vector", 1, range(2, 6))
-        invert(1)
-        times_a("vector", 1, range(6, 8))
-        spread_r(0, 0)
-        spread_r(0, 1)
-        keep_clock_up(1)
-        copy_x("scalar", 2)
-        sum_squares(2)
-        keep_clock_up(2)
-        times_a("scalar", 2, range(0, 3))
-        spread_r(1, 0)
-        keep_clock_up(1)
-        spread_r(1, 1)
-        transpose_x(4)
-        keep_clock_up(1)
+        times_a("vector", 0, range(5, 8))
+        times_a("gpsimd", 1, range(0, 8))
+        spread_r(0)
+        cap("vector", 1)
+        square_x(2, b2)
+        spread_r(1)
         normalise(0, 0)
-        clamp(2)
+        b3 = transpose_x(3)
+        sum_squares(2)
+        copy_x("scalar", 2, b2)
         root(2)
-        times_a("scalar", 2, range(3, 4))
-        square_x(3)
         normalise(0, 1)
-        invert(2)
+        square_x(3, b3)
         quantise(0)
-        spread_r(2, 0)
-        spread_r(2, 1)
-        keep_clock_up(1)
+        cap("vector", 2)
+        for u in range(2, 4):
+            times_a("gpsimd", u, range(VP, 8))
+        row_block(0)
+        normalise(1, 0)
+        spread_r(2)
+        copy_x("scalar", 3, b3)
+        for u in range(4, 6):
+            times_a("gpsimd", u, range(VP, 8))
         sum_squares(3)
-        times_a("scalar", 2, range(4, 8))
-        square_x(4)
-
-        for v in range(PAIRS):
-            u = v + 1
-            if u < PAIRS:
-                normalise(u, 0)
-                if u == 1:
-                    copy_x("vector", 3)
-                    times_a("gpsimd", 3, range(0, 8))
-                elif u == 2:
-                    invert(3)
-                elif u == 3:
-                    invert(4)
-                normalise(u, 1)
-                if u == 1:
-                    clamp(3)
-                quantise(u)
-            row_block(v)
-            if v == 0:
-                root(3)
-                copy_x("scalar", 4)
-                times_a("gpsimd", 4, range(0, 8))
-            elif v == 1:
-                sum_squares(4)
-            mirror_block(v)
-            if v == 1:
-                clamp(4)
-                root(4)
-            if v + 3 < PAIRS:
-                spread_r(v + 3, 0)
-                spread_r(v + 3, 1)
+        b4 = transpose_x(4)
+        normalise(1, 1)
+        quantise(1)
+        times_a("vector", 2, range(0, VP))
+        square_x(4, b4)
+        root(3)
+        row_block(1)
+        normalise(2, 0)
+        cap("vector", 3)
+        sum_squares(4)
+        spread_r(3)
+        copy_x("scalar", 4, b4)
+        for w in range(6, 8):
+            times_a("gpsimd", w, range(VP, 8))
+        root(4)
+        normalise(2, 1)
+        times_a("vector", 3, range(0, VP))
+        quantise(2)
+        cap("vector", 4)
+        mirror_block((1,))
+        spread_r(4)
+        for u in range(3, PAIRS):
+            normalise(u, 0)
+            normalise(u, 1)
+            if u + 1 < PAIRS:
+                times_a("vector", u + 1, range(0, VP))
+            quantise(u)
+            row_block(u - 1)
+            if u + 2 < PAIRS:
+                spread_r(u + 2)
+            if u - 1 < WIDE_FROM:
+                mirror_block((u - 1,))
+            elif u % 2 == 0:
+                mirror_block((u - 2, u - 1))
+        row_block(7)
+        mirror_block((6, 7) if WIDE_FROM < 7 else (7,))

@@ -19,11 +19,10 @@ PAIR = 2 * P
 PAIRS = N // PAIR
 EPS = 1e-12
 FLOPS = 2 * N * N * K
-GROUPS = ((0, 2), (2, 2), (4, 4), (8, 4), (12, 4))
-VD = (0,0,0,0,0,0,4,4)
-MD = (0,0,0,0,0,0,7,7)
-WIDE_FROM = 6
-VP = 2
+GROUPS = tuple((t, 1) for t in range(TILES))
+LOADS = ((0, 2), (2, 2), (4, 4), (8, 8))
+VN = (0, 0, 1, 1, 2, 2, 3, 0)
+R_MAX = EPS ** -0.5
 R_MAX = EPS ** -0.5
 
 
@@ -33,20 +32,20 @@ def tile_attentive_kernel(tc, x, attn_vectors, out):
         ctx.enter_context(tc.manual_schedule())
         keep = ctx.enter_context(tc.tile_pool(name="keep", bufs=1))
         small = ctx.enter_context(tc.tile_pool(name="small", bufs=5))
+        y_pool = ctx.enter_context(tc.tile_pool(name="y", bufs=3))
         grouped_pool = ctx.enter_context(tc.tile_pool(name="grouped", bufs=3))
-        rows_pool = ctx.enter_context(tc.tile_pool(name="rows", bufs=3))
-        mirror_pool = ctx.enter_context(tc.tile_pool(name="mirror", bufs=10))
+        piece_pool = ctx.enter_context(tc.tile_pool(name="piece", bufs=1))
         spread_psum = ctx.enter_context(tc.psum_pool(name="spread", bufs=4))
         work_psum = ctx.enter_context(tc.psum_pool(name="work", bufs=4))
 
         a_rows = keep.tile([P, D], BF16)
         nc.vector.memset(a_rows[:], 0.0)
-        x_sb = keep.tile([P, TILES * D], BF16)
-        for first, count in GROUPS:
+        x_sb = keep.tile([P, TILES, D], BF16)
+        for first, count in LOADS:
             if first == 2:
                 nc.sync.dma_start(out=a_rows[0:H, :], in_=attn_vectors)
             nc.sync.dma_start(
-                out=x_sb[:, first * D:(first + count) * D].rearrange("p (t d) -> p t d", d=D),
+                out=x_sb[:, first:first + count, :],
                 in_=x[first * P:(first + count) * P, :].rearrange("(t p) d -> p t d", p=P),
             )
         zeros = keep.tile([P, 4 * P], BF16)
@@ -57,20 +56,19 @@ def tile_attentive_kernel(tc, x, attn_vectors, out):
         nc.scalar.activation(out=unused_root[:], in_=one[:], func=ACT.Abs_reciprocal_sqrt)
         identity = keep.tile([P, P], F32)
         make_identity(nc, identity[:])
+        pick_head = keep.tile([P, H], BF16)
+        nc.vector.tensor_copy(out=pick_head[:], in_=identity[:, 0:H])
 
-        xT_words = keep.tile([P, N], F32)
         x2T = keep.tile([P, 2, N], F32)
-        aT = keep.tile([P, 2 * H], F32)
         a2T = keep.tile([P, 2, H], F32)
+        a_all = keep.tile([P, H, D], BF16)
         r_sb = keep.tile([P, TILES * H], F32)
-        ax = keep.tile([P, 2, 4, N], F32)
-        codes = keep.tile([P, 2, N], U32, align_bytes=64)
-        scales = keep.tile([P, 2, N], U8, align_bytes=64)
+        codes = keep.tile([P, PAIRS, 2, PAIR], U32, align_bytes=64)
+        scales = keep.tile([P, PAIRS, 2, PAIR], U8, align_bytes=64)
 
-        x_words = x_sb[:].bitcast(F32)
-        xT = xT_words[:].bitcast(BF16).rearrange("p (n e) -> p n e", e=2)
+        x_words = x_sb[:].rearrange("p t d -> p (t d)").bitcast(F32)
 
-        sums_psum, roots, spread, grouped, rows = {}, {}, {}, {}, {}
+        sums_psum, roots, y_rows, turned, grouped, pieces, filled = {}, {}, {}, {}, {}, {}, {}
 
         def keep_clock_up(count):
             for repeat in range(count):
@@ -93,13 +91,6 @@ def tile_attentive_kernel(tc, x, attn_vectors, out):
                 func=ACT.Square,
             )
 
-        def copy_x(engine, g, bank):
-            first, count = GROUPS[g]
-            if engine == "vector":
-                nc.vector.tensor_copy(out=xT_words[:, first * P:(first + count) * P], in_=bank[:])
-            else:
-                nc.scalar.copy(out=xT_words[:, first * P:(first + count) * P], in_=bank[:])
-
         def sum_squares(g):
             first, count = GROUPS[g]
             bank = work_psum.tile([P, count * H], F32, tag="work")
@@ -120,195 +111,172 @@ def tile_attentive_kernel(tc, x, attn_vectors, out):
             roots[g] = rsqrt
             nc.scalar.activation(out=rsqrt[:], in_=sums_psum[g][:], func=ACT.Abs_reciprocal_sqrt)
 
-        def cap(engine, g):
+        def cap(g):
             first, count = GROUPS[g]
-            dst = r_sb[:, first * H:(first + count) * H]
-            if engine == "vector":
-                nc.vector.tensor_scalar_min(out=dst, in0=roots[g][:], scalar1=R_MAX)
-            else:
-                nc.gpsimd.tensor_scalar_min(out=dst, in0=roots[g][:], scalar1=R_MAX)
+            nc.vector.tensor_scalar_min(out=r_sb[:, first * H:(first + count) * H], in0=roots[g][:], scalar1=R_MAX)
 
-        def times_a(engine, u, planes):
-            cols = slice(u * PAIR, (u + 1) * PAIR)
-            for plane in planes:
-                c, t = plane // 4, plane % 4
-                h, e = 2 * c + t // 2, t % 2
-                dst = ax[:, c, t, cols]
-                src = xT[:, cols, e]
-                a_col = aT[:, 2 * h + e:2 * h + e + 1]
-                if engine == "vector":
-                    nc.vector.tensor_scalar_mul(out=dst, in0=src, scalar1=a_col)
-                elif engine == "scalar":
-                    nc.scalar.activation(out=dst, in_=src, func=ACT.Copy, scale=a_col)
-                else:
-                    nc.gpsimd.tensor_scalar(out=dst, in0=src, scalar1=a_col, scalar2=0.0, op0=ALU.mult, op1=ALU.add)
-
-        def spread_r(u):
-            for c in range(2):
-                bank = spread_psum.tile([P, 2, PAIR], F32, tag="spread")
-                spread[u, c] = bank
-                for hh in range(2):
-                    for q in range(2):
-                        col = (2 * u + q) * H + 2 * c + hh
-                        nc.tensor.transpose(
-                            bank[:, hh, q * P:(q + 1) * P],
-                            r_sb[:, col:col + 1].to_broadcast([P, P]),
-                            identity[:],
-                        )
-
-        def normalise(u, c):
-            if c == 0:
-                words = grouped_pool.tile([P, 2, PAIR, 4], BF16, tag="grouped", align_bytes=64)
-                grouped[u] = words
-            nc.vector.tensor_tensor(
-                out=grouped[u][:, c, :, :].rearrange("p n (h e) -> p n h e", e=2),
-                in0=ax[:, c, :, u * PAIR:(u + 1) * PAIR].rearrange("p (h e) n -> p n h e", e=2),
-                in1=spread[u, c][:].rearrange("p h n -> p n h").unsqueeze(3).to_broadcast([P, PAIR, 2, 2]),
-                op=ALU.mult,
-            )
-
-        def quantise(u):
-            for c in range(2):
-                nc.vector.quantize_mx(
-                    out=codes[:, c, u * PAIR:(u + 1) * PAIR].bitcast(FP8X4),
-                    scales=scales[:, c, u * PAIR:(u + 1) * PAIR],
-                    in_=grouped[u][:, c, :, :].rearrange("p n j -> p (n j)"),
+        def scale(t):
+            y = y_pool.tile([P, H, D], BF16, tag="y")
+            y_rows[t] = y
+            for h in range(H):
+                nc.vector.scalar_tensor_tensor(
+                    out=y[:, h, :],
+                    in0=x_sb[:, t, :],
+                    scalar=r_sb[:, t * H + h:t * H + h + 1],
+                    in1=a_all[:, h, :],
+                    op0=ALU.mult,
+                    op1=ALU.mult,
                 )
 
-        def store(tile_ap, v, w, units):
-            nc.sync.dma_start(
-                out=out[v * PAIR:(v + 1) * PAIR, w * PAIR:(w + units) * PAIR].rearrange("(r p) c -> p r c", p=P),
-                in_=tile_ap,
+        def turn(t):
+            bank = spread_psum.tile([P, H, P], F32, tag="spread")
+            turned[t] = bank
+            for h in range(H):
+                nc.tensor.transpose(bank[:, h, :], y_rows[t][:, h, :].bitcast(F32), identity[:])
+
+        def group(engine, t):
+            u, q = t // 2, t % 2
+            if q == 0:
+                words = grouped_pool.tile([P, 2, PAIR, 4], BF16, tag="grouped", align_bytes=64)
+                grouped[u] = words
+            dst = grouped[u][:, :, q * P:(q + 1) * P, :].bitcast(F32)
+            src = turned[t][:].rearrange("p (c h) n -> p c n h", c=2)
+            if engine == "vector":
+                nc.vector.tensor_copy(out=dst, in_=src)
+            else:
+                nc.scalar.copy(out=dst, in_=src)
+
+        def quantise(u):
+            nc.vector.quantize_mx(
+                out=codes[:, u, :, :].rearrange("p c n -> p (c n)").bitcast(FP8X4),
+                scales=scales[:, u, :, :].rearrange("p c n -> p (c n)"),
+                in_=grouped[u][:].rearrange("p c n j -> p (c n j)"),
             )
 
-        def drain(engine, dst, bank, scale):
-            if engine == "vector" and scale:
+        def block_of(row, col):
+            if row < 4:
+                return (col, 1) if col < 2 else (col // 2 * 2, 2)
+            return (col // 2 * 2, 2)
+
+        def take(engine, row, col, bank, from_mx):
+            first, count = block_of(row, col)
+            if (row, first) not in pieces:
+                piece = piece_pool.tile([P, 2, count * PAIR], F32, tag="piece%d" % count, bufs={1: 4, 2: 20, 4: 6}[count])
+                pieces[row, first] = piece
+                filled[row, first] = 0
+            dst = pieces[row, first][:, :, (col - first) * PAIR:(col - first + 1) * PAIR]
+            if engine == "vector" and from_mx:
                 nc.vector.tensor_scalar_mul(out=dst, in0=bank[:], scalar1=0.25)
             elif engine == "vector":
                 nc.vector.tensor_copy(out=dst, in_=bank[:])
-            elif scale:
+            elif from_mx:
                 nc.scalar.mul(out=dst, in_=bank[:], mul=0.25)
             else:
                 nc.scalar.copy(out=dst, in_=bank[:])
+            filled[row, first] += 1
+            if filled[row, first] == count:
+                nc.sync.dma_start(
+                    out=out[row * PAIR:(row + 1) * PAIR, first * PAIR:(first + count) * PAIR].rearrange("(r p) c -> p r c", p=P),
+                    in_=pieces[row, first][:],
+                )
 
-        def pick(n, left):
-            return "vector" if left < 2 * n and left % 2 == 0 else "scalar"
+        def unit_mx(engine, v, w):
+            bank = work_psum.tile([P, 2, PAIR], F32, tag="work")
+            for r in range(2):
+                for c in range(2):
+                    nc.tensor.matmul_mx(
+                        out=bank[:, r, :],
+                        lhsT=codes[:, v, c, r * P:(r + 1) * P].bitcast(FP8X4),
+                        lhsT_scale=scales[:, v, c, r * P:(r + 1) * P],
+                        rhs=codes[:, w, c, :].bitcast(FP8X4),
+                        rhs_scale=scales[:, w, c, :],
+                        start=(c == 0),
+                        stop=(c == 1),
+                    )
+            take(engine, v, w, bank, True)
 
-        def row_block(v):
-            block = rows_pool.tile([P, 2, (v + 1) * PAIR], F32, tag="rows")
-            rows[v] = block
+        def unit_mirror(engine, w, v):
+            first, count = block_of(v, w)
+            below = pieces[v, first]
+            bank = work_psum.tile([P, 2, PAIR], F32, tag="work")
+            for r in range(2):
+                for q in range(2):
+                    at = (w - first) * PAIR + r * P
+                    nc.tensor.transpose(bank[:, r, q * P:(q + 1) * P], below[:, q, at:at + P], identity[:])
+            take(engine, w, v, bank, False)
+
+        def row_block(v, engines="s"):
             for w in range(v + 1):
-                bank = work_psum.tile([P, 2, PAIR], F32, tag="work")
-                for r in range(2):
-                    i = 2 * v + r
-                    for c in range(2):
-                        nc.tensor.matmul_mx(
-                            out=bank[:, r, :],
-                            lhsT=codes[:, c, i * P:(i + 1) * P].bitcast(FP8X4),
-                            lhsT_scale=scales[:, c, i * P:(i + 1) * P],
-                            rhs=codes[:, c, w * PAIR:(w + 1) * PAIR].bitcast(FP8X4),
-                            rhs_scale=scales[:, c, w * PAIR:(w + 1) * PAIR],
-                            start=(c == 0),
-                            stop=(c == 1),
-                        )
-                drain(pick(VD[v], v - w), block[:, :, w * PAIR:(w + 1) * PAIR], bank, True)
-                n_store = 2 if v < 5 else 4
-                if (w + 1) % n_store == 0 or w == v:
-                    w0 = w - w % n_store
-                    store(block[:, :, w0 * PAIR:(w + 1) * PAIR], v, w0, w - w0 + 1)
+                unit_mx("vector" if engines[w % len(engines)] == "v" else "scalar", v, w)
 
-        def mirror_block(pairs):
-            for w in range(pairs[-1]):
-                unit = mirror_pool.tile([P, 2, 2 * PAIR], F32, tag="mirror")
-                vs = [v for v in pairs if v > w]
-                for at, v in enumerate(vs):
-                    bank = work_psum.tile([P, 2, PAIR], F32, tag="work")
-                    for r in range(2):
-                        for q in range(2):
-                            nc.tensor.transpose(
-                                bank[:, r, q * P:(q + 1) * P],
-                                rows[v][:, q, (2 * w + r) * P:(2 * w + r + 1) * P],
-                                identity[:],
-                            )
-                    drain(pick(MD[v], v - 1 - w), unit[:, :, at * PAIR:(at + 1) * PAIR], bank, False)
-                store(unit[:, :, 0:len(vs) * PAIR], w, vs[0], len(vs))
+        def mirrors(units, engines="s"):
+            for i, (w, v) in enumerate(units):
+                unit_mirror("vector" if engines[i % len(engines)] == "v" else "scalar", w, v)
 
-        keep_clock_up(3)
+        keep_clock_up(4)
         aT_psum = spread_psum.tile([P, P], F32, tag="spread")
         nc.tensor.transpose(aT_psum[:], a_rows[:].bitcast(F32), identity[:])
-        nc.vector.tensor_copy(out=aT[:], in_=aT_psum[:].bitcast(BF16)[:, 0:2 * H])
-        nc.scalar.activation(out=a2T[:], in_=aT[:].rearrange("p (h e) -> p e h", e=2), func=ACT.Square)
-        b0 = transpose_x(0)
-        b0b = transpose_x(0, spread_psum, "spread")
-        b1 = transpose_x(1)
-        b2 = transpose_x(2)
-        square_x(0, b0)
-        copy_x("vector", 0, b0b)
-        times_a("vector", 0, range(0, 5))
-        sum_squares(0)
-        square_x(1, b1)
-        root(0)
-        copy_x("scalar", 1, b1)
-        cap("vector", 0)
-        sum_squares(1)
-        root(1)
-        times_a("vector", 0, range(5, 8))
-        times_a("gpsimd", 1, range(0, 8))
-        spread_r(0)
-        cap("vector", 1)
-        square_x(2, b2)
-        spread_r(1)
-        normalise(0, 0)
-        b3 = transpose_x(3)
-        sum_squares(2)
-        copy_x("scalar", 2, b2)
-        root(2)
-        normalise(0, 1)
-        square_x(3, b3)
-        quantise(0)
-        cap("vector", 2)
-        for u in range(2, 4):
-            times_a("gpsimd", u, range(VP, 8))
-        row_block(0)
-        normalise(1, 0)
-        spread_r(2)
-        copy_x("scalar", 3, b3)
-        for u in range(4, 6):
-            times_a("gpsimd", u, range(VP, 8))
-        sum_squares(3)
-        b4 = transpose_x(4)
-        normalise(1, 1)
-        quantise(1)
-        times_a("vector", 2, range(0, VP))
-        square_x(4, b4)
-        root(3)
-        row_block(1)
-        normalise(2, 0)
-        cap("vector", 3)
-        sum_squares(4)
-        spread_r(3)
-        copy_x("scalar", 4, b4)
-        for w in range(6, 8):
-            times_a("gpsimd", w, range(VP, 8))
-        root(4)
-        normalise(2, 1)
-        times_a("vector", 3, range(0, VP))
-        quantise(2)
-        cap("vector", 4)
-        mirror_block((1,))
-        spread_r(4)
-        for u in range(3, PAIRS):
-            normalise(u, 0)
-            normalise(u, 1)
-            if u + 1 < PAIRS:
-                times_a("vector", u + 1, range(0, VP))
-            quantise(u)
-            row_block(u - 1)
-            if u + 2 < PAIRS:
-                spread_r(u + 2)
-            if u - 1 < WIDE_FROM:
-                mirror_block((u - 1,))
-            elif u % 2 == 0:
-                mirror_block((u - 2, u - 1))
-        row_block(7)
-        mirror_block((6, 7) if WIDE_FROM < 7 else (7,))
+        nc.scalar.activation(
+            out=a2T[:], in_=aT_psum[:].bitcast(BF16)[:, 0:2 * H].rearrange("p (h e) -> p e h", e=2), func=ACT.Square
+        )
+        banks = {}
+
+        def prepare_a():
+            for half in range(2):
+                bank = spread_psum.tile([P, 2, D], F32, tag="spread")
+                for j in range(2):
+                    h = 2 * half + j
+                    nc.tensor.matmul(
+                        out=bank[:, j, :], lhsT=pick_head[:, h:h + 1].to_broadcast([P, P]), rhs=a_rows[:], start=True, stop=True
+                    )
+                nc.vector.tensor_copy(out=a_all[:, 2 * half:2 * half + 2, :], in_=bank[:])
+
+        waiting = []
+        for step in range(-3, TILES + 4):
+            ahead = step + 3
+            if 0 <= ahead < TILES:
+                banks[ahead] = transpose_x(ahead)
+                square_x(ahead, banks[ahead])
+            if step == -2:
+                prepare_a()
+            if 0 <= step + 2 < TILES:
+                sum_squares(step + 2)
+                root(step + 2)
+            if 0 <= step + 1 < TILES:
+                cap(step + 1)
+            if 3 <= step < TILES + 3 and (step - 3) % 2 == 0:
+                quantise((step - 3) // 2)
+            if 0 <= step < TILES:
+                scale(step)
+            if 0 <= step - 1 < TILES:
+                turn(step - 1)
+                group("scalar", step - 1)
+            if step < 8:
+                keep_clock_up(1)
+            v = (step - 4) // 2
+            if step > 3:
+                if (step - 4) % 2 == 0:
+                    made = [(v, w) for w in range(v + 1)]
+                    turned_over = [(w, v) for w in range(v)] if v < 4 else [(w, v - 1) for w in range(v - 1)] if v > 4 else []
+                    while made or turned_over:
+                        waiting += made[:3]
+                        made = made[3:]
+                        waiting += turned_over[:2]
+                        turned_over = turned_over[2:]
+                    if v == 7:
+                        waiting += [(w, 7) for w in range(7)]
+                quota = (len(waiting) + 1) // 2 if (step - 4) % 2 == 0 else len(waiting)
+                for i in range(quota):
+                    row, col = waiting[i]
+                    engine = "vector" if i % 2 == 1 and i // 2 < VN[v] else "scalar"
+                    if row >= col:
+                        unit_mx(engine, row, col)
+                    else:
+                        unit_mirror(engine, row, col)
+                waiting = waiting[quota:]
+        for i, (row, col) in enumerate(list(waiting)):
+            engine = "vector" if i % 2 else "scalar"
+            if row >= col:
+                unit_mx(engine, row, col)
+            else:
+                unit_mirror(engine, row, col)

@@ -21,7 +21,6 @@ EPS = 1e-12
 FLOPS = 2 * N * N * K
 GROUPS = tuple((t, 1) for t in range(TILES))
 LOADS = ((0, 2), (2, 2), (4, 4), (8, 8))
-VN = (0, 0, 1, 1, 2, 2, 3, 0)
 R_MAX = EPS ** -0.5
 R_MAX = EPS ** -0.5
 
@@ -35,8 +34,8 @@ def tile_attentive_kernel(tc, x, attn_vectors, out):
         y_pool = ctx.enter_context(tc.tile_pool(name="y", bufs=3))
         grouped_pool = ctx.enter_context(tc.tile_pool(name="grouped", bufs=3))
         piece_pool = ctx.enter_context(tc.tile_pool(name="piece", bufs=1))
-        spread_psum = ctx.enter_context(tc.psum_pool(name="spread", bufs=4))
-        work_psum = ctx.enter_context(tc.psum_pool(name="work", bufs=4))
+        spread_psum = ctx.enter_context(tc.psum_pool(name="spread", bufs=3))
+        work_psum = ctx.enter_context(tc.psum_pool(name="work", bufs=5))
 
         a_rows = keep.tile([P, D], BF16)
         nc.vector.memset(a_rows[:], 0.0)
@@ -213,13 +212,12 @@ def tile_attentive_kernel(tc, x, attn_vectors, out):
             for i, (w, v) in enumerate(units):
                 unit_mirror("vector" if engines[i % len(engines)] == "v" else "scalar", w, v)
 
-        keep_clock_up(4)
+        keep_clock_up(3)
         aT_psum = spread_psum.tile([P, P], F32, tag="spread")
         nc.tensor.transpose(aT_psum[:], a_rows[:].bitcast(F32), identity[:])
         nc.scalar.activation(
             out=a2T[:], in_=aT_psum[:].bitcast(BF16)[:, 0:2 * H].rearrange("p (h e) -> p e h", e=2), func=ACT.Square
         )
-        banks = {}
 
         def prepare_a():
             for half in range(2):
@@ -229,54 +227,47 @@ def tile_attentive_kernel(tc, x, attn_vectors, out):
                     nc.tensor.matmul(
                         out=bank[:, j, :], lhsT=pick_head[:, h:h + 1].to_broadcast([P, P]), rhs=a_rows[:], start=True, stop=True
                     )
-                nc.vector.tensor_copy(out=a_all[:, 2 * half:2 * half + 2, :], in_=bank[:])
+                if half == 0:
+                    nc.vector.tensor_copy(out=a_all[:, 0:2, :], in_=bank[:])
+                else:
+                    nc.scalar.copy(out=a_all[:, 2:4, :], in_=bank[:])
 
-        waiting = []
-        for step in range(-3, TILES + 4):
-            ahead = step + 3
-            if 0 <= ahead < TILES:
-                banks[ahead] = transpose_x(ahead)
-                square_x(ahead, banks[ahead])
-            if step == -2:
+        mx_queue, mirror_queue = [], []
+        for step in range(-4, TILES + 6):
+            fresh = (step - 4) % 2 == 0
+            v = (step - 4) // 2
+            if fresh and 0 <= v < PAIRS:
+                mx_queue += [(v, w) for w in range(v + 1)]
+            m = (step - 5) // 2
+            if (step - 5) % 2 == 0 and 0 <= m < PAIRS:
+                mirror_queue += [(w, m) for w in range(m)]
+            n = (len(mx_queue) + 1) // 2 if fresh else len(mx_queue)
+            now_mx, mx_queue = mx_queue[:n], mx_queue[n:]
+            n = (len(mirror_queue) + 1) // 2 if (step - 5) % 2 == 0 else len(mirror_queue)
+            now_mirror, mirror_queue = mirror_queue[:n], mirror_queue[n:]
+            if step == -3:
                 prepare_a()
-            if 0 <= step + 2 < TILES:
-                sum_squares(step + 2)
-                root(step + 2)
-            if 0 <= step + 1 < TILES:
-                cap(step + 1)
+            t = step + 4
+            if 0 <= t < TILES:
+                bank = transpose_x(t)
+                square_x(t, bank)
+            if step < 7:
+                keep_clock_up(1)
             if 3 <= step < TILES + 3 and (step - 3) % 2 == 0:
                 quantise((step - 3) // 2)
+            t = step + 3
+            if 0 <= t < TILES:
+                sum_squares(t)
+                root(t)
+            for i, (row, col) in enumerate(now_mx):
+                unit_mx("vector" if step > 9 and i % 2 == 1 else "scalar", row, col)
             if 0 <= step < TILES:
                 scale(step)
             if 0 <= step - 1 < TILES:
                 turn(step - 1)
                 group("scalar", step - 1)
-            if step < 8:
-                keep_clock_up(1)
-            v = (step - 4) // 2
-            if step > 3:
-                if (step - 4) % 2 == 0:
-                    made = [(v, w) for w in range(v + 1)]
-                    turned_over = [(w, v) for w in range(v)] if v < 4 else [(w, v - 1) for w in range(v - 1)] if v > 4 else []
-                    while made or turned_over:
-                        waiting += made[:3]
-                        made = made[3:]
-                        waiting += turned_over[:2]
-                        turned_over = turned_over[2:]
-                    if v == 7:
-                        waiting += [(w, 7) for w in range(7)]
-                quota = (len(waiting) + 1) // 2 if (step - 4) % 2 == 0 else len(waiting)
-                for i in range(quota):
-                    row, col = waiting[i]
-                    engine = "vector" if i % 2 == 1 and i // 2 < VN[v] else "scalar"
-                    if row >= col:
-                        unit_mx(engine, row, col)
-                    else:
-                        unit_mirror(engine, row, col)
-                waiting = waiting[quota:]
-        for i, (row, col) in enumerate(list(waiting)):
-            engine = "vector" if i % 2 else "scalar"
-            if row >= col:
-                unit_mx(engine, row, col)
-            else:
-                unit_mirror(engine, row, col)
+            t = step + 2
+            if 0 <= t < TILES:
+                cap(t)
+            for i, (row, col) in enumerate(now_mirror):
+                unit_mirror("vector" if step > 9 and i % 2 == 1 else "scalar", row, col)

@@ -174,7 +174,8 @@ def tile_attentive_kernel(tc, x, attn_vectors, out):
                 nc.scalar.copy(out=dst, in_=bank[:])
             filled[row, first] += 1
             if filled[row, first] == count:
-                nc.sync.dma_start(
+                queue = nc.sync if from_mx or col == PAIRS - 1 else nc.gpsimd
+                queue.dma_start(
                     out=out[row * PAIR:(row + 1) * PAIR, first * PAIR:(first + count) * PAIR].rearrange("(r p) c -> p r c", p=P),
                     in_=pieces[row, first][:],
                 )

@@ -22,7 +22,6 @@ FLOPS = 2 * N * N * K
 GROUPS = tuple((t, 1) for t in range(TILES))
 LOADS = ((0, 2), (2, 2), (4, 4), (8, 8))
 R_MAX = EPS ** -0.5
-R_MAX = EPS ** -0.5
 
 
 def tile_attentive_kernel(tc, x, attn_vectors, out):
@@ -153,9 +152,11 @@ def tile_attentive_kernel(tc, x, attn_vectors, out):
             )
 
         def block_of(row, col):
-            if row < 4:
-                return (col, 1) if col < 2 else (col // 2 * 2, 2)
-            return (col // 2 * 2, 2)
+            if row < 4 and col < 2:
+                return col, 1
+            if row >= 6 and col < 4:
+                return 0, 4
+            return col // 2 * 2, 2
 
         def take(engine, row, col, bank, from_mx):
             first, count = block_of(row, col)
@@ -214,27 +215,37 @@ def tile_attentive_kernel(tc, x, attn_vectors, out):
                 unit_mirror("vector" if engines[i % len(engines)] == "v" else "scalar", w, v)
 
         keep_clock_up(3)
+
+        def spread_a(half):
+            bank = spread_psum.tile([P, 2, D], F32, tag="spread")
+            for j in range(2):
+                h = 2 * half + j
+                nc.tensor.matmul(
+                    out=bank[:, j, :], lhsT=pick_head[:, h:h + 1].to_broadcast([P, P]), rhs=a_rows[:], start=True, stop=True
+                )
+            return bank
+
+        x_bank = {}
+        x_bank[0] = transpose_x(0)
         aT_psum = spread_psum.tile([P, P], F32, tag="spread")
         nc.tensor.transpose(aT_psum[:], a_rows[:].bitcast(F32), identity[:])
         nc.scalar.activation(
             out=a2T[:], in_=aT_psum[:].bitcast(BF16)[:, 0:2 * H].rearrange("p (h e) -> p e h", e=2), func=ACT.Square
         )
-
-        def prepare_a():
-            for half in range(2):
-                bank = spread_psum.tile([P, 2, D], F32, tag="spread")
-                for j in range(2):
-                    h = 2 * half + j
-                    nc.tensor.matmul(
-                        out=bank[:, j, :], lhsT=pick_head[:, h:h + 1].to_broadcast([P, P]), rhs=a_rows[:], start=True, stop=True
-                    )
-                if half == 0:
-                    nc.vector.tensor_copy(out=a_all[:, 0:2, :], in_=bank[:])
-                else:
-                    nc.scalar.copy(out=a_all[:, 2:4, :], in_=bank[:])
-
+        square_x(0, x_bank[0])
+        x_bank[1] = transpose_x(1)
+        square_x(1, x_bank[1])
+        bank = spread_a(0)
+        nc.vector.tensor_copy(out=a_all[:, 0:2, :], in_=bank[:])
+        sum_squares(0)
+        root(0)
+        bank = spread_a(1)
+        nc.scalar.copy(out=a_all[:, 2:4, :], in_=bank[:])
+        cap(0)
+        sum_squares(1)
+        root(1)
         mx_queue, mirror_queue = [], []
-        for step in range(-4, TILES + 6):
+        for step in range(-2, TILES + 6):
             fresh = (step - 4) % 2 == 0
             v = (step - 4) // 2
             if fresh and 0 <= v < PAIRS:
@@ -246,19 +257,21 @@ def tile_attentive_kernel(tc, x, attn_vectors, out):
             now_mx, mx_queue = mx_queue[:n], mx_queue[n:]
             n = (len(mirror_queue) + 1) // 2 if (step - 5) % 2 == 0 else len(mirror_queue)
             now_mirror, mirror_queue = mirror_queue[:n], mirror_queue[n:]
-            if step == -3:
-                prepare_a()
             t = step + 4
-            if 0 <= t < TILES:
-                bank = transpose_x(t)
-                square_x(t, bank)
+            if 2 <= t < TILES:
+                x_bank[t] = transpose_x(t)
+            t = step + 4
+            if 2 <= t < TILES:
+                square_x(t, x_bank[t])
             if step < 7:
                 keep_clock_up(1)
             if 3 <= step < TILES + 3 and (step - 3) % 2 == 0:
                 quantise((step - 3) // 2)
             t = step + 3
-            if 0 <= t < TILES:
+            if 2 <= t < TILES:
                 sum_squares(t)
+            t = step + 3
+            if 2 <= t < TILES:
                 root(t)
             for i, (row, col) in enumerate(now_mx):
                 unit_mx("vector" if step > 9 and i % 2 == 1 else "scalar", row, col)
@@ -266,9 +279,10 @@ def tile_attentive_kernel(tc, x, attn_vectors, out):
                 scale(step)
             if 0 <= step - 1 < TILES:
                 turn(step - 1)
+            if 0 <= step - 1 < TILES:
                 group("scalar", step - 1)
             t = step + 2
-            if 0 <= t < TILES:
+            if 1 <= t < TILES:
                 cap(t)
             for i, (row, col) in enumerate(now_mirror):
                 unit_mirror("vector" if step > 9 and i % 2 == 1 else "scalar", row, col)

from contextlib import ExitStack

import concourse.mybir as mybir
from concourse.masks import make_identity

F32 = mybir.dt.float32
BF16 = mybir.dt.bfloat16
U32 = mybir.dt.uint32
U8 = mybir.dt.uint8
FP8X4 = mybir.dt.float8_e4m3fn_x4
ACT = mybir.ActivationFunctionType
ALU = mybir.AluOpType

N, D, H = 2048, 256, 4
K = H * D
P = 128
TILES = N // P
PAIR = 2 * P
PAIRS = N // PAIR
EPS = 1e-12
FLOPS = 2 * N * N * K
GROUPS = tuple((t, 1) for t in range(TILES))
LOADS = ((0, 2), (2, 2), (4, 4), (8, 8))
R_MAX = EPS ** -0.5


def tile_attentive_kernel(tc, x, attn_vectors, out):
    nc = tc.nc
    with ExitStack() as ctx:
        ctx.enter_context(tc.manual_schedule())
        keep = ctx.enter_context(tc.tile_pool(name="keep", bufs=1))
        small = ctx.enter_context(tc.tile_pool(name="small", bufs=5))
        y_pool = ctx.enter_context(tc.tile_pool(name="y", bufs=3))
        grouped_pool = ctx.enter_context(tc.tile_pool(name="grouped", bufs=3))
        piece_pool = ctx.enter_context(tc.tile_pool(name="piece", bufs=1))
        spread_psum = ctx.enter_context(tc.psum_pool(name="spread", bufs=3))
        work_psum = ctx.enter_context(tc.psum_pool(name="work", bufs=5))

        a_rows = keep.tile([P, D], BF16)
        nc.vector.memset(a_rows[:], 0.0)
        x_sb = keep.tile([P, TILES, D], BF16)
        for first, count in LOADS:
            if first == 2:
                nc.sync.dma_start(out=a_rows[0:H, :], in_=attn_vectors)
            nc.sync.dma_start(
                out=x_sb[:, first:first + count, :],
                in_=x[first * P:(first + count) * P, :].rearrange("(t p) d -> p t d", p=P),
            )
        zeros = keep.tile([P, 4 * P], BF16)
        nc.vector.memset(zeros[:], 0.0)
        one = keep.tile([P, 1], F32)
        nc.vector.memset(one[:], 1.0)
        unused_root = keep.tile([P, 1], F32)
        nc.scalar.activation(out=unused_root[:], in_=one[:], func=ACT.Abs_reciprocal_sqrt)
        identity = keep.tile([P, P], F32)
        make_identity(nc, identity[:])
        pick_head = keep.tile([P, H], BF16)
        nc.vector.tensor_copy(out=pick_head[:], in_=identity[:, 0:H])

        x2T = keep.tile([P, 2, N], F32)
        a2T = keep.tile([P, 2, H], F32)
        a_all = keep.tile([P, H, D], BF16)
        r_sb = keep.tile([P, TILES * H], F32)
        codes = keep.tile([P, PAIRS, 2, PAIR], U32, align_bytes=64)
        scales = keep.tile([P, PAIRS, 2, PAIR], U8, align_bytes=64)

        x_words = x_sb[:].rearrange("p t d -> p (t d)").bitcast(F32)

        sums_psum, roots, y_rows, turned, grouped, pieces, filled = {}, {}, {}, {}, {}, {}, {}

        def keep_clock_up(count):
            for repeat in range(count):
                idle = work_psum.tile([P, 4 * P], F32, tag="work")
                nc.tensor.matmul(out=idle[:], lhsT=zeros[:, 0:P], rhs=zeros[:], start=True, stop=True)

        def transpose_x(g, pool=None, tag="work"):
            first, count = GROUPS[g]
            bank = (pool or work_psum).tile([P, count * P], F32, tag=tag)
            for j in range(count):
                t = first + j
                nc.tensor.transpose(bank[:, j * P:(j + 1) * P], x_words[:, t * P:(t + 1) * P], identity[:])
            return bank

        def square_x(g, bank):
            first, count = GROUPS[g]
            nc.scalar.activation(
                out=x2T[:, :, first * P:(first + count) * P],
                in_=bank[:].bitcast(BF16).rearrange("p (n e) -> p e n", e=2),
                func=ACT.Square,
            )

        def sum_squares(g):
            first, count = GROUPS[g]
            bank = work_psum.tile([P, count * H], F32, tag="work")
            sums_psum[g] = bank
            for j in range(count):
                t = first + j
                for e in range(2):
                    nc.tensor.matmul(
                        out=bank[:, j * H:(j + 1) * H],
                        lhsT=x2T[:, e, t * P:(t + 1) * P],
                        rhs=a2T[:, e, :],
                        start=(e == 0),
                        stop=(e == 1),
                    )

        def root(g):
            rsqrt = small.tile([P, GROUPS[g][1] * H], F32, tag="roots")
            roots[g] = rsqrt
            nc.scalar.activation(out=rsqrt[:], in_=sums_psum[g][:], func=ACT.Abs_reciprocal_sqrt)

        def cap(g):
            first, count = GROUPS[g]
            nc.vector.tensor_scalar_min(out=r_sb[:, first * H:(first + count) * H], in0=roots[g][:], scalar1=R_MAX)

        def scale(t):
            y = y_pool.tile([P, H, D], BF16, tag="y")
            y_rows[t] = y
            for h in range(H):
                nc.vector.scalar_tensor_tensor(
                    out=y[:, h, :],
                    in0=x_sb[:, t, :],
                    scalar=r_sb[:, t * H + h:t * H + h + 1],
                    in1=a_all[:, h, :],
                    op0=ALU.mult,
                    op1=ALU.mult,
                )

        def turn(t):
            bank = spread_psum.tile([P, H, P], F32, tag="spread")
            turned[t] = bank
            for h in range(H):
                nc.tensor.transpose(bank[:, h, :], y_rows[t][:, h, :].bitcast(F32), identity[:])

        def group(engine, t):
            u, q = t // 2, t % 2
            if q == 0:
                words = grouped_pool.tile([P, 2, PAIR, 4], BF16, tag="grouped", align_bytes=64)
                grouped[u] = words
            dst = grouped[u][:, :, q * P:(q + 1) * P, :].bitcast(F32)
            src = turned[t][:].rearrange("p (c h) n -> p c n h", c=2)
            if engine == "vector":
                nc.vector.tensor_copy(out=dst, in_=src)
            else:
                nc.scalar.copy(out=dst, in_=src)

        def quantise(u):
            nc.vector.quantize_mx(
                out=codes[:, u, :, :].rearrange("p c n -> p (c n)").bitcast(FP8X4),
                scales=scales[:, u, :, :].rearrange("p c n -> p (c n)"),
                in_=grouped[u][:].rearrange("p c n j -> p (c n j)"),
            )

        def block_of(row, col):
            if row < 4 and col < 2:
                return col, 1
            if row >= 6 and col < 4:
                return 0, 4
            return col // 2 * 2, 2

        def take(engine, row, col, bank, from_mx):
            first, count = block_of(row, col)
            if (row, first) not in pieces:
                piece = piece_pool.tile([P, 2, count * PAIR], F32, tag="piece%d" % count, bufs={1: 4, 2: 20, 4: 6}[count])
                pieces[row, first] = piece
                filled[row, first] = 0
            dst = pieces[row, first][:, :, (col - first) * PAIR:(col - first + 1) * PAIR]
            if engine == "vector" and from_mx:
                nc.vector.tensor_scalar_mul(out=dst, in0=bank[:], scalar1=0.25)
            elif engine == "vector":
                nc.vector.tensor_copy(out=dst, in_=bank[:])
            elif from_mx:
                nc.scalar.mul(out=dst, in_=bank[:], mul=0.25)
            else:
                nc.scalar.copy(out=dst, in_=bank[:])
            filled[row, first] += 1
            if filled[row, first] == count:
                queue = nc.sync if from_mx or col == PAIRS - 1 else nc.gpsimd
                queue.dma_start(
                    out=out[row * PAIR:(row + 1) * PAIR, first * PAIR:(first + count) * PAIR].rearrange("(r p) c -> p r c", p=P),
                    in_=pieces[row, first][:],
                )

        def unit_mx(engine, v, w):
            bank = work_psum.tile([P, 2, PAIR], F32, tag="work")
            for r in range(2):
                for c in range(2):
                    nc.tensor.matmul_mx(
                        out=bank[:, r, :],
                        lhsT=codes[:, v, c, r * P:(r + 1) * P].bitcast(FP8X4),
                        lhsT_scale=scales[:, v, c, r * P:(r + 1) * P],
                        rhs=codes[:, w, c, :].bitcast(FP8X4),
                        rhs_scale=scales[:, w, c, :],
                        start=(c == 0),
                        stop=(c == 1),
                    )
            take(engine, v, w, bank, True)

        def unit_mirror(engine, w, v):
            first, count = block_of(v, w)
            below = pieces[v, first]
            bank = work_psum.tile([P, 2, PAIR], F32, tag="work")
            for r in range(2):
                for q in range(2):
                    at = (w - first) * PAIR + r * P
                    nc.tensor.transpose(bank[:, r, q * P:(q + 1) * P], below[:, q, at:at + P], identity[:])
            take(engine, w, v, bank, False)

        def row_block(v, engines="s"):
            for w in range(v + 1):
                unit_mx("vector" if engines[w % len(engines)] == "v" else "scalar", v, w)

        def mirrors(units, engines="s"):
            for i, (w, v) in enumerate(units):
                unit_mirror("vector" if engines[i % len(engines)] == "v" else "scalar", w, v)

        keep_clock_up(3)

        def spread_a(half):
            bank = spread_psum.tile([P, 2, D], F32, tag="spread")
            for j in range(2):
                h = 2 * half + j
                nc.tensor.matmul(
                    out=bank[:, j, :], lhsT=pick_head[:, h:h + 1].to_broadcast([P, P]), rhs=a_rows[:], start=True, stop=True
                )
            return bank

        x_bank = {}
        x_bank[0] = transpose_x(0)
        aT_psum = spread_psum.tile([P, P], F32, tag="spread")
        nc.tensor.transpose(aT_psum[:], a_rows[:].bitcast(F32), identity[:])
        nc.scalar.activation(
            out=a2T[:], in_=aT_psum[:].bitcast(BF16)[:, 0:2 * H].rearrange("p (h e) -> p e h", e=2), func=ACT.Square
        )
        square_x(0, x_bank[0])
        x_bank[1] = transpose_x(1)
        square_x(1, x_bank[1])
        bank = spread_a(0)
        nc.vector.tensor_copy(out=a_all[:, 0:2, :], in_=bank[:])
        sum_squares(0)
        root(0)
        bank = spread_a(1)
        nc.scalar.copy(out=a_all[:, 2:4, :], in_=bank[:])
        cap(0)
        sum_squares(1)
        root(1)
        mx_queue, mirror_queue = [], []
        for step in range(-2, TILES + 6):
            fresh = (step - 4) % 2 == 0
            v = (step - 4) // 2
            if fresh and 0 <= v < PAIRS:
                mx_queue += [(v, w) for w in range(v + 1)]
            m = (step - 5) // 2
            if (step - 5) % 2 == 0 and 0 <= m < PAIRS:
                mirror_queue += [(w, m) for w in range(m)]
            n = (len(mx_queue) + 1) // 2 if fresh else len(mx_queue)
            now_mx, mx_queue = mx_queue[:n], mx_queue[n:]
            n = (len(mirror_queue) + 1) // 2 if (step - 5) % 2 == 0 else len(mirror_queue)
            now_mirror, mirror_queue = mirror_queue[:n], mirror_queue[n:]
            t = step + 4
            if 2 <= t < TILES:
                x_bank[t] = transpose_x(t)
            t = step + 4
            if 2 <= t < TILES:
                square_x(t, x_bank[t])
            if step < 7:
                keep_clock_up(1)
            if 3 <= step < TILES + 3 and (step - 3) % 2 == 0:
                quantise((step - 3) // 2)
            t = step + 3
            if 2 <= t < TILES:
                sum_squares(t)
            t = step + 3
            if 2 <= t < TILES:
                root(t)
            for i, (row, col) in enumerate(now_mx):
                unit_mx("vector" if step > 9 and i % 2 == 1 else "scalar", row, col)
            if 0 <= step < TILES:
                scale(step)
            if 0 <= step - 1 < TILES:
                turn(step - 1)
            if 0 <= step - 1 < TILES:
                group("scalar", step - 1)
            t = step + 2
            if 1 <= t < TILES:
                cap(t)
            for i, (row, col) in enumerate(now_mirror):
                unit_mirror("vector" if step > 9 and i % 2 == 1 else "scalar", row, col)
